import numpy as np
import ml_dtypes


def mxq(x, axis, fmt="e4m3"):
    dtype, down = {"e4m3": (ml_dtypes.float8_e4m3fn, 7), "e5m2": (ml_dtypes.float8_e5m2, 14)}[fmt]
    v = np.moveaxis(np.asarray(x, np.float32).astype(ml_dtypes.bfloat16).astype(np.float64), axis, -1)
    blocks = v.reshape(v.shape[:-1] + (-1, 32))
    amax = np.abs(blocks).max(-1, keepdims=True)
    byte = np.maximum(np.where(amax > 0, np.frexp(amax)[1] - 1 + 127, 0) - down, 1)
    scale = np.exp2(byte - 127.0)
    codes = (blocks / scale).astype(np.float32).astype(dtype).astype(np.float64)
    return np.moveaxis((codes * scale).reshape(v.shape), -1, axis)


WIDE = False


def mx_kscale(k):
    if not WIDE:
        return np.ones(k)
    levels = np.array([10, -10, 5, -5, 0])
    if k % 512:
        return np.exp2(np.random.permutation(np.resize(levels, k // 32))).repeat(32)
    a = np.empty((k // 512, 16))
    for p in range(k // 512):
        a[p, :8] = np.random.permutation(np.resize(levels, 8))
        for g in range(8):
            far = levels[np.abs(levels - a[p, g]) >= 10]
            a[p, g + 8] = far[np.random.randint(len(far))]
    return np.exp2(a.ravel()).repeat(32)


BF16 = ml_dtypes.bfloat16


def bf(x):
    return np.asarray(x, np.float32).astype(BF16)


def f64(x):
    return np.asarray(x).astype(np.float64)


B, S, D, H = 2, 256, 1024, 4096
NS = int(round(np.log2(H)))


def erf(z):
    z = np.clip(z, -6.0, 6.0)
    z2 = 2.0 * z * z
    term = z.copy()
    tot = z.copy()
    for n in range(1, 130):
        term = term * (z2 / (2 * n + 1))
        tot = tot + term
    return 2.0 / np.sqrt(np.pi) * np.exp(-z * z) * tot


def gelu_exact(v):
    return 0.5 * v * (1.0 + erf(v / np.sqrt(2.0)))


def butterfly(y, weights, dim):
    lead = y.shape[:-1]
    for stage in range(weights.shape[0]):
        s = 2 ** stage
        nb = dim // (2 * s)
        yr = y.reshape(*lead, nb, 2, s)
        a = yr[..., 0, :]
        b = yr[..., 1, :]
        w = weights[stage].reshape(nb, s, 2, 2)
        na = w[..., 0, 0] * a + w[..., 0, 1] * b
        nb2 = w[..., 1, 0] * a + w[..., 1, 1] * b
        y = np.stack([na, nb2], axis=-2).reshape(*lead, dim)
    return y


def bfly_draw():
    g = np.random.standard_normal((NS, H // 2, 2, 2))
    return np.sign(g) * 0.58 + 0.15 * g


def draw0():
    s, t = mx_kscale(D), mx_kscale(H)
    x = np.random.standard_normal((B, S, D)) * s
    W_exp = np.random.standard_normal((D, H)) / np.sqrt(D) / s[:, None]
    b_exp = np.random.standard_normal(H) * 0.1
    up_weights = bfly_draw()
    up_bias = np.random.standard_normal(H) * 0.1
    down_weights = bfly_draw()
    down_weights[NS - 1] = down_weights[NS - 1] * t.reshape(2, H // 2).T[:, :, None]
    W_con = np.random.standard_normal((H, D)) * 1.5 / np.sqrt(H) / t[:, None]
    b_con = np.random.standard_normal(D) * 0.1
    down_bias = np.random.standard_normal(D) * 0.1
    return {"x": bf(x), "W_exp": bf(W_exp), "b_exp": bf(b_exp), "up_weights": bf(up_weights), "up_bias": bf(up_bias),
            "down_weights": bf(down_weights), "W_con": bf(W_con), "b_con": bf(b_con), "down_bias": bf(down_bias)}


def core(x, W_exp, b_exp, up_weights, up_bias, down_weights, W_con, b_con, down_bias):
    h = (mxq(f64(x), 2, "e4m3") @ mxq(f64(W_exp), 0, "e4m3")) + f64(b_exp)
    h = butterfly(h, f64(up_weights), H)
    h = gelu_exact(h + f64(up_bias))
    h = butterfly(h, f64(down_weights), H)
    y = (mxq(h, 2, "e4m3") @ mxq(f64(W_con), 0, "e4m3")) + f64(b_con)
    return y + f64(down_bias)


def e4m3fn_bytes(y):
    return np.clip(np.asarray(y, np.float64), -448.0, 448.0).astype(np.float32).astype(ml_dtypes.float8_e4m3fn).view(np.uint8)


def e4m3fn_values(b):
    return np.asarray(b, np.uint8).view(ml_dtypes.float8_e4m3fn).astype(np.float64)


def setup_inputs():
    d = draw0()
    x0 = np.asarray(d['W_exp']).astype(np.float64)
    s = (np.max(np.abs(x0), axis=(1,), keepdims=True) / 448.0).astype(np.float32)
    out = {}
    for k, v in d.items():
        if k == 'W_exp':
            out['W_exp_bytes'] = e4m3fn_bytes(x0 / s.astype(np.float64))
            out['W_exp_scale'] = s
        else:
            out[k] = v
    return out


def reference(x, W_exp_bytes, W_exp_scale, b_exp, up_weights, up_bias, down_weights, W_con, b_con, down_bias):
    return core(x, e4m3fn_values(W_exp_bytes) * W_exp_scale.astype(np.float64), b_exp, up_weights, up_bias, down_weights, W_con, b_con, down_bias)

@@ -1,0 +1,502 @@
+from contextlib import ExitStack
+
+import concourse.mybir as mybir
+from concourse.masks import make_identity
+
+F32 = mybir.dt.float32
+BF16 = mybir.dt.bfloat16
+U32 = mybir.dt.uint32
+U8 = mybir.dt.uint8
+FP8 = mybir.dt.float8_e4m3fn
+FP8X4 = mybir.dt.float8_e4m3fn_x4
+ALU = mybir.AluOpType
+ACT = mybir.ActivationFunctionType
+
+TOK, D, H = 512, 1024, 4096
+FLOPS = 2 * 2 * TOK * D * H + 2 * 12 * 3 * TOK * H
+
+N1 = 304
+N2 = TOK - N1
+CHUNKS = ((0, N1, 0), (1, 384, 384 - N1))
+
+
+def pairs(bit):
+    return [(b, b | (1 << bit)) for b in range(32) if not b & (1 << bit)]
+
+
+def tile_butterflymlp_kernel(tc, x, w_bytes, w_scale, b_exp, up_w, up_bias, down_w, w_con, b_con, down_bias, out):
+    nc = tc.nc
+    with ExitStack() as ctx:
+        cons = ctx.enter_context(tc.tile_pool(name="cons", bufs=1))
+        tmp = ctx.enter_context(tc.tile_pool(name="tmp", bufs=1))
+        work = ctx.enter_context(tc.tile_pool(name="work", bufs=2))
+        psum = ctx.enter_context(tc.psum_pool(name="psum", bufs=8))
+
+        def bank(shape):
+            ps = psum.tile([128, 512], F32, tag="ps", name="ps")
+            return ps
+
+        def y1tile():
+            return work.tile([128, N1], F32, tag="y1", name="y1", bufs=35)
+
+        def y2tile():
+            return work.tile([128, N2], F32, tag="y2", name="y2", bufs=34)
+
+        def stt(o, in0, s, in1):
+            nc.vector.scalar_tensor_tensor(out=o, in0=in0, scalar=s, in1=in1, op0=ALU.mult, op1=ALU.add)
+
+        def scaled(o, i, s, b=None):
+            if b is None:
+                nc.scalar.activation(out=o, in_=i, func=ACT.Copy, scale=s)
+            else:
+                nc.scalar.activation(out=o, in_=i, func=ACT.Identity, scale=s, bias=b)
+
+        ident = cons.tile([128, 128], F32, name="ident")
+        make_identity(nc, ident[:])
+        wsc = cons.tile([128, 2, 4], F32, name="wsc")
+        nc.sync.dma_start(out=wsc[:], in_=w_scale.rearrange("(g p t) o -> p g (t o)", g=2, t=4))
+        xrows = x.rearrange("b s d -> (b s) d").rearrange("(i p) d -> p i d", p=128)
+        xraw = []
+        for h in range(2):
+            xr = work.tile([128, 2, D], BF16, tag="wide", name="xr", bufs=3, align_bytes=64)
+            nc.sync.dma_start(out=xr[:], in_=xrows[:, 2 * h : 2 * h + 2, :])
+            xraw.append(xr)
+
+        wsrc = w_bytes.rearrange("(g p t) n -> g p t n", g=2, t=4)
+
+        def load_wexp(c):
+            wb = work.tile([128, 2, 4, 512], U8, tag="wb", name="wb", bufs=3, align_bytes=64)
+            for g in range(2):
+                nc.sync.dma_start(out=wb[:, g, :, :], in_=wsrc[g][:, :, 512 * c : 512 * c + 512])
+            return wb
+
+        wbs = {0: load_wexp(0)}
+
+        def load_main(w, name):
+            raw = cons.tile([128, 5, 64], BF16, name=name)
+            for k, s in ((0, 0), (1, 1)):
+                nc.sync.dma_start(out=raw[:, k, :].rearrange("p (c r) -> p c r", c=8),
+                                  in_=w[s].rearrange("k o i -> (k o i)").rearrange("(c p r) -> p c r", p=128, r=8))
+            for k, s in ((2, 9), (3, 10), (4, 11)):
+                nc.sync.dma_start(out=raw[:, k, :].rearrange("p (c r) -> p c r", c=4),
+                                  in_=w[s].rearrange("k o i -> (k o i)").rearrange("(c p r) -> p c r", p=128, r=16))
+            return raw
+
+        um_raw = load_main(up_w, "um_raw")
+        bm_raw = cons.tile([128, 2, 32], BF16, name="bm_raw")
+        for k, v in ((0, b_exp), (1, up_bias)):
+            nc.sync.dma_start(out=bm_raw[:, k, :].rearrange("p (c t) -> p c t", t=4), in_=v.rearrange("(c p t) -> p c t", p=128, t=4))
+        wbs[1] = load_wexp(1)
+        r1_raw = cons.tile([128, 5, 64], BF16, name="r1_raw")
+        nc.sync.dma_start(out=r1_raw[:], in_=up_w[0:5].rearrange("s k o i -> s (k o i)").rearrange("s (q r) -> q s r", r=64))
+        b2_raw = cons.tile([128, 32], BF16, name="b2_raw")
+        nc.sync.dma_start(out=b2_raw[:], in_=b_exp.rearrange("(q l) -> q l", l=32))
+        wbs[2] = load_wexp(2)
+
+        def load_factors(w):
+            ft = cons.tile([128, 16 * 127 * 8], BF16, tag="fh", name="ft")
+            views = []
+            off = 0
+            for j in range(7):
+                run = 16 << j
+                fj = ft[:, off : off + 8 * run].rearrange("p (c e) -> p c e", c=8)
+                off += 8 * run
+                views.append(fj)
+                src = w[2 + j].rearrange("k o i -> (k o i)").rearrange("(c h e) -> h c e", c=8, e=run)
+                n_lo, n_hi = 1 << j, 1 << (6 - j)
+                for i in range(2):
+                    if n_lo <= n_hi:
+                        for lo in range(n_lo):
+                            nc.sync.dma_start(out=fj[i * n_lo + lo :: 2 * n_lo, :, 0 : run - 1], in_=src[:, :, i : i + run - 1])
+                    else:
+                        for h in range(n_hi):
+                            p0 = h * 2 * n_lo + i * n_lo
+                            nc.sync.dma_start(out=fj[p0 : p0 + n_lo, :, 0 : run - 1], in_=src[h][:, i : i + run - 1].partition_broadcast(n_lo))
+            return views
+
+        f_up = load_factors(up_w)
+        r2_raw = cons.tile([128, 4, 64], BF16, name="r2_raw")
+        for k in range(4):
+            src = up_w[5 + k].rearrange("k o i -> (k o i)").rearrange("(h u l q) -> h l u q", h=4, u=16, l=32)
+            for h in range(4):
+                nc.sync.dma_start(out=r2_raw[h::4, k, :].rearrange("p (u q) -> p u q", q=4), in_=src[h])
+
+        dm_raw = load_main(down_w, "dm_raw")
+
+        def tt(eng, o, a, b, op):
+            eng.tensor_tensor(out=o, in0=a, in1=b, op=op)
+
+        def half(a, bit, o):
+            return a.rearrange("p (h o l) -> p h o l", o=2, l=1 << bit)[:, :, o, :]
+
+        def coefficients(raws, name):
+            n = sum(m for raw, m in raws)
+            wd = cons.tile([128, n, 32], F32, name=name + "_wd")
+            wo = cons.tile([128, n, 32], F32, name=name + "_wo")
+            k0 = 0
+            for raw, m in raws:
+                for k in range(m):
+                    lo = 1 << k
+                    src = raw[:, k, :].rearrange("p (h l q) -> p h l q", l=lo, q=4)
+                    nc.gpsimd.tensor_copy(out=wd[:, k0 + k, :].rearrange("p (h o l) -> p h l o", o=2, l=lo), in_=src[:, :, :, 0:4:3])
+                    nc.gpsimd.tensor_copy(out=wo[:, k0 + k, :].rearrange("p (h o l) -> p h l o", o=2, l=lo), in_=src[:, :, :, 1:3])
+                k0 += m
+            d = wd[:].rearrange("p k b -> p (k b)")
+            o = wo[:].rearrange("p k b -> p (k b)")
+            ta = tmp.tile([128, 448], F32, tag="ta", name="ta")[:, 0 : 32 * n]
+            tb = tmp.tile([128, 448], F32, tag="tb", name="tb")[:, 0 : 32 * n]
+            tk = tmp.tile([128, 448], F32, tag="tk", name="tk")[:, 0 : 32 * n]
+            den = cons.tile([128, n, 32], F32, name=name + "_den")
+            inv = cons.tile([128, n, 32], F32, name=name + "_inv")
+            rr = cons.tile([128, n, 32], F32, name=name + "_rr")
+            dn = den[:].rearrange("p k b -> p (k b)")
+            iv = inv[:].rearrange("p k b -> p (k b)")
+            v, g = nc.vector, nc.gpsimd
+            v.scalar_tensor_tensor(out=tb, in0=o, scalar=-1.0, in1=o, op0=ALU.mult, op1=ALU.max)
+            v.scalar_tensor_tensor(out=ta, in0=d, scalar=-1.0, in1=d, op0=ALU.mult, op1=ALU.max)
+            g.tensor_scalar(out=tb, in0=tb, scalar1=2.0**-20, scalar2=2.0**-40, op0=ALU.mult, op1=ALU.max)
+            tt(v, tk, ta, tb, ALU.is_ge)
+            tt(g, ta, tk, d, ALU.mult)
+            g.tensor_scalar(out=tk, in0=tk, scalar1=-1.0, scalar2=1.0, op0=ALU.mult, op1=ALU.add)
+            tt(g, tb, tk, tb, ALU.mult)
+            tt(g, dn, ta, tb, ALU.add)
+            v.reciprocal(out=iv, in_=dn)
+            tt(g, rr[:].rearrange("p k b -> p (k b)"), o, iv, ALU.mult)
+            res = []
+            k0 = 0
+            for raw, m in raws:
+                res.append(dict([(key, t[:, k0 : k0 + m, :]) for key, t in (("wd", wd), ("wo", wo), ("den", den), ("inv", inv), ("rr", rr))]))
+                k0 += m
+            return res
+
+        def partner_mul(o, a, b, bit):
+            for i in range(2):
+                tt(nc.gpsimd, half(o, bit, i), half(a, bit, i), half(b, bit, 1 - i), ALU.mult)
+
+        def small(name):
+            return cons.tile([128, 32], F32, name=name)[:]
+
+        def chain(cf, ks, name):
+            rs = [cf["rr"][:, ks[0], :]]
+            al, ial = cf["den"][:, ks[0], :], cf["inv"][:, ks[0], :]
+            for k in ks[1:]:
+                r = small("%s_r%d" % (name, k))
+                partner_mul(r, cf["rr"][:, k, :], al, k)
+                tt(nc.gpsimd, r, r, ial, ALU.mult)
+                a2 = small("%s_a%d" % (name, k))
+                tt(nc.gpsimd, a2, al, cf["den"][:, k, :], ALU.mult)
+                i2 = small("%s_i%d" % (name, k))
+                tt(nc.gpsimd, i2, ial, cf["inv"][:, k, :], ALU.mult)
+                rs.append(r)
+                al, ial = a2, i2
+            return rs, al
+
+        def closing(cf, k, al, name):
+            ss = small(name + "_ss")
+            so = small(name + "_so")
+            tt(nc.gpsimd, ss, cf["wd"][:, k, :], al, ALU.mult)
+            partner_mul(so, cf["wo"][:, k, :], al, k)
+            return ss, so
+
+        def first_bias(cf, b, name):
+            c0 = small(name + "_c")
+            t0 = small(name + "_t")
+            tt(nc.gpsimd, t0, cf["wd"][:, 0, :], b, ALU.mult)
+            partner_mul(c0, cf["wo"][:, 0, :], b, 0)
+            tt(nc.gpsimd, c0, c0, t0, ALU.add)
+            return c0
+
+        um = coefficients([(um_raw, 5)], "um")[0]
+        bm = cons.tile([128, 2, 32], F32, name="bm")
+        nc.gpsimd.tensor_copy(out=bm[:], in_=bm_raw[:])
+        c_main = first_bias(um, bm[:, 0, :], "um")
+        um_r, um_al = chain(um, (2, 3, 4), "um")
+        upb = bm[:, 1, :]
+
+        xc = cons.tile([128, 2, TOK], U32, name="xc", align_bytes=64)
+        xs = cons.tile([128, 2, TOK], U8, name="xs", align_bytes=64)
+        xc2 = cons.tile([128, 2, 128], U32, name="xc2", align_bytes=64)
+        xs2 = cons.tile([128, 2, 128], U8, name="xs2", align_bytes=64)
+        for g in range(2):
+            xg = work.tile([128, TOK * 4], BF16, tag="inter", name="xg", bufs=3, align_bytes=64)
+            for h in range(2):
+                ps = bank(0)
+                words = xraw[h][:].rearrange("p i d -> p (i d)").bitcast(F32)
+                for i in range(2):
+                    for u in range(2):
+                        w0 = 512 * i + 256 * g
+                        nc.tensor.transpose(ps[:, 256 * i + 128 * u : 256 * i + 128 * u + 128], words[:, w0 + u : w0 + 256 : 2], ident[:])
+                nc.vector.tensor_copy(out=xg[:].bitcast(F32)[:, 512 * h : 512 * h + 512].rearrange("p (i r u) -> p i r u", i=2, u=2),
+                                      in_=ps[:].rearrange("p (i u r) -> p i r u", i=2, u=2))
+            nc.vector.quantize_mx(out=xc[:, g, :].bitcast(FP8X4), scales=xs[:, g, :], in_=xg[:])
+            nc.vector.quantize_mx(out=xc2[:, g, :].bitcast(FP8X4), scales=xs2[:, g, :], in_=xg[:, 4 * N1 : 4 * N1 + 512])
+
+        zt = [cons.tile([128, H], F32, tag="zc", name="zt%d" % k, bufs=2, align_bytes=64) for k in range(2)]
+
+        def products(f, al):
+            def make(k):
+                prev = None
+                for j in range(7):
+                    n = 4 << j
+                    if j < 6:
+                        cur = tmp.tile([128, 2, 2 * n], F32, tag="p%d" % j, name="pj")
+                    else:
+                        cur = work.tile([128, 2, 2 * n], F32, tag="pmat", name="pmat", bufs=4)
+                    for o in range(2):
+                        src = f[j][:, 2 * k : 2 * k + 2, 2 * o :: 4]
+                        if j == 0:
+                            other = al[:, 8 * k : 8 * k + 8].rearrange("p (c t) -> p c t", t=4)
+                        else:
+                            other = prev[:]
+                        tt(nc.vector, cur[:, :, o * n : o * n + n], other, src, ALU.mult)
+                    prev = cur
+                return prev
+            return make
+
+        def pe_block(pm, b, y, n, dst):
+            nc.tensor.matmul(dst, pm[b // 8][:, (b // 4) % 2, b % 4 :: 4], y[:, 0:n], start=True, stop=True)
+
+        def norm(lo, hi, r, b, tile):
+            new = tile()
+            stt(new[:], hi[:], r[:, b[0] : b[0] + 1], lo[:])
+            stt(hi[:], lo[:], r[:, b[1] : b[1] + 1], hi[:])
+            return new, hi
+
+        def norm_stage(y, bit, r, tile, sel=None):
+            for lo, hi in pairs(bit):
+                if sel is None or (lo, hi) in sel:
+                    y[lo], y[hi] = norm(y[lo], y[hi], r, (lo, hi), tile)
+
+        def norm_psum(a_lo, ps_hi, r, b, tile):
+            hi = tile()
+            stt(hi[:], a_lo[:], r[:, b[1] : b[1] + 1], ps_hi)
+            stt(a_lo[:], ps_hi, r[:, b[0] : b[0] + 1], a_lo[:])
+            return a_lo, hi
+
+        def first_stage(ps_lo, ps_hi, cf, c0, b, tile):
+            res = []
+            for me, src in ((0, ps_lo), (1, ps_hi)):
+                a = tile()
+                scaled(a[:], src, cf["wd"][:, 0, b[me] : b[me] + 1], c0[:, b[me] : b[me] + 1])
+                res.append(a)
+            for me, other in ((0, ps_hi), (1, ps_lo)):
+                stt(res[me][:], other, cf["wo"][:, 0, b[me] : b[me] + 1], res[me][:])
+            return res
+
+        def close_pair(lo, hi, ss, so, b, tile, dst=None):
+            ts = []
+            for me, src in ((0, lo), (1, hi)):
+                t = tile()
+                scaled(t[:], src[:], ss[:, b[me] : b[me] + 1])
+                ts.append(t)
+            for me, other in ((0, hi), (1, lo)):
+                o = ts[me][:] if dst is None else dst[me]
+                stt(o, other[:], so[:, b[me] : b[me] + 1], ts[me][:])
+            return ts
+
+        p_up = products(f_up, um["den"][:, 1, :])
+        pm_up = {}
+        y1 = {}
+        for c in range(8):
+            if c not in wbs:
+                wbs[c] = load_wexp(c)
+            wb = wbs[c]
+            wc = work.tile([128, 2, 512], U32, tag="wc", name="wc", bufs=2, align_bytes=64)
+            ws = work.tile([128, 2, 512], U8, tag="ws", name="ws", bufs=2, align_bytes=64)
+            for g in range(2):
+                wd = work.tile([128, 4, 512], BF16, tag="wide", name="wd", bufs=3, align_bytes=64)
+                for j in range(4):
+                    nc.scalar.activation(out=wd[:, j, :], in_=wb[:, g, j, :].bitcast(FP8), func=ACT.Copy, scale=wsc[:, g, j : j + 1])
+                wi = work.tile([128, 2048], BF16, tag="inter", name="wi", bufs=3, align_bytes=64)
+                cp = nc.vector.tensor_copy if c < 2 and g == 0 else nc.scalar.copy
+                for t in range(4):
+                    cp(out=wi[:, 512 * t : 512 * t + 512].rearrange("p (m j) -> p m j", j=4),
+                       in_=wd[:].rearrange("p j (m t) -> p t m j", t=4)[:, t])
+                nc.vector.quantize_mx(out=wc[:, g, :].bitcast(FP8X4), scales=ws[:, g, :], in_=wi[:])
+            if c % 2 == 0:
+                pm_up[c // 2] = p_up(c // 2)
+            for t0 in (0, 2):
+                pss = []
+                for t in (t0, t0 + 1):
+                    ps = bank(0)
+                    for g in range(2):
+                        nc.tensor.matmul_mx(out=ps[:], lhsT=wc[:, g, 128 * t : 128 * t + 128].bitcast(FP8X4), lhsT_scale=ws[:, g, 128 * t : 128 * t + 128],
+                                            rhs=xc[:, g, :].bitcast(FP8X4), rhs_scale=xs[:, g, :], start=g == 0, stop=g == 1)
+                    pss.append(ps)
+                b = (4 * c + t0, 4 * c + t0 + 1)
+                y1[b[0]], y1[b[1]] = first_stage(pss[0][:, 0:N1], pss[1][:, 0:N1], um, c_main, b, y1tile)
+            for k, tok, loc in CHUNKS:
+                ps = bank(0)
+                for g in range(2):
+                    lc = xc2[:, g, :] if k == 0 else xc[:, g, tok : tok + 128]
+                    ls = xs2[:, g, :] if k == 0 else xs[:, g, tok : tok + 128]
+                    nc.tensor.matmul_mx(out=ps[:], lhsT=lc.bitcast(FP8X4), lhsT_scale=ls, rhs=wc[:, g, :].bitcast(FP8X4), rhs_scale=ws[:, g, :],
+                                        start=g == 0, stop=g == 1)
+                nc.scalar.copy(out=zt[k][:].rearrange("p (t c m) -> p c t m", t=4, c=8)[:, c], in_=ps[:].rearrange("p (t m) -> p t m", t=4))
+            for t in (0, 1):
+                b = (4 * c + t, 4 * c + t + 2)
+                y1[b[0]], y1[b[1]] = norm(y1[b[0]], y1[b[1]], um["rr"][:, 1, :], b, y1tile)
+            for t in range(4):
+                b = 4 * c + t
+                ps = bank(0)
+                pe_block(pm_up, b, y1[b], N1, ps[:, 0:N1])
+                if c % 2 == 0:
+                    a = y1tile()
+                    nc.scalar.copy(out=a[:], in_=ps[:, 0:N1])
+                    y1[b] = a
+                else:
+                    y1[b - 4], y1[b] = norm_psum(y1[b - 4], ps[:, 0:N1], um_r[0], (b - 4, b), y1tile)
+            if c % 4 == 3:
+                norm_stage(y1, 3, um_r[1], y1tile, [p for p in pairs(3) if p[0] // 16 == c // 4])
+
+        r1, r2, dm = coefficients([(r1_raw, 5), (r2_raw, 4), (dm_raw, 5)], "cf")
+        b2 = cons.tile([128, 32], F32, name="b2")
+        nc.gpsimd.tensor_copy(out=b2[:], in_=b2_raw[:])
+        c_r1 = first_bias(r1, b2[:], "r1")
+        r1_r, r1_al = chain(r1, (1, 2, 3), "r1")
+        r1_ss, r1_so = closing(r1, 4, r1_al, "r1")
+        r2_r, r2_al = chain(r2, (0, 1, 2), "r2")
+        r2_ss, r2_so = closing(r2, 3, r2_al, "r2")
+
+        def turn_back(view, blocks):
+            ps = bank(0)
+            for e, b in enumerate(blocks):
+                for k, tok, loc in CHUNKS:
+                    nc.tensor.transpose(ps[:, 256 * e + loc : 256 * e + loc + 128], view(zt[k], b), ident[:])
+            return [ps[:, 256 * e : 256 * e + N2] for e in range(2)]
+
+        def turn_out(y):
+            for b0 in range(0, 32, 4):
+                for k, tok, loc in CHUNKS:
+                    ps = bank(0)
+                    for e in range(4):
+                        nc.tensor.transpose(ps[:, 128 * e : 128 * e + 128], y[b0 + e][:, loc : loc + 128], ident[:])
+                    nc.scalar.copy(out=zt[k][:, 128 * b0 : 128 * b0 + 512], in_=ps[:])
+
+        y2 = {}
+        for b in pairs(0):
+            def view(z, l):
+                t, ml = l % 4, l // 4
+                return z[:, 1024 * t + ml : 1024 * t + 1024 : 8]
+            lo, hi = turn_back(view, b)
+            y2[b[0]], y2[b[1]] = first_stage(lo, hi, r1, c_r1, b, y2tile)
+        for bit in (1, 2, 3):
+            norm_stage(y2, bit, r1_r[bit - 1], y2tile)
+        for b in pairs(4):
+            y2[b[0]], y2[b[1]] = close_pair(y2[b[0]], y2[b[1]], r1_ss, r1_so, b, y2tile)
+        turn_out(y2)
+
+        y2 = {}
+        for b in pairs(0):
+            lo, hi = turn_back(lambda z, v: z[:, v::32], b)
+            a = y2tile()
+            nc.scalar.copy(out=a[:], in_=lo)
+            y2[b[0]], y2[b[1]] = norm_psum(a, hi, r2_r[0], b, y2tile)
+        for bit in (1, 2):
+            norm_stage(y2, bit, r2_r[bit], y2tile)
+        for b in pairs(3):
+            y2[b[0]], y2[b[1]] = close_pair(y2[b[0]], y2[b[1]], r2_ss, r2_so, b, y2tile)
+        turn_out(y2)
+
+        d01_r, d01_al = chain(dm, (0, 1), "d0")
+        d9_r, d9_al = chain(dm, (2, 3), "d9")
+        d_ss, d_so = closing(dm, 4, d9_al, "d11")
+        f_dn = load_factors(down_w)
+        p_dn = products(f_dn, d01_al)
+        pm_dn = {k: p_dn(k) for k in range(4)}
+
+        def gelu_blocks(y, blocks):
+            for b in blocks:
+                nc.scalar.activation(out=y[b][:], in_=y[b][:], func=ACT.Gelu, scale=um_al[:, b : b + 1], bias=upb[:, b : b + 1])
+
+        def down_first(y, tile, n):
+            for bit in (0, 1):
+                norm_stage(y, bit, d01_r[bit], tile)
+            for t in range(4):
+                for c in range(0, 8, 2):
+                    b = (4 * c + t, 4 * c + 4 + t)
+                    if 2 * n <= 512:
+                        ps = bank(0)
+                        dst = [ps[:, 0:n], ps[:, 256 : 256 + n]]
+                    else:
+                        dst = []
+                        for e in range(2):
+                            ps = bank(0)
+                            dst.append(ps[:, 0:n])
+                    for e in range(2):
+                        pe_block(pm_dn, b[e], y[b[e]], n, dst[e])
+                    a = tile()
+                    nc.scalar.copy(out=a[:], in_=dst[0])
+                    y[b[0]], y[b[1]] = norm_psum(a, dst[1], d9_r[0], b, tile)
+                norm_stage(y, 3, d9_r[1], tile, [p for p in pairs(3) if p[0] % 4 == t])
+
+        y2 = {}
+        for t in range(4):
+            for c in range(0, 8, 2):
+                b = (4 * c + t, 4 * c + 4 + t)
+                def view(z, blk):
+                    cc, tq = blk // 4, blk % 4
+                    z0 = (cc % 2) * 2048 + tq * 4 + cc // 2
+                    return z[:, z0 : (cc % 2) * 2048 + 2048 : 16]
+                lo, hi = turn_back(view, b)
+                a = y2tile()
+                nc.scalar.copy(out=a[:], in_=lo)
+                y2[b[0]], y2[b[1]] = norm_psum(a, hi, um_r[0], b, y2tile)
+            norm_stage(y2, 3, um_r[1], y2tile, [p for p in pairs(3) if p[0] % 4 == t])
+            norm_stage(y2, 4, um_r[2], y2tile, [p for p in pairs(4) if p[0] % 4 == t])
+            gelu_blocks(y2, range(t, 32, 4))
+        down_first(y2, y2tile, N2)
+
+        norm_stage(y1, 4, um_r[2], y1tile)
+        gelu_blocks(y1, range(32))
+        down_first(y1, y1tile, N1)
+
+        wcc = [cons.tile([128, 4, D], U32, tag="zc", name="wcc%d" % k, bufs=2, align_bytes=64) for k in range(2)]
+        wcs = cons.tile([128, 8, D], U8, name="wcs", align_bytes=64)
+        csrc = w_con.rearrange("(c p j) d -> c p j d", p=128, j=4)
+        for c in range(8):
+            for dh in range(2):
+                wr = work.tile([128, 4, 512], BF16, tag="wide", name="wr", bufs=3, align_bytes=64)
+                nc.sync.dma_start(out=wr[:], in_=csrc[c][:, :, 512 * dh : 512 * dh + 512])
+                wi = work.tile([128, 2048], BF16, tag="inter", name="wi2", bufs=3, align_bytes=64)
+                nc.scalar.copy(out=wi[:].rearrange("p (d j) -> p d j", j=4), in_=wr[:].rearrange("p j d -> p d j"))
+                nc.vector.quantize_mx(out=wcc[c // 4][:, c % 4, 512 * dh : 512 * dh + 512].bitcast(FP8X4), scales=wcs[:, c, 512 * dh : 512 * dh + 512], in_=wi[:])
+
+        bb = work.tile([128, D], F32, tag="wb", name="bb", bufs=3, align_bytes=64)
+        braw = []
+        for v in (b_con, down_bias):
+            br = work.tile([128, D], BF16, tag="wb", name="br", bufs=3, align_bytes=64)
+            nc.sync.dma_start(out=br[:], in_=v.partition_broadcast(128))
+            braw.append(br)
+        tt(nc.gpsimd, bb[:], braw[0][:], braw[1][:], ALU.add)
+
+        ht = cons.tile([128, 8, 4, TOK], BF16, tag="fh", name="ht")
+        for c in range(4):
+            for y, tile, t0, n in ((y1, y1tile, 0, N1), (y2, y2tile, N1, N2)):
+                for t in range(4):
+                    b = (4 * c + t, 4 * c + 16 + t)
+                    close_pair(y[b[0]], y[b[1]], d_ss, d_so, b, tile, [ht[:, cc, t, t0 : t0 + n] for cc in (c, c + 4)])
+        orows = out.rearrange("b s d -> (b s) d")
+        order = [0, 4, 1, 5, 2, 6, 3, 7]
+        for hf in range(2):
+            acc = {}
+            for i in range(2):
+                for dh in range(2):
+                    acc[i, dh] = bank(0)
+            for n, c in enumerate(order):
+                hi = work.tile([128, 1024], BF16, tag="inter", name="hi", bufs=3, align_bytes=64)
+                nc.scalar.copy(out=hi[:].rearrange("p (r t) -> p r t", t=4), in_=ht[:, c, :, 256 * hf : 256 * hf + 256].rearrange("p t r -> p r t"))
+                hq = work.tile([128, 256], U32, tag="wc", name="hq", bufs=2, align_bytes=64)
+                hs = work.tile([128, 256], U8, tag="ws", name="hs", bufs=2, align_bytes=64)
+                nc.vector.quantize_mx(out=hq[:].bitcast(FP8X4), scales=hs[:], in_=hi[:])
+                for i in range(2):
+                    for dh in range(2):
+                        nc.tensor.matmul_mx(out=acc[i, dh][:], lhsT=hq[:, 128 * i : 128 * i + 128].bitcast(FP8X4), lhsT_scale=hs[:, 128 * i : 128 * i + 128],
+                                            rhs=wcc[c // 4][:, c % 4, 512 * dh : 512 * dh + 512].bitcast(FP8X4), rhs_scale=wcs[:, c, 512 * dh : 512 * dh + 512],
+                                            start=n == 0, stop=n == 7)
+            for i in range(2):
+                for dh in range(2):
+                    ot = work.tile([128, 512], F32, tag="wb", name="ot", bufs=3, align_bytes=64)
+                    tt(nc.vector, ot[:], acc[i, dh][:], bb[:, 512 * dh : 512 * dh + 512], ALU.add)
+                    r0 = 256 * hf + 128 * i
+                    nc.sync.dma_start(out=orows[r0 : r0 + 128, 512 * dh : 512 * dh + 512], in_=ot[:])

@@ -17,6 +17,9 @@ FLOPS = 2 * 2 * TOK * D * H + 2 * 12 * 3 * TOK * H
 
 N1 = 304
 N2 = TOK - N1
+GROUP = 2
+NFULL = 35
+NEXTRA = 6
 CHUNKS = ((0, N1, 0), (1, 384, 384 - N1))
 
 
@@ -36,11 +39,17 @@ def tile_butterflymlp_kernel(tc, x, w_bytes, w_scale, b_exp, up_w, up_bias, down
             ps = psum.tile([128, 512], F32, tag="ps", name="ps")
             return ps
 
-        def y1tile():
-            return work.tile([128, N1], F32, tag="y1", name="y1", bufs=35)
+        areas = [cons.tile([128, TOK], F32, name="ar%d" % k) for k in range(NFULL)]
+        areas += [cons.tile([128, N2], F32, name="ax%d" % k) for k in range(NEXTRA)]
 
-        def y2tile():
-            return work.tile([128, N2], F32, tag="y2", name="y2", bufs=34)
+        def full(k):
+            return areas[k][:]
+
+        def left(k):
+            return areas[k][:, 0:N1]
+
+        def right(k):
+            return areas[k][:, N1:TOK] if k < NFULL else areas[k][:]
 
         def stt(o, in0, s, in1):
             nc.vector.scalar_tensor_tensor(out=o, in0=in0, scalar=s, in1=in1, op0=ALU.mult, op1=ALU.add)
@@ -115,13 +124,6 @@ def tile_butterflymlp_kernel(tc, x, w_bytes, w_scale, b_exp, up_w, up_bias, down
             return views
 
         f_up = load_factors(up_w)
-        r2_raw = cons.tile([128, 4, 64], BF16, name="r2_raw")
-        for k in range(4):
-            src = up_w[5 + k].rearrange("k o i -> (k o i)").rearrange("(h u l q) -> h l u q", h=4, u=16, l=32)
-            for h in range(4):
-                nc.sync.dma_start(out=r2_raw[h::4, k, :].rearrange("p (u q) -> p u q", q=4), in_=src[h])
-
-        dm_raw = load_main(down_w, "dm_raw")
 
         def tt(eng, o, a, b, op):
             eng.tensor_tensor(out=o, in0=a, in1=b, op=op)
@@ -143,9 +145,9 @@ def tile_butterflymlp_kernel(tc, x, w_bytes, w_scale, b_exp, up_w, up_bias, down
                 k0 += m
             d = wd[:].rearrange("p k b -> p (k b)")
             o = wo[:].rearrange("p k b -> p (k b)")
-            ta = tmp.tile([128, 448], F32, tag="ta", name="ta")[:, 0 : 32 * n]
-            tb = tmp.tile([128, 448], F32, tag="tb", name="tb")[:, 0 : 32 * n]
-            tk = tmp.tile([128, 448], F32, tag="tk", name="tk")[:, 0 : 32 * n]
+            ta = work.tile([128, 1024], F32, tag="pmat", name="ta", bufs=4)[:, 0 : 32 * n]
+            tb = work.tile([128, 1024], F32, tag="pmat", name="tb", bufs=4)[:, 0 : 32 * n]
+            tk = work.tile([128, 1024], F32, tag="pmat", name="tk", bufs=4)[:, 0 : 32 * n]
             den = cons.tile([128, n, 32], F32, name=name + "_den")
             inv = cons.tile([128, n, 32], F32, name=name + "_inv")
             rr = cons.tile([128, n, 32], F32, name=name + "_rr")
@@ -253,46 +255,73 @@ def tile_butterflymlp_kernel(tc, x, w_bytes, w_scale, b_exp, up_w, up_bias, down
                 return prev
             return make
 
-        def pe_block(pm, b, y, n, dst):
-            nc.tensor.matmul(dst, pm[b // 8][:, (b // 4) % 2, b % 4 :: 4], y[:, 0:n], start=True, stop=True)
+        def pe_block(pm, b, y, dst):
+            nc.tensor.matmul(dst, pm[b // 8][:, (b // 4) % 2, b % 4 :: 4], y, start=True, stop=True)
 
-        def norm(lo, hi, r, b, tile):
-            new = tile()
-            stt(new[:], hi[:], r[:, b[0] : b[0] + 1], lo[:])
-            stt(hi[:], lo[:], r[:, b[1] : b[1] + 1], hi[:])
-            return new, hi
+        def norm_group(y, group, r, view, new, done):
+            fresh = {}
+            for lo, hi in group:
+                fresh[lo] = new(lo)
+                stt(view(fresh[lo]), view(y[hi]), r[:, lo : lo + 1], view(y[lo]))
+            for lo, hi in group:
+                stt(view(y[hi]), view(y[lo]), r[:, hi : hi + 1], view(y[hi]))
+                done(y[lo])
+                y[lo] = fresh[lo]
 
-        def norm_stage(y, bit, r, tile, sel=None):
-            for lo, hi in pairs(bit):
-                if sel is None or (lo, hi) in sel:
-                    y[lo], y[hi] = norm(y[lo], y[hi], r, (lo, hi), tile)
+        def norm_stage(y, todo, r, view, new, done):
+            for k in range(0, len(todo), GROUP):
+                norm_group(y, todo[k : k + GROUP], r, view, new, done)
 
-        def norm_psum(a_lo, ps_hi, r, b, tile):
-            hi = tile()
-            stt(hi[:], a_lo[:], r[:, b[1] : b[1] + 1], ps_hi)
-            stt(a_lo[:], ps_hi, r[:, b[0] : b[0] + 1], a_lo[:])
-            return a_lo, hi
+        def norm_psum(y, group, ps, r, view, new):
+            for lo, hi in group:
+                y[hi] = new(hi)
+                stt(view(y[hi]), view(y[lo]), r[:, hi : hi + 1], ps[hi])
+            for lo, hi in group:
+                stt(view(y[lo]), ps[hi], r[:, lo : lo + 1], view(y[lo]))
 
-        def first_stage(ps_lo, ps_hi, cf, c0, b, tile):
-            res = []
-            for me, src in ((0, ps_lo), (1, ps_hi)):
-                a = tile()
-                scaled(a[:], src, cf["wd"][:, 0, b[me] : b[me] + 1], c0[:, b[me] : b[me] + 1])
-                res.append(a)
-            for me, other in ((0, ps_hi), (1, ps_lo)):
-                stt(res[me][:], other, cf["wo"][:, 0, b[me] : b[me] + 1], res[me][:])
-            return res
+        def first_stage(y, ps, cf, c0, b, view, new):
+            for k in b:
+                y[k] = new(k)
+                scaled(view(y[k]), ps[k], cf["wd"][:, 0, k : k + 1], c0[:, k : k + 1])
+            for k in b:
+                stt(view(y[k]), ps[k ^ 1], cf["wo"][:, 0, k : k + 1], view(y[k]))
 
-        def close_pair(lo, hi, ss, so, b, tile, dst=None):
-            ts = []
-            for me, src in ((0, lo), (1, hi)):
-                t = tile()
-                scaled(t[:], src[:], ss[:, b[me] : b[me] + 1])
-                ts.append(t)
-            for me, other in ((0, hi), (1, lo)):
-                o = ts[me][:] if dst is None else dst[me]
-                stt(o, other[:], so[:, b[me] : b[me] + 1], ts[me][:])
-            return ts
+        def close_pair(y, b, ss, so, view, new, done, dst=None):
+            ts = {}
+            for k in b:
+                ts[k] = new(k)
+                scaled(view(ts[k]), view(y[k]), ss[:, k : k + 1])
+            for k in b:
+                other = b[0] + b[1] - k
+                stt(view(ts[k]) if dst is None else dst[k], view(y[other]), so[:, k : k + 1], view(ts[k]))
+            for k in b:
+                done(y[k])
+                if dst is None:
+                    y[k] = ts[k]
+                else:
+                    done(ts[k])
+
+        lfree = list(range(NFULL))
+        rfree = list(range(NFULL + NEXTRA))
+        placed = {}
+
+        def lnew(k):
+            return lfree.pop(0)
+
+        def rnew(k):
+            return rfree.pop(0)
+
+        def logged(step):
+            def new(k):
+                placed[step, k] = lfree.pop(0)
+                return placed[step, k]
+            return new
+
+        def replay(step):
+            return lambda k: placed[step, k]
+
+        def keep(a):
+            return None
 
         p_up = products(f_up, um["den"][:, 1, :])
         pm_up = {}
@@ -308,7 +337,7 @@ def tile_butterflymlp_kernel(tc, x, w_bytes, w_scale, b_exp, up_w, up_bias, down
                 for j in range(4):
                     nc.scalar.activation(out=wd[:, j, :], in_=wb[:, g, j, :].bitcast(FP8), func=ACT.Copy, scale=wsc[:, g, j : j + 1])
                 wi = work.tile([128, 2048], BF16, tag="inter", name="wi", bufs=3, align_bytes=64)
-                cp = nc.vector.tensor_copy if c < 2 and g == 0 else nc.scalar.copy
+                cp = nc.vector.tensor_copy if g == 0 else nc.scalar.copy
                 for t in range(4):
                     cp(out=wi[:, 512 * t : 512 * t + 512].rearrange("p (m j) -> p m j", j=4),
                        in_=wd[:].rearrange("p j (m t) -> p t m j", t=4)[:, t])
@@ -316,15 +345,14 @@ def tile_butterflymlp_kernel(tc, x, w_bytes, w_scale, b_exp, up_w, up_bias, down
             if c % 2 == 0:
                 pm_up[c // 2] = p_up(c // 2)
             for t0 in (0, 2):
-                pss = []
+                pss = {}
                 for t in (t0, t0 + 1):
                     ps = bank(0)
                     for g in range(2):
                         nc.tensor.matmul_mx(out=ps[:], lhsT=wc[:, g, 128 * t : 128 * t + 128].bitcast(FP8X4), lhsT_scale=ws[:, g, 128 * t : 128 * t + 128],
                                             rhs=xc[:, g, :].bitcast(FP8X4), rhs_scale=xs[:, g, :], start=g == 0, stop=g == 1)
-                    pss.append(ps)
-                b = (4 * c + t0, 4 * c + t0 + 1)
-                y1[b[0]], y1[b[1]] = first_stage(pss[0][:, 0:N1], pss[1][:, 0:N1], um, c_main, b, y1tile)
+                    pss[4 * c + t] = ps[:, 0:N1]
+                first_stage(y1, pss, um, c_main, (4 * c + t0, 4 * c + t0 + 1), left, lnew)
             for k, tok, loc in CHUNKS:
                 ps = bank(0)
                 for g in range(2):
@@ -332,23 +360,30 @@ def tile_butterflymlp_kernel(tc, x, w_bytes, w_scale, b_exp, up_w, up_bias, down
                     ls = xs2[:, g, :] if k == 0 else xs[:, g, tok : tok + 128]
                     nc.tensor.matmul_mx(out=ps[:], lhsT=lc.bitcast(FP8X4), lhsT_scale=ls, rhs=wc[:, g, :].bitcast(FP8X4), rhs_scale=ws[:, g, :],
                                         start=g == 0, stop=g == 1)
-                nc.scalar.copy(out=zt[k][:].rearrange("p (t c m) -> p c t m", t=4, c=8)[:, c], in_=ps[:].rearrange("p (t m) -> p t m", t=4))
-            for t in (0, 1):
-                b = (4 * c + t, 4 * c + t + 2)
-                y1[b[0]], y1[b[1]] = norm(y1[b[0]], y1[b[1]], um["rr"][:, 1, :], b, y1tile)
-            for t in range(4):
-                b = 4 * c + t
-                ps = bank(0)
-                pe_block(pm_up, b, y1[b], N1, ps[:, 0:N1])
-                if c % 2 == 0:
-                    a = y1tile()
-                    nc.scalar.copy(out=a[:], in_=ps[:, 0:N1])
-                    y1[b] = a
-                else:
-                    y1[b - 4], y1[b] = norm_psum(y1[b - 4], ps[:, 0:N1], um_r[0], (b - 4, b), y1tile)
+                nc.scalar.copy(out=zt[k][:].rearrange("p (t l c h) -> p c t l h", t=4, l=8, c=8)[:, c], in_=ps[:].rearrange("p (t h l) -> p t l h", t=4, l=8))
+            norm_group(y1, [(4 * c + t, 4 * c + t + 2) for t in (0, 1)], um["rr"][:, 1, :], left, lnew, lfree.append)
+            for t0 in (0, 2):
+                pss = {}
+                for t in (t0, t0 + 1):
+                    b = 4 * c + t
+                    ps = bank(0)
+                    pe_block(pm_up, b, left(y1[b]), ps[:, 0:N1])
+                    lfree.append(y1[b])
+                    pss[b] = ps[:, 0:N1]
+                    if c % 2 == 0:
+                        y1[b] = logged("lo")(b)
+                        nc.scalar.copy(out=left(y1[b]), in_=ps[:, 0:N1])
+                if c % 2 == 1:
+                    norm_psum(y1, [(b - 4, b) for b in (4 * c + t0, 4 * c + t0 + 1)], pss, um_r[0], left, logged("hi"))
             if c % 4 == 3:
-                norm_stage(y1, 3, um_r[1], y1tile, [p for p in pairs(3) if p[0] // 16 == c // 4])
+                norm_stage(y1, [p for p in pairs(3) if p[0] // 16 == c // 4], um_r[1], left, logged("s10"), lfree.append)
 
+        r2_raw = cons.tile([128, 4, 64], BF16, name="r2_raw")
+        for k in range(4):
+            src = up_w[5 + k].rearrange("k o i -> (k o i)").rearrange("(h u l q) -> h l u q", h=4, u=16, l=32)
+            for h in range(4):
+                nc.sync.dma_start(out=r2_raw[h::4, k, :].rearrange("p (u q) -> p u q", q=4), in_=src[h])
+        dm_raw = load_main(down_w, "dm_raw")
         r1, r2, dm = coefficients([(r1_raw, 5), (r2_raw, 4), (dm_raw, 5)], "cf")
         b2 = cons.tile([128, 32], F32, name="b2")
         nc.gpsimd.tensor_copy(out=b2[:], in_=b2_raw[:])
@@ -357,99 +392,103 @@ def tile_butterflymlp_kernel(tc, x, w_bytes, w_scale, b_exp, up_w, up_bias, down
         r1_ss, r1_so = closing(r1, 4, r1_al, "r1")
         r2_r, r2_al = chain(r2, (0, 1, 2), "r2")
         r2_ss, r2_so = closing(r2, 3, r2_al, "r2")
-
-        def turn_back(view, blocks):
-            ps = bank(0)
-            for e, b in enumerate(blocks):
-                for k, tok, loc in CHUNKS:
-                    nc.tensor.transpose(ps[:, 256 * e + loc : 256 * e + loc + 128], view(zt[k], b), ident[:])
-            return [ps[:, 256 * e : 256 * e + N2] for e in range(2)]
-
-        def turn_out(y):
-            for b0 in range(0, 32, 4):
-                for k, tok, loc in CHUNKS:
-                    ps = bank(0)
-                    for e in range(4):
-                        nc.tensor.transpose(ps[:, 128 * e : 128 * e + 128], y[b0 + e][:, loc : loc + 128], ident[:])
-                    nc.scalar.copy(out=zt[k][:, 128 * b0 : 128 * b0 + 512], in_=ps[:])
-
-        y2 = {}
-        for b in pairs(0):
-            def view(z, l):
-                t, ml = l % 4, l // 4
-                return z[:, 1024 * t + ml : 1024 * t + 1024 : 8]
-            lo, hi = turn_back(view, b)
-            y2[b[0]], y2[b[1]] = first_stage(lo, hi, r1, c_r1, b, y2tile)
-        for bit in (1, 2, 3):
-            norm_stage(y2, bit, r1_r[bit - 1], y2tile)
-        for b in pairs(4):
-            y2[b[0]], y2[b[1]] = close_pair(y2[b[0]], y2[b[1]], r1_ss, r1_so, b, y2tile)
-        turn_out(y2)
-
-        y2 = {}
-        for b in pairs(0):
-            lo, hi = turn_back(lambda z, v: z[:, v::32], b)
-            a = y2tile()
-            nc.scalar.copy(out=a[:], in_=lo)
-            y2[b[0]], y2[b[1]] = norm_psum(a, hi, r2_r[0], b, y2tile)
-        for bit in (1, 2):
-            norm_stage(y2, bit, r2_r[bit], y2tile)
-        for b in pairs(3):
-            y2[b[0]], y2[b[1]] = close_pair(y2[b[0]], y2[b[1]], r2_ss, r2_so, b, y2tile)
-        turn_out(y2)
-
         d01_r, d01_al = chain(dm, (0, 1), "d0")
         d9_r, d9_al = chain(dm, (2, 3), "d9")
         d_ss, d_so = closing(dm, 4, d9_al, "d11")
         f_dn = load_factors(down_w)
+
+        def turn_back(place, b):
+            ps = bank(0)
+            for e in range(2):
+                for k, tok, loc in CHUNKS:
+                    z0 = 128 * place(b[e])
+                    nc.tensor.transpose(ps[:, 256 * e + loc : 256 * e + loc + 128], zt[k][:, z0 : z0 + 128], ident[:])
+            return {b[0]: ps[:, 0:N2], b[1]: ps[:, 256 : 256 + N2]}
+
+        def turn_out(y, to, frm):
+            for b0 in range(0, 32, 4):
+                for k, tok, loc in CHUNKS:
+                    ps = bank(0)
+                    for e in range(4):
+                        nc.tensor.transpose(ps[:, 128 * e : 128 * e + 128], right(y[b0 + e])[:, loc : loc + 128], ident[:])
+                    nc.scalar.copy(out=to(zt[k], b0 // 4), in_=frm(ps))
+                for e in range(4):
+                    rfree.append(y[b0 + e])
+
+        y2 = {}
+        for b in pairs(0):
+            first_stage(y2, turn_back(lambda l: 8 * (l % 4) + l // 4, b), r1, c_r1, b, right, rnew)
+        for bit in (1, 2, 3):
+            norm_stage(y2, pairs(bit), r1_r[bit - 1], right, rnew, rfree.append)
+        for b in pairs(4):
+            close_pair(y2, b, r1_ss, r1_so, right, rnew, rfree.append)
+        turn_out(y2, lambda z, g: z[:].rearrange("p (v g l h) -> p g v l h", v=32, g=8, l=4)[:, g],
+                 lambda ps: ps[:].rearrange("p (l h v) -> p v l h", l=4, h=4))
+
+        d0_todo = pairs(0)
+        d1_todo = [p for t in (0, 1) for p in pairs(1) if p[0] % 4 == t]
+
+        def to_second(y, view, new, done):
+            norm_stage(y, pairs(4), um_r[2], view, new("s11"), done)
+            for b in range(32):
+                nc.scalar.activation(out=view(y[b]), in_=view(y[b]), func=ACT.Gelu, scale=um_al[:, b : b + 1], bias=upb[:, b : b + 1])
+            norm_stage(y, d0_todo, d01_r[0], view, new("d0"), done)
+            norm_stage(y, d1_todo, d01_r[1], view, new("d1"), done)
+
+        to_second(y1, left, logged, lfree.append)
+
+        y2 = {}
+        for k in range(0, 16, GROUP):
+            group = pairs(0)[k : k + GROUP]
+            his = {}
+            for b in group:
+                ps = turn_back(lambda v: v, b)
+                y2[b[0]] = rnew(b[0])
+                nc.scalar.copy(out=right(y2[b[0]]), in_=ps[b[0]])
+                his[b[1]] = ps[b[1]]
+            norm_psum(y2, group, his, r2_r[0], right, rnew)
+        for bit in (1, 2):
+            norm_stage(y2, pairs(bit), r2_r[bit], right, rnew, rfree.append)
+        for b in pairs(3):
+            close_pair(y2, b, r2_ss, r2_so, right, rnew, rfree.append)
+        turn_out(y2, lambda z, g: z[:].rearrange("p (e x g v l) -> p e g x v l", e=2, x=16, g=4, v=4)[:, g // 4, g % 4],
+                 lambda ps: ps[:].rearrange("p (v l x) -> p x v l", v=4, l=8))
+
         p_dn = products(f_dn, d01_al)
         pm_dn = {k: p_dn(k) for k in range(4)}
 
-        def gelu_blocks(y, blocks):
-            for b in blocks:
-                nc.scalar.activation(out=y[b][:], in_=y[b][:], func=ACT.Gelu, scale=um_al[:, b : b + 1], bias=upb[:, b : b + 1])
-
-        def down_first(y, tile, n):
-            for bit in (0, 1):
-                norm_stage(y, bit, d01_r[bit], tile)
-            for t in range(4):
-                for c in range(0, 8, 2):
-                    b = (4 * c + t, 4 * c + 4 + t)
-                    if 2 * n <= 512:
-                        ps = bank(0)
-                        dst = [ps[:, 0:n], ps[:, 256 : 256 + n]]
-                    else:
-                        dst = []
-                        for e in range(2):
-                            ps = bank(0)
-                            dst.append(ps[:, 0:n])
-                    for e in range(2):
-                        pe_block(pm_dn, b[e], y[b[e]], n, dst[e])
-                    a = tile()
-                    nc.scalar.copy(out=a[:], in_=dst[0])
-                    y[b[0]], y[b[1]] = norm_psum(a, dst[1], d9_r[0], b, tile)
-                norm_stage(y, 3, d9_r[1], tile, [p for p in pairs(3) if p[0] % 4 == t])
-
         y2 = {}
-        for t in range(4):
-            for c in range(0, 8, 2):
-                b = (4 * c + t, 4 * c + 4 + t)
-                def view(z, blk):
-                    cc, tq = blk // 4, blk % 4
-                    z0 = (cc % 2) * 2048 + tq * 4 + cc // 2
-                    return z[:, z0 : (cc % 2) * 2048 + 2048 : 16]
-                lo, hi = turn_back(view, b)
-                a = y2tile()
-                nc.scalar.copy(out=a[:], in_=lo)
-                y2[b[0]], y2[b[1]] = norm_psum(a, hi, um_r[0], b, y2tile)
-            norm_stage(y2, 3, um_r[1], y2tile, [p for p in pairs(3) if p[0] % 4 == t])
-            norm_stage(y2, 4, um_r[2], y2tile, [p for p in pairs(4) if p[0] % 4 == t])
-            gelu_blocks(y2, range(t, 32, 4))
-        down_first(y2, y2tile, N2)
+        for c in range(0, 8, 2):
+            for t0 in (0, 2):
+                todo = [(4 * c + t, 4 * c + 4 + t) for t in (t0, t0 + 1)]
+                his = {}
+                for b in todo:
+                    ps = turn_back(lambda k: 16 * (k // 4 % 2) + 4 * (k % 4) + k // 8, b)
+                    y2[b[0]] = placed["lo", b[0]]
+                    nc.scalar.copy(out=right(y2[b[0]]), in_=ps[b[0]])
+                    his[b[1]] = ps[b[1]]
+                norm_psum(y2, todo, his, um_r[0], right, replay("hi"))
+            if c % 4 == 2:
+                norm_stage(y2, [p for p in pairs(3) if p[0] // 16 == c // 4], um_r[1], right, replay("s10"), keep)
+        to_second(y2, right, replay, keep)
 
-        norm_stage(y1, 4, um_r[2], y1tile)
-        gelu_blocks(y1, range(32))
-        down_first(y1, y1tile, N1)
+        y = y1
+        for t in (0, 2, 1, 3):
+            todo = [(4 * c + t, 4 * c + 4 + t) for c in range(0, 8, 2)]
+            for k in range(0, 4, GROUP):
+                his = {}
+                for b in todo[k : k + GROUP]:
+                    for blk in b:
+                        ps = bank(0)
+                        pe_block(pm_dn, blk, full(y[blk]), ps[:])
+                        lfree.append(y[blk])
+                        if blk == b[0]:
+                            y[blk] = lnew(blk)
+                            nc.scalar.copy(out=full(y[blk]), in_=ps[:])
+                        else:
+                            his[blk] = ps[:]
+                norm_psum(y, todo[k : k + GROUP], his, d9_r[0], full, lnew)
+            norm_stage(y, [p for p in pairs(3) if p[0] % 4 == t], d9_r[1], full, lnew, lfree.append)
 
         wcc = [cons.tile([128, 4, D], U32, tag="zc", name="wcc%d" % k, bufs=2, align_bytes=64) for k in range(2)]
         wcs = cons.tile([128, 8, D], U8, name="wcs", align_bytes=64)
@@ -472,31 +511,25 @@ def tile_butterflymlp_kernel(tc, x, w_bytes, w_scale, b_exp, up_w, up_bias, down
 
         ht = cons.tile([128, 8, 4, TOK], BF16, tag="fh", name="ht")
         for c in range(4):
-            for y, tile, t0, n in ((y1, y1tile, 0, N1), (y2, y2tile, N1, N2)):
-                for t in range(4):
-                    b = (4 * c + t, 4 * c + 16 + t)
-                    close_pair(y[b[0]], y[b[1]], d_ss, d_so, b, tile, [ht[:, cc, t, t0 : t0 + n] for cc in (c, c + 4)])
+            for t in range(4):
+                b = (4 * c + t, 4 * c + 16 + t)
+                close_pair(y, b, d_ss, d_so, full, lnew, lfree.append, {b[0]: ht[:, c, t, :], b[1]: ht[:, c + 4, t, :]})
         orows = out.rearrange("b s d -> (b s) d")
-        order = [0, 4, 1, 5, 2, 6, 3, 7]
-        for hf in range(2):
-            acc = {}
-            for i in range(2):
-                for dh in range(2):
-                    acc[i, dh] = bank(0)
-            for n, c in enumerate(order):
-                hi = work.tile([128, 1024], BF16, tag="inter", name="hi", bufs=3, align_bytes=64)
-                nc.scalar.copy(out=hi[:].rearrange("p (r t) -> p r t", t=4), in_=ht[:, c, :, 256 * hf : 256 * hf + 256].rearrange("p t r -> p r t"))
-                hq = work.tile([128, 256], U32, tag="wc", name="hq", bufs=2, align_bytes=64)
-                hs = work.tile([128, 256], U8, tag="ws", name="hs", bufs=2, align_bytes=64)
-                nc.vector.quantize_mx(out=hq[:].bitcast(FP8X4), scales=hs[:], in_=hi[:])
-                for i in range(2):
-                    for dh in range(2):
-                        nc.tensor.matmul_mx(out=acc[i, dh][:], lhsT=hq[:, 128 * i : 128 * i + 128].bitcast(FP8X4), lhsT_scale=hs[:, 128 * i : 128 * i + 128],
-                                            rhs=wcc[c // 4][:, c % 4, 512 * dh : 512 * dh + 512].bitcast(FP8X4), rhs_scale=wcs[:, c, 512 * dh : 512 * dh + 512],
-                                            start=n == 0, stop=n == 7)
-            for i in range(2):
-                for dh in range(2):
-                    ot = work.tile([128, 512], F32, tag="wb", name="ot", bufs=3, align_bytes=64)
-                    tt(nc.vector, ot[:], acc[i, dh][:], bb[:, 512 * dh : 512 * dh + 512], ALU.add)
-                    r0 = 256 * hf + 128 * i
-                    nc.sync.dma_start(out=orows[r0 : r0 + 128, 512 * dh : 512 * dh + 512], in_=ot[:])
+        acc = [bank(0) for n in range(8)]
+        for n, c in enumerate((0, 4, 1, 5, 2, 6, 3, 7)):
+            hi = work.tile([128, 2048], BF16, tag="inter", name="hi", bufs=3, align_bytes=64)
+            cp = nc.scalar.copy if n % 2 == 0 else nc.vector.tensor_copy
+            cp(out=hi[:].rearrange("p (r t) -> p r t", t=4), in_=ht[:, c].rearrange("p t r -> p r t"))
+            hq = work.tile([128, 512], U32, tag="wc", name="hq", bufs=2, align_bytes=64)
+            hs = work.tile([128, 512], U8, tag="ws", name="hs", bufs=2, align_bytes=64)
+            nc.vector.quantize_mx(out=hq[:].bitcast(FP8X4), scales=hs[:], in_=hi[:])
+            for k in range(8):
+                i, dh = k // 2, k % 2
+                nc.tensor.matmul_mx(out=acc[k][:], lhsT=hq[:, 128 * i : 128 * i + 128].bitcast(FP8X4), lhsT_scale=hs[:, 128 * i : 128 * i + 128],
+                                    rhs=wcc[c // 4][:, c % 4, 512 * dh : 512 * dh + 512].bitcast(FP8X4), rhs_scale=wcs[:, c, 512 * dh : 512 * dh + 512],
+                                    start=n == 0, stop=n == 7)
+        for k in range(8):
+            i, dh = k // 2, k % 2
+            ot = work.tile([128, 512], F32, tag="wb", name="ot", bufs=3, align_bytes=64)
+            tt(nc.vector, ot[:], acc[k][:], bb[:, 512 * dh : 512 * dh + 512], ALU.add)
+            nc.sync.dma_start(out=orows[128 * i : 128 * i + 128, 512 * dh : 512 * dh + 512], in_=ot[:])

@@ -17,7 +17,6 @@ FLOPS = 2 * 2 * TOK * D * H + 2 * 12 * 3 * TOK * H
 
 N1 = 304
 N2 = TOK - N1
-GROUP = 2
 NFULL = 35
 NEXTRA = 6
 CHUNKS = ((0, N1, 0), (1, 384, 384 - N1))
@@ -34,8 +33,9 @@ def tile_butterflymlp_kernel(tc, x, w_bytes, w_scale, b_exp, up_w, up_bias, down
         tmp = ctx.enter_context(tc.tile_pool(name="tmp", bufs=1))
         work = ctx.enter_context(tc.tile_pool(name="work", bufs=2))
         psum = ctx.enter_context(tc.psum_pool(name="psum", bufs=8))
+        ctx.enter_context(tc.manual_schedule())
 
-        def bank(shape):
+        def bank():
             ps = psum.tile([128, 512], F32, tag="ps", name="ps")
             return ps
 
@@ -62,8 +62,17 @@ def tile_butterflymlp_kernel(tc, x, w_bytes, w_scale, b_exp, up_w, up_bias, down
 
         ident = cons.tile([128, 128], F32, name="ident")
         make_identity(nc, ident[:])
+        wsrc = w_bytes.rearrange("(g p t) n -> g p t n", g=2, t=4)
         wsc = cons.tile([128, 2, 4], F32, name="wsc")
         nc.sync.dma_start(out=wsc[:], in_=w_scale.rearrange("(g p t) o -> p g (t o)", g=2, t=4))
+        wbs = {}
+
+        def load_wexp(c):
+            wbs[c] = work.tile([128, 2, 4, 512], U8, tag="wb", name="wb", bufs=3, align_bytes=64)
+            for g in range(2):
+                nc.sync.dma_start(out=wbs[c][:, g, :, :], in_=wsrc[g][:, :, 512 * c : 512 * c + 512])
+
+        load_wexp(0)
         xrows = x.rearrange("b s d -> (b s) d").rearrange("(i p) d -> p i d", p=128)
         xraw = []
         for h in range(2):
@@ -71,36 +80,21 @@ def tile_butterflymlp_kernel(tc, x, w_bytes, w_scale, b_exp, up_w, up_bias, down
             nc.sync.dma_start(out=xr[:], in_=xrows[:, 2 * h : 2 * h + 2, :])
             xraw.append(xr)
 
-        wsrc = w_bytes.rearrange("(g p t) n -> g p t n", g=2, t=4)
-
-        def load_wexp(c):
-            wb = work.tile([128, 2, 4, 512], U8, tag="wb", name="wb", bufs=3, align_bytes=64)
-            for g in range(2):
-                nc.sync.dma_start(out=wb[:, g, :, :], in_=wsrc[g][:, :, 512 * c : 512 * c + 512])
-            return wb
-
-        wbs = {0: load_wexp(0)}
+        def flat(w, s):
+            return w[s].rearrange("k o i -> (k o i)")
 
         def load_main(w, name):
             raw = cons.tile([128, 5, 64], BF16, name=name)
-            for k, s in ((0, 0), (1, 1)):
-                nc.sync.dma_start(out=raw[:, k, :].rearrange("p (c r) -> p c r", c=8),
-                                  in_=w[s].rearrange("k o i -> (k o i)").rearrange("(c p r) -> p c r", p=128, r=8))
-            for k, s in ((2, 9), (3, 10), (4, 11)):
-                nc.sync.dma_start(out=raw[:, k, :].rearrange("p (c r) -> p c r", c=4),
-                                  in_=w[s].rearrange("k o i -> (k o i)").rearrange("(c p r) -> p c r", p=128, r=16))
+            for k, s in enumerate((0, 1, 9, 10, 11)):
+                n = 8 if k < 2 else 4
+                nc.sync.dma_start(out=raw[:, k, :].rearrange("p (c r) -> p c r", c=n), in_=flat(w, s).rearrange("(c p r) -> p c r", c=n, p=128))
             return raw
 
         um_raw = load_main(up_w, "um_raw")
         bm_raw = cons.tile([128, 2, 32], BF16, name="bm_raw")
         for k, v in ((0, b_exp), (1, up_bias)):
             nc.sync.dma_start(out=bm_raw[:, k, :].rearrange("p (c t) -> p c t", t=4), in_=v.rearrange("(c p t) -> p c t", p=128, t=4))
-        wbs[1] = load_wexp(1)
-        r1_raw = cons.tile([128, 5, 64], BF16, name="r1_raw")
-        nc.sync.dma_start(out=r1_raw[:], in_=up_w[0:5].rearrange("s k o i -> s (k o i)").rearrange("s (q r) -> q s r", r=64))
-        b2_raw = cons.tile([128, 32], BF16, name="b2_raw")
-        nc.sync.dma_start(out=b2_raw[:], in_=b_exp.rearrange("(q l) -> q l", l=32))
-        wbs[2] = load_wexp(2)
+        load_wexp(1)
 
         def load_factors(w):
             ft = cons.tile([128, 16 * 127 * 8], BF16, tag="fh", name="ft")
@@ -111,7 +105,7 @@ def tile_butterflymlp_kernel(tc, x, w_bytes, w_scale, b_exp, up_w, up_bias, down
                 fj = ft[:, off : off + 8 * run].rearrange("p (c e) -> p c e", c=8)
                 off += 8 * run
                 views.append(fj)
-                src = w[2 + j].rearrange("k o i -> (k o i)").rearrange("(c h e) -> h c e", c=8, e=run)
+                src = flat(w, 2 + j).rearrange("(c h e) -> h c e", c=8, e=run)
                 n_lo, n_hi = 1 << j, 1 << (6 - j)
                 for i in range(2):
                     if n_lo <= n_hi:
@@ -123,7 +117,12 @@ def tile_butterflymlp_kernel(tc, x, w_bytes, w_scale, b_exp, up_w, up_bias, down
                             nc.sync.dma_start(out=fj[p0 : p0 + n_lo, :, 0 : run - 1], in_=src[h][:, i : i + run - 1].partition_broadcast(n_lo))
             return views
 
+        load_wexp(2)
         f_up = load_factors(up_w)
+        r1_raw = cons.tile([128, 5, 64], BF16, name="r1_raw")
+        nc.sync.dma_start(out=r1_raw[:], in_=up_w[0:5].rearrange("s k o i -> s (k o i)").rearrange("s (q r) -> q s r", r=64))
+        b2_raw = cons.tile([128, 32], BF16, name="b2_raw")
+        nc.sync.dma_start(out=b2_raw[:], in_=b_exp.rearrange("(q l) -> q l", l=32))
 
         def tt(eng, o, a, b, op):
             eng.tensor_tensor(out=o, in0=a, in1=b, op=op)
@@ -131,23 +130,17 @@ def tile_butterflymlp_kernel(tc, x, w_bytes, w_scale, b_exp, up_w, up_bias, down
         def half(a, bit, o):
             return a.rearrange("p (h o l) -> p h o l", o=2, l=1 << bit)[:, :, o, :]
 
-        def coefficients(raws, name):
-            n = sum(m for raw, m in raws)
+        def coefficients(raw, n, name):
             wd = cons.tile([128, n, 32], F32, name=name + "_wd")
             wo = cons.tile([128, n, 32], F32, name=name + "_wo")
-            k0 = 0
-            for raw, m in raws:
-                for k in range(m):
-                    lo = 1 << k
-                    src = raw[:, k, :].rearrange("p (h l q) -> p h l q", l=lo, q=4)
-                    nc.gpsimd.tensor_copy(out=wd[:, k0 + k, :].rearrange("p (h o l) -> p h l o", o=2, l=lo), in_=src[:, :, :, 0:4:3])
-                    nc.gpsimd.tensor_copy(out=wo[:, k0 + k, :].rearrange("p (h o l) -> p h l o", o=2, l=lo), in_=src[:, :, :, 1:3])
-                k0 += m
+            for k in range(n):
+                lo = 1 << k
+                src = raw[:, k, :].rearrange("p (h l q) -> p h l q", l=lo, q=4)
+                nc.gpsimd.tensor_copy(out=wd[:, k, :].rearrange("p (h o l) -> p h l o", o=2, l=lo), in_=src[:, :, :, 0:4:3])
+                nc.gpsimd.tensor_copy(out=wo[:, k, :].rearrange("p (h o l) -> p h l o", o=2, l=lo), in_=src[:, :, :, 1:3])
             d = wd[:].rearrange("p k b -> p (k b)")
             o = wo[:].rearrange("p k b -> p (k b)")
-            ta = work.tile([128, 1024], F32, tag="pmat", name="ta", bufs=4)[:, 0 : 32 * n]
-            tb = work.tile([128, 1024], F32, tag="pmat", name="tb", bufs=4)[:, 0 : 32 * n]
-            tk = work.tile([128, 1024], F32, tag="pmat", name="tk", bufs=4)[:, 0 : 32 * n]
+            ta, tb, tk = [right(NFULL - 1 - e)[:, 0 : 32 * n] for e in range(3)]
             den = cons.tile([128, n, 32], F32, name=name + "_den")
             inv = cons.tile([128, n, 32], F32, name=name + "_inv")
             rr = cons.tile([128, n, 32], F32, name=name + "_rr")
@@ -156,20 +149,18 @@ def tile_butterflymlp_kernel(tc, x, w_bytes, w_scale, b_exp, up_w, up_bias, down
             v, g = nc.vector, nc.gpsimd
             v.scalar_tensor_tensor(out=tb, in0=o, scalar=-1.0, in1=o, op0=ALU.mult, op1=ALU.max)
             v.scalar_tensor_tensor(out=ta, in0=d, scalar=-1.0, in1=d, op0=ALU.mult, op1=ALU.max)
-            g.tensor_scalar(out=tb, in0=tb, scalar1=2.0**-20, scalar2=2.0**-40, op0=ALU.mult, op1=ALU.max)
+            v.tensor_scalar(out=tb, in0=tb, scalar1=2.0**-20, scalar2=2.0**-40, op0=ALU.mult, op1=ALU.max)
             tt(v, tk, ta, tb, ALU.is_ge)
             tt(g, ta, tk, d, ALU.mult)
             g.tensor_scalar(out=tk, in0=tk, scalar1=-1.0, scalar2=1.0, op0=ALU.mult, op1=ALU.add)
             tt(g, tb, tk, tb, ALU.mult)
             tt(g, dn, ta, tb, ALU.add)
-            v.reciprocal(out=iv, in_=dn)
-            tt(g, rr[:].rearrange("p k b -> p (k b)"), o, iv, ALU.mult)
-            res = []
-            k0 = 0
-            for raw, m in raws:
-                res.append(dict([(key, t[:, k0 : k0 + m, :]) for key, t in (("wd", wd), ("wo", wo), ("den", den), ("inv", inv), ("rr", rr))]))
-                k0 += m
-            return res
+
+            def finish():
+                v.reciprocal(out=iv, in_=dn)
+                tt(g, rr[:].rearrange("p k b -> p (k b)"), o, iv, ALU.mult)
+
+            return dict(wd=wd, wo=wo, den=den, inv=inv, rr=rr), finish
 
         def partner_mul(o, a, b, bit):
             for i in range(2):
@@ -187,10 +178,12 @@ def tile_butterflymlp_kernel(tc, x, w_bytes, w_scale, b_exp, up_w, up_bias, down
                 tt(nc.gpsimd, r, r, ial, ALU.mult)
                 a2 = small("%s_a%d" % (name, k))
                 tt(nc.gpsimd, a2, al, cf["den"][:, k, :], ALU.mult)
-                i2 = small("%s_i%d" % (name, k))
-                tt(nc.gpsimd, i2, ial, cf["inv"][:, k, :], ALU.mult)
                 rs.append(r)
-                al, ial = a2, i2
+                if k != ks[-1]:
+                    i2 = small("%s_i%d" % (name, k))
+                    tt(nc.gpsimd, i2, ial, cf["inv"][:, k, :], ALU.mult)
+                    ial = i2
+                al = a2
             return rs, al
 
         def closing(cf, k, al, name):
@@ -208,55 +201,26 @@ def tile_butterflymlp_kernel(tc, x, w_bytes, w_scale, b_exp, up_w, up_bias, down
             tt(nc.gpsimd, c0, c0, t0, ALU.add)
             return c0
 
-        um = coefficients([(um_raw, 5)], "um")[0]
-        bm = cons.tile([128, 2, 32], F32, name="bm")
-        nc.gpsimd.tensor_copy(out=bm[:], in_=bm_raw[:])
-        c_main = first_bias(um, bm[:, 0, :], "um")
-        um_r, um_al = chain(um, (2, 3, 4), "um")
-        upb = bm[:, 1, :]
+        def products(f, al, k):
+            steps = []
+            cur = {}
 
-        xc = cons.tile([128, 2, TOK], U32, name="xc", align_bytes=64)
-        xs = cons.tile([128, 2, TOK], U8, name="xs", align_bytes=64)
-        xc2 = cons.tile([128, 2, 128], U32, name="xc2", align_bytes=64)
-        xs2 = cons.tile([128, 2, 128], U8, name="xs2", align_bytes=64)
-        for g in range(2):
-            xg = work.tile([128, TOK * 4], BF16, tag="inter", name="xg", bufs=3, align_bytes=64)
-            for h in range(2):
-                ps = bank(0)
-                words = xraw[h][:].rearrange("p i d -> p (i d)").bitcast(F32)
-                for i in range(2):
-                    for u in range(2):
-                        w0 = 512 * i + 256 * g
-                        nc.tensor.transpose(ps[:, 256 * i + 128 * u : 256 * i + 128 * u + 128], words[:, w0 + u : w0 + 256 : 2], ident[:])
-                nc.vector.tensor_copy(out=xg[:].bitcast(F32)[:, 512 * h : 512 * h + 512].rearrange("p (i r u) -> p i r u", i=2, u=2),
-                                      in_=ps[:].rearrange("p (i u r) -> p i r u", i=2, u=2))
-            nc.vector.quantize_mx(out=xc[:, g, :].bitcast(FP8X4), scales=xs[:, g, :], in_=xg[:])
-            nc.vector.quantize_mx(out=xc2[:, g, :].bitcast(FP8X4), scales=xs2[:, g, :], in_=xg[:, 4 * N1 : 4 * N1 + 512])
+            def step(j):
+                n = 4 << j
+                if j < 6:
+                    cur[j] = tmp.tile([128, 2, 2 * n], F32, tag="p%d" % j, name="pj")
+                else:
+                    cur[j] = work.tile([128, 2, 2 * n], F32, tag="pmat", name="pmat", bufs=4)
+                for o in range(2):
+                    other = al[:, 8 * k : 8 * k + 8].rearrange("p (c t) -> p c t", t=4) if j == 0 else cur[j - 1][:]
+                    tt(nc.vector, cur[j][:, :, o * n : o * n + n], other, f[j][:, 2 * k : 2 * k + 2, 2 * o :: 4], ALU.mult)
 
-        zt = [cons.tile([128, H], F32, tag="zc", name="zt%d" % k, bufs=2, align_bytes=64) for k in range(2)]
+            for j in range(7):
+                steps.append(lambda j=j: step(j))
+            return steps, cur
 
-        def products(f, al):
-            def make(k):
-                prev = None
-                for j in range(7):
-                    n = 4 << j
-                    if j < 6:
-                        cur = tmp.tile([128, 2, 2 * n], F32, tag="p%d" % j, name="pj")
-                    else:
-                        cur = work.tile([128, 2, 2 * n], F32, tag="pmat", name="pmat", bufs=4)
-                    for o in range(2):
-                        src = f[j][:, 2 * k : 2 * k + 2, 2 * o :: 4]
-                        if j == 0:
-                            other = al[:, 8 * k : 8 * k + 8].rearrange("p (c t) -> p c t", t=4)
-                        else:
-                            other = prev[:]
-                        tt(nc.vector, cur[:, :, o * n : o * n + n], other, src, ALU.mult)
-                    prev = cur
-                return prev
-            return make
-
-        def pe_block(pm, b, y, dst):
-            nc.tensor.matmul(dst, pm[b // 8][:, (b // 4) % 2, b % 4 :: 4], y, start=True, stop=True)
+        def block_matrix(cur, b):
+            return cur[6][:, (b // 4) % 2, b % 4 :: 4]
 
         def norm_group(y, group, r, view, new, done):
             fresh = {}
@@ -268,10 +232,6 @@ def tile_butterflymlp_kernel(tc, x, w_bytes, w_scale, b_exp, up_w, up_bias, down
                 done(y[lo])
                 y[lo] = fresh[lo]
 
-        def norm_stage(y, todo, r, view, new, done):
-            for k in range(0, len(todo), GROUP):
-                norm_group(y, todo[k : k + GROUP], r, view, new, done)
-
         def norm_psum(y, group, ps, r, view, new):
             for lo, hi in group:
                 y[hi] = new(hi)
@@ -279,27 +239,29 @@ def tile_butterflymlp_kernel(tc, x, w_bytes, w_scale, b_exp, up_w, up_bias, down
             for lo, hi in group:
                 stt(view(y[lo]), ps[hi], r[:, lo : lo + 1], view(y[lo]))
 
-        def first_stage(y, ps, cf, c0, b, view, new):
+        def first_scaled(y, ps, cf, c0, b, view, new):
             for k in b:
                 y[k] = new(k)
                 scaled(view(y[k]), ps[k], cf["wd"][:, 0, k : k + 1], c0[:, k : k + 1])
+
+        def first_sum(y, ps, cf, b, view):
             for k in b:
                 stt(view(y[k]), ps[k ^ 1], cf["wo"][:, 0, k : k + 1], view(y[k]))
 
-        def close_pair(y, b, ss, so, view, new, done, dst=None):
+        def close_scaled(y, b, ss, view, new):
             ts = {}
             for k in b:
                 ts[k] = new(k)
                 scaled(view(ts[k]), view(y[k]), ss[:, k : k + 1])
+            return ts
+
+        def close_sum(y, b, ts, so, view, dst):
             for k in b:
                 other = b[0] + b[1] - k
-                stt(view(ts[k]) if dst is None else dst[k], view(y[other]), so[:, k : k + 1], view(ts[k]))
-            for k in b:
-                done(y[k])
-                if dst is None:
-                    y[k] = ts[k]
-                else:
-                    done(ts[k])
+                stt(dst[k], view(y[other]), so[:, k : k + 1], view(ts[k]))
+
+        def groups(todo, n=2):
+            return [todo[k : k + n] for k in range(0, len(todo), n)]
 
         lfree = list(range(NFULL))
         rfree = list(range(NFULL + NEXTRA))
@@ -323,183 +285,195 @@ def tile_butterflymlp_kernel(tc, x, w_bytes, w_scale, b_exp, up_w, up_bias, down
         def keep(a):
             return None
 
-        p_up = products(f_up, um["den"][:, 1, :])
-        pm_up = {}
-        y1 = {}
-        for c in range(8):
-            if c not in wbs:
-                wbs[c] = load_wexp(c)
-            wb = wbs[c]
-            wc = work.tile([128, 2, 512], U32, tag="wc", name="wc", bufs=2, align_bytes=64)
-            ws = work.tile([128, 2, 512], U8, tag="ws", name="ws", bufs=2, align_bytes=64)
+        xc = cons.tile([128, 2, TOK], U32, name="xc", align_bytes=64)
+        xs = cons.tile([128, 2, TOK], U8, name="xs", align_bytes=64)
+        xc2 = cons.tile([128, 2, 128], U32, name="xc2", align_bytes=64)
+        xs2 = cons.tile([128, 2, 128], U8, name="xs2", align_bytes=64)
+        wd_t, wi_t, wc_t, ws_t = {}, {}, {}, {}
+
+        def widen(c, g):
+            wd_t[c, g] = work.tile([128, 4, 512], BF16, tag="wide", name="wd", bufs=3, align_bytes=64)
+            for j in range(4):
+                nc.scalar.activation(out=wd_t[c, g][:, j, :], in_=wbs[c][:, g, j, :].bitcast(FP8), func=ACT.Copy, scale=wsc[:, g, j : j + 1])
+            wi_t[c, g] = work.tile([128, 2048], BF16, tag="inter", name="wi", bufs=3, align_bytes=64)
+
+        def weave(c, g, cp, ts):
+            for t in ts:
+                cp(out=wi_t[c, g][:, 512 * t : 512 * t + 512].rearrange("p (m j) -> p m j", j=4),
+                   in_=wd_t[c, g][:].rearrange("p j (m t) -> p t m j", t=4)[:, t])
+
+        def quant(c, g):
+            if g == 0:
+                wc_t[c] = work.tile([128, 2, 512], U32, tag="wc", name="wc", bufs=2, align_bytes=64)
+                ws_t[c] = work.tile([128, 2, 512], U8, tag="ws", name="ws", bufs=2, align_bytes=64)
+            nc.vector.quantize_mx(out=wc_t[c][:, g, :].bitcast(FP8X4), scales=ws_t[c][:, g, :], in_=wi_t[c, g][:])
+
+        widen(0, 0)
+        for g in range(2):
+            xg = work.tile([128, TOK * 4], BF16, tag="inter", name="xg", bufs=3, align_bytes=64)
+            for h in range(2):
+                ps = bank()
+                words = xraw[h][:].rearrange("p i d -> p (i d)").bitcast(F32)
+                for i in range(2):
+                    for u in range(2):
+                        w0 = 512 * i + 256 * g
+                        nc.tensor.transpose(ps[:, 256 * i + 128 * u : 256 * i + 128 * u + 128], words[:, w0 + u : w0 + 256 : 2], ident[:])
+                nc.vector.tensor_copy(out=xg[:].bitcast(F32)[:, 512 * h : 512 * h + 512].rearrange("p (i r u) -> p i r u", i=2, u=2),
+                                      in_=ps[:].rearrange("p (i u r) -> p i r u", i=2, u=2))
+            nc.vector.quantize_mx(out=xc[:, g, :].bitcast(FP8X4), scales=xs[:, g, :], in_=xg[:])
+            nc.vector.quantize_mx(out=xc2[:, g, :].bitcast(FP8X4), scales=xs2[:, g, :], in_=xg[:, 4 * N1 : 4 * N1 + 512])
+            if g == 0:
+                weave(0, 0, nc.vector.tensor_copy, range(4))
+        quant(0, 0)
+        um, um_finish = coefficients(um_raw, 5, "um")
+        widen(0, 1)
+        weave(0, 1, nc.vector.tensor_copy, range(2))
+        weave(0, 1, nc.scalar.copy, range(2, 4))
+        um_finish()
+        bm = cons.tile([128, 2, 32], F32, name="bm")
+        nc.gpsimd.tensor_copy(out=bm[:], in_=bm_raw[:])
+        c_main = first_bias(um, bm[:, 0, :], "um")
+        um_r, um_al = chain(um, (2, 3, 4), "um")
+        upb = bm[:, 1, :]
+        quant(0, 1)
+
+        zt = [cons.tile([128, H], F32, tag="zc", name="zt%d" % k, bufs=2, align_bytes=64) for k in range(2)]
+
+        def first_product(c, t):
+            ps = bank()
             for g in range(2):
-                wd = work.tile([128, 4, 512], BF16, tag="wide", name="wd", bufs=3, align_bytes=64)
-                for j in range(4):
-                    nc.scalar.activation(out=wd[:, j, :], in_=wb[:, g, j, :].bitcast(FP8), func=ACT.Copy, scale=wsc[:, g, j : j + 1])
-                wi = work.tile([128, 2048], BF16, tag="inter", name="wi", bufs=3, align_bytes=64)
-                cp = nc.vector.tensor_copy if g == 0 else nc.scalar.copy
-                for t in range(4):
-                    cp(out=wi[:, 512 * t : 512 * t + 512].rearrange("p (m j) -> p m j", j=4),
-                       in_=wd[:].rearrange("p j (m t) -> p t m j", t=4)[:, t])
-                nc.vector.quantize_mx(out=wc[:, g, :].bitcast(FP8X4), scales=ws[:, g, :], in_=wi[:])
-            if c % 2 == 0:
-                pm_up[c // 2] = p_up(c // 2)
-            for t0 in (0, 2):
-                pss = {}
-                for t in (t0, t0 + 1):
-                    ps = bank(0)
-                    for g in range(2):
-                        nc.tensor.matmul_mx(out=ps[:], lhsT=wc[:, g, 128 * t : 128 * t + 128].bitcast(FP8X4), lhsT_scale=ws[:, g, 128 * t : 128 * t + 128],
-                                            rhs=xc[:, g, :].bitcast(FP8X4), rhs_scale=xs[:, g, :], start=g == 0, stop=g == 1)
-                    pss[4 * c + t] = ps[:, 0:N1]
-                first_stage(y1, pss, um, c_main, (4 * c + t0, 4 * c + t0 + 1), left, lnew)
-            for k, tok, loc in CHUNKS:
-                ps = bank(0)
-                for g in range(2):
-                    lc = xc2[:, g, :] if k == 0 else xc[:, g, tok : tok + 128]
-                    ls = xs2[:, g, :] if k == 0 else xs[:, g, tok : tok + 128]
-                    nc.tensor.matmul_mx(out=ps[:], lhsT=lc.bitcast(FP8X4), lhsT_scale=ls, rhs=wc[:, g, :].bitcast(FP8X4), rhs_scale=ws[:, g, :],
-                                        start=g == 0, stop=g == 1)
-                nc.scalar.copy(out=zt[k][:].rearrange("p (t l c h) -> p c t l h", t=4, l=8, c=8)[:, c], in_=ps[:].rearrange("p (t h l) -> p t l h", t=4, l=8))
-            norm_group(y1, [(4 * c + t, 4 * c + t + 2) for t in (0, 1)], um["rr"][:, 1, :], left, lnew, lfree.append)
-            for t0 in (0, 2):
-                pss = {}
-                for t in (t0, t0 + 1):
-                    b = 4 * c + t
-                    ps = bank(0)
-                    pe_block(pm_up, b, left(y1[b]), ps[:, 0:N1])
-                    lfree.append(y1[b])
-                    pss[b] = ps[:, 0:N1]
-                    if c % 2 == 0:
-                        y1[b] = logged("lo")(b)
-                        nc.scalar.copy(out=left(y1[b]), in_=ps[:, 0:N1])
-                if c % 2 == 1:
-                    norm_psum(y1, [(b - 4, b) for b in (4 * c + t0, 4 * c + t0 + 1)], pss, um_r[0], left, logged("hi"))
-            if c % 4 == 3:
-                norm_stage(y1, [p for p in pairs(3) if p[0] // 16 == c // 4], um_r[1], left, logged("s10"), lfree.append)
+                nc.tensor.matmul_mx(out=ps[:], lhsT=wc_t[c][:, g, 128 * t : 128 * t + 128].bitcast(FP8X4), lhsT_scale=ws_t[c][:, g, 128 * t : 128 * t + 128],
+                                    rhs=xc[:, g, :].bitcast(FP8X4), rhs_scale=xs[:, g, :], start=g == 0, stop=g == 1)
+            return ps[:, 0:N1]
 
-        r2_raw = cons.tile([128, 4, 64], BF16, name="r2_raw")
+        def token_product(c, k, tok):
+            ps = bank()
+            for g in range(2):
+                lc = xc2[:, g, :] if k == 0 else xc[:, g, tok : tok + 128]
+                ls = xs2[:, g, :] if k == 0 else xs[:, g, tok : tok + 128]
+                nc.tensor.matmul_mx(out=ps[:], lhsT=lc.bitcast(FP8X4), lhsT_scale=ls, rhs=wc_t[c][:, g, :].bitcast(FP8X4), rhs_scale=ws_t[c][:, g, :],
+                                    start=g == 0, stop=g == 1)
+            nc.scalar.copy(out=zt[k][:].rearrange("p (t l c h) -> p c t l h", t=4, l=8, c=8)[:, c], in_=ps[:].rearrange("p (t h l) -> p t l h", t=4, l=8))
+
+        y1 = {}
+        pm_up = {}
+        psu = {}
+        steps_up = []
         for k in range(4):
-            src = up_w[5 + k].rearrange("k o i -> (k o i)").rearrange("(h u l q) -> h l u q", h=4, u=16, l=32)
-            for h in range(4):
-                nc.sync.dma_start(out=r2_raw[h::4, k, :].rearrange("p (u q) -> p u q", q=4), in_=src[h])
-        dm_raw = load_main(down_w, "dm_raw")
-        r1, r2, dm = coefficients([(r1_raw, 5), (r2_raw, 4), (dm_raw, 5)], "cf")
-        b2 = cons.tile([128, 32], F32, name="b2")
-        nc.gpsimd.tensor_copy(out=b2[:], in_=b2_raw[:])
-        c_r1 = first_bias(r1, b2[:], "r1")
-        r1_r, r1_al = chain(r1, (1, 2, 3), "r1")
-        r1_ss, r1_so = closing(r1, 4, r1_al, "r1")
-        r2_r, r2_al = chain(r2, (0, 1, 2), "r2")
-        r2_ss, r2_so = closing(r2, 3, r2_al, "r2")
-        d01_r, d01_al = chain(dm, (0, 1), "d0")
-        d9_r, d9_al = chain(dm, (2, 3), "d9")
-        d_ss, d_so = closing(dm, 4, d9_al, "d11")
-        f_dn = load_factors(down_w)
+            steps, pm_up[k] = products(f_up, um["den"][:, 1, :], k)
+            steps_up += steps
 
-        def turn_back(place, b):
-            ps = bank(0)
-            for e in range(2):
-                for k, tok, loc in CHUNKS:
-                    z0 = 128 * place(b[e])
-                    nc.tensor.transpose(ps[:, 256 * e + loc : 256 * e + loc + 128], zt[k][:, z0 : z0 + 128], ident[:])
-            return {b[0]: ps[:, 0:N2], b[1]: ps[:, 256 : 256 + N2]}
+        def matrix_steps(n):
+            for k in range(min(n, len(steps_up))):
+                steps_up.pop(0)()
 
-        def turn_out(y, to, frm):
-            for b0 in range(0, 32, 4):
-                for k, tok, loc in CHUNKS:
-                    ps = bank(0)
-                    for e in range(4):
-                        nc.tensor.transpose(ps[:, 128 * e : 128 * e + 128], right(y[b0 + e])[:, loc : loc + 128], ident[:])
-                    nc.scalar.copy(out=to(zt[k], b0 // 4), in_=frm(ps))
-                for e in range(4):
-                    rfree.append(y[b0 + e])
+        def middle(c):
+            for t in range(4):
+                b = 4 * c + t
+                ps = bank()
+                nc.tensor.matmul(ps[:, 0:N1], block_matrix(pm_up[c // 2], b), left(y1[b]), start=True, stop=True)
+                lfree.append(y1[b])
+                psu[b] = ps[:, 0:N1]
+                if c % 2 == 0:
+                    y1[b] = logged("lo")(b)
+                    nc.scalar.copy(out=left(y1[b]), in_=psu[b])
 
-        y2 = {}
-        for b in pairs(0):
-            first_stage(y2, turn_back(lambda l: 8 * (l % 4) + l // 4, b), r1, c_r1, b, right, rnew)
-        for bit in (1, 2, 3):
-            norm_stage(y2, pairs(bit), r1_r[bit - 1], right, rnew, rfree.append)
-        for b in pairs(4):
-            close_pair(y2, b, r1_ss, r1_so, right, rnew, rfree.append)
-        turn_out(y2, lambda z, g: z[:].rearrange("p (v g l h) -> p g v l h", v=32, g=8, l=4)[:, g],
-                 lambda ps: ps[:].rearrange("p (l h v) -> p v l h", l=4, h=4))
-
-        d0_todo = pairs(0)
-        d1_todo = [p for t in (0, 1) for p in pairs(1) if p[0] % 4 == t]
-
-        def to_second(y, view, new, done):
-            norm_stage(y, pairs(4), um_r[2], view, new("s11"), done)
-            for b in range(32):
-                nc.scalar.activation(out=view(y[b]), in_=view(y[b]), func=ACT.Gelu, scale=um_al[:, b : b + 1], bias=upb[:, b : b + 1])
-            norm_stage(y, d0_todo, d01_r[0], view, new("d0"), done)
-            norm_stage(y, d1_todo, d01_r[1], view, new("d1"), done)
-
-        to_second(y1, left, logged, lfree.append)
-
-        y2 = {}
-        for k in range(0, 16, GROUP):
-            group = pairs(0)[k : k + GROUP]
-            his = {}
-            for b in group:
-                ps = turn_back(lambda v: v, b)
-                y2[b[0]] = rnew(b[0])
-                nc.scalar.copy(out=right(y2[b[0]]), in_=ps[b[0]])
-                his[b[1]] = ps[b[1]]
-            norm_psum(y2, group, his, r2_r[0], right, rnew)
-        for bit in (1, 2):
-            norm_stage(y2, pairs(bit), r2_r[bit], right, rnew, rfree.append)
-        for b in pairs(3):
-            close_pair(y2, b, r2_ss, r2_so, right, rnew, rfree.append)
-        turn_out(y2, lambda z, g: z[:].rearrange("p (e x g v l) -> p e g x v l", e=2, x=16, g=4, v=4)[:, g // 4, g % 4],
-                 lambda ps: ps[:].rearrange("p (v l x) -> p x v l", v=4, l=8))
-
-        p_dn = products(f_dn, d01_al)
-        pm_dn = {k: p_dn(k) for k in range(4)}
-
-        y2 = {}
-        for c in range(0, 8, 2):
+        def upper(c):
             for t0 in (0, 2):
-                todo = [(4 * c + t, 4 * c + 4 + t) for t in (t0, t0 + 1)]
-                his = {}
-                for b in todo:
-                    ps = turn_back(lambda k: 16 * (k // 4 % 2) + 4 * (k % 4) + k // 8, b)
-                    y2[b[0]] = placed["lo", b[0]]
-                    nc.scalar.copy(out=right(y2[b[0]]), in_=ps[b[0]])
-                    his[b[1]] = ps[b[1]]
-                norm_psum(y2, todo, his, um_r[0], right, replay("hi"))
-            if c % 4 == 2:
-                norm_stage(y2, [p for p in pairs(3) if p[0] // 16 == c // 4], um_r[1], right, replay("s10"), keep)
-        to_second(y2, right, replay, keep)
+                norm_psum(y1, [(4 * c - 4 + t, 4 * c + t) for t in (t0, t0 + 1)], psu, um_r[0], left, logged("hi"))
 
-        y = y1
-        for t in (0, 2, 1, 3):
-            todo = [(4 * c + t, 4 * c + 4 + t) for c in range(0, 8, 2)]
-            for k in range(0, 4, GROUP):
-                his = {}
-                for b in todo[k : k + GROUP]:
-                    for blk in b:
-                        ps = bank(0)
-                        pe_block(pm_dn, blk, full(y[blk]), ps[:])
-                        lfree.append(y[blk])
-                        if blk == b[0]:
-                            y[blk] = lnew(blk)
-                            nc.scalar.copy(out=full(y[blk]), in_=ps[:])
-                        else:
-                            his[blk] = ps[:]
-                norm_psum(y, todo[k : k + GROUP], his, d9_r[0], full, lnew)
-            norm_stage(y, [p for p in pairs(3) if p[0] % 4 == t], d9_r[1], full, lnew, lfree.append)
-
-        wcc = [cons.tile([128, 4, D], U32, tag="zc", name="wcc%d" % k, bufs=2, align_bytes=64) for k in range(2)]
-        wcs = cons.tile([128, 8, D], U8, name="wcs", align_bytes=64)
-        csrc = w_con.rearrange("(c p j) d -> c p j d", p=128, j=4)
+        widen(1, 0)
+        widen(1, 1)
         for c in range(8):
-            for dh in range(2):
-                wr = work.tile([128, 4, 512], BF16, tag="wide", name="wr", bufs=3, align_bytes=64)
-                nc.sync.dma_start(out=wr[:], in_=csrc[c][:, :, 512 * dh : 512 * dh + 512])
-                wi = work.tile([128, 2048], BF16, tag="inter", name="wi2", bufs=3, align_bytes=64)
-                nc.scalar.copy(out=wi[:].rearrange("p (d j) -> p d j", j=4), in_=wr[:].rearrange("p j d -> p d j"))
-                nc.vector.quantize_mx(out=wcc[c // 4][:, c % 4, 512 * dh : 512 * dh + 512].bitcast(FP8X4), scales=wcs[:, c, 512 * dh : 512 * dh + 512], in_=wi[:])
+            if c + 3 < 8:
+                load_wexp(c + 3)
+            pss = {4 * c + t: first_product(c, t) for t in range(4)}
+            for t0 in (0, 2):
+                first_scaled(y1, pss, um, c_main, (4 * c + t0, 4 * c + t0 + 1), left, lnew)
+            if c + 2 < 8:
+                widen(c + 2, 0)
+            if c + 1 < 8:
+                weave(c + 1, 0, nc.vector.tensor_copy, range(4))
+            matrix_steps(1)
+            first_sum(y1, pss, um, (4 * c, 4 * c + 1), left)
+            matrix_steps(1)
+            if c + 1 < 8:
+                quant(c + 1, 0)
+            first_sum(y1, pss, um, (4 * c + 2, 4 * c + 3), left)
+            for k, tok, loc in CHUNKS:
+                token_product(c, k, tok)
+            if c + 1 < 8:
+                weave(c + 1, 1, nc.vector.tensor_copy, range(3))
+                weave(c + 1, 1, nc.scalar.copy, range(3, 4))
+            matrix_steps(1)
+            norm_group(y1, [(4 * c + t, 4 * c + t + 2) for t in (0, 1)], um["rr"][:, 1, :], left, lnew, lfree.append)
+            if c == 0:
+                matrix_steps(4)
+            middle(c)
+            if c + 2 < 8:
+                widen(c + 2, 1)
+            if c + 1 < 8:
+                quant(c + 1, 1)
+            matrix_steps(1)
+            if c >= 2 and c % 2 == 0:
+                upper(c - 1)
+            if c == 2:
+                r1, r1_finish = coefficients(r1_raw, 5, "r1")
+                r2_raw = cons.tile([128, 4, 64], BF16, name="r2_raw")
+                for k in range(4):
+                    src = flat(up_w, 5 + k).rearrange("(h u l q) -> h l u q", h=4, u=16, l=32)
+                    for h in range(4):
+                        nc.sync.dma_start(out=r2_raw[h::4, k, :].rearrange("p (u q) -> p u q", q=4), in_=src[h])
+            if c == 3:
+                r1_finish()
+                b2 = cons.tile([128, 32], F32, name="b2")
+                nc.gpsimd.tensor_copy(out=b2[:], in_=b2_raw[:])
+                c_r1 = first_bias(r1, b2[:], "r1")
+                r1_r, r1_al = chain(r1, (1, 2, 3), "r1")
+                r1_ss, r1_so = closing(r1, 4, r1_al, "r1")
+                dm_raw = load_main(down_w, "dm_raw")
+            if c == 4:
+                r2, r2_finish = coefficients(r2_raw, 4, "r2")
+            if c == 5:
+                r2_finish()
+                r2_r, r2_al = chain(r2, (0, 1, 2), "r2")
+                r2_ss, r2_so = closing(r2, 3, r2_al, "r2")
+                dm, dm_finish = coefficients(dm_raw, 5, "dm")
+            if c == 6:
+                dm_finish()
+                d01_r, d01_al = chain(dm, (0, 1), "d0")
+                d9_r, d9_al = chain(dm, (2, 3), "d9")
+                d_ss, d_so = closing(dm, 4, d9_al, "d11")
+
+        fill = []
+
+        def filler(n):
+            for k in range(min(n, len(fill))):
+                fill.pop(0)()
+
+        def gelu(y, b, view):
+            nc.scalar.activation(out=view(y[b]), in_=view(y[b]), func=ACT.Gelu, scale=um_al[:, b : b + 1], bias=upb[:, b : b + 1])
+
+        def last_stage(y, grp, view, new, done):
+            norm_group(y, grp, um_r[2], view, new("s11"), done)
+            for p in grp:
+                for b in p:
+                    gelu(y, b, view)
+
+        def down_stage(y, grp, bit, view, new, done):
+            norm_group(y, grp, d01_r[bit], view, new("d%d" % bit), done)
+
+        def turnover(y, view, new, done):
+            steps = []
+            for kind, c in ((11, 0), (11, 1), (0, 0), (11, 2), (1, 0), (0, 1), (11, 3), (1, 1), (0, 2), (1, 2), (0, 3), (1, 3)):
+                if kind == 11:
+                    for grp in groups([(4 * c + t, 4 * c + 16 + t) for t in range(4)]):
+                        steps.append(lambda grp=grp: last_stage(y, grp, view, new, done))
+                else:
+                    for cc in (c, c + 4):
+                        grp = [(4 * cc + p[0], 4 * cc + p[1]) for p in pairs(kind)[0:2]]
+                        steps.append(lambda grp=grp, kind=kind: down_stage(y, grp, kind, view, new, done))
+            return steps
 
         bb = work.tile([128, D], F32, tag="wb", name="bb", bufs=3, align_bytes=64)
         braw = []
@@ -508,28 +482,286 @@ def tile_butterflymlp_kernel(tc, x, w_bytes, w_scale, b_exp, up_w, up_bias, down
             nc.sync.dma_start(out=br[:], in_=v.partition_broadcast(128))
             braw.append(br)
         tt(nc.gpsimd, bb[:], braw[0][:], braw[1][:], ALU.add)
+        f_dn = load_factors(down_w)
+
+        def turn_back(place, b):
+            ps = bank()
+            for e in range(2):
+                for k, tok, loc in CHUNKS:
+                    z0 = 128 * place(b[e])
+                    nc.tensor.transpose(ps[:, 256 * e + loc : 256 * e + loc + 128], zt[k][:, z0 : z0 + 128], ident[:])
+            return {b[0]: ps[:, 0:N2], b[1]: ps[:, 256 : 256 + N2]}
+
+        def turn_out(y, g, to, frm):
+            for k, tok, loc in CHUNKS:
+                ps = bank()
+                for e in range(4):
+                    nc.tensor.transpose(ps[:, 128 * e : 128 * e + 128], right(y[4 * g + e])[:, loc : loc + 128], ident[:])
+                nc.scalar.copy(out=to(zt[k], g), in_=frm(ps))
+            for e in range(4):
+                rfree.append(y[4 * g + e])
+
+        def turn_start(y, place, cf, c0, ahead, n_fill):
+            todo = pairs(0)
+            pss = {}
+
+            def begin(b):
+                pss.update(turn_back(place, b))
+                first_scaled(y, pss, cf, c0, b, right, rnew)
+
+            for b in todo[0:ahead]:
+                begin(b)
+            filler(n_fill)
+            for k, b in enumerate(todo):
+                first_sum(y, pss, cf, b, right)
+                if k + ahead < 16:
+                    begin(todo[k + ahead])
+
+        def close_turn(y, bit, ss, so, to, frm, n_fill):
+            todo = pairs(bit)
+            step = 1 << (bit - 2)
+            ts = {}
+            ts[0] = close_scaled(y, todo[0], ss, right, rnew)
+            ts[1] = close_scaled(y, todo[1], ss, right, rnew)
+            ready = []
+            for k, b in enumerate(todo):
+                if k + 2 < 16:
+                    ts[k + 2] = close_scaled(y, todo[k + 2], ss, right, rnew)
+                close_sum(y, b, ts[k], so, right, {q: right(ts[k][q]) for q in b})
+                for q in b:
+                    rfree.append(y[q])
+                    y[q] = ts[k][q]
+                if k % 4 == 3:
+                    ready += [b[0] // 4, b[1] // 4]
+                    filler(n_fill)
+                elif k % 4 in (0, 1) and ready:
+                    turn_out(y, ready.pop(0), to, frm)
+            for g in ready:
+                turn_out(y, g, to, frm)
+
+        upper(7)
+        y2 = {}
+        fill += [lambda grp=grp: norm_group(y1, grp, um_r[1], left, logged("s10"), lfree.append) for grp in groups(pairs(3))]
+        fill += turnover(y1, left, logged, lfree.append)
+        turn_start(y2, lambda l: 8 * (l % 4) + l // 4, r1, c_r1, 3, 3)
+        for bit in (1, 2, 3):
+            for n, grp in enumerate(groups(pairs(bit))):
+                norm_group(y2, grp, r1_r[bit - 1], right, rnew, rfree.append)
+                if n % 4 != 3:
+                    filler(1)
+        close_turn(y2, 4, r1_ss, r1_so, lambda z, g: z[:].rearrange("p (v g l h) -> p g v l h", v=32, g=8, l=4)[:, g],
+                   lambda ps: ps[:].rearrange("p (l h v) -> p v l h", l=4, h=4), 2)
+        y2 = {}
+        his = {}
+        todo = groups(pairs(0))
+
+        def r2_begin(grp):
+            for b in grp:
+                ps = turn_back(lambda v: v, b)
+                y2[b[0]] = rnew(b[0])
+                nc.scalar.copy(out=right(y2[b[0]]), in_=ps[b[0]])
+                his[b[1]] = ps[b[1]]
+
+        r2_begin(todo[0])
+        r2_begin(todo[1])
+        filler(2)
+        for n, grp in enumerate(todo):
+            norm_psum(y2, grp, his, r2_r[0], right, rnew)
+            if n + 2 < 8:
+                r2_begin(todo[n + 2])
+        for bit in (1, 2):
+            for grp in groups(pairs(bit)):
+                norm_group(y2, grp, r2_r[bit], right, rnew, rfree.append)
+        pm_dn = {}
+        for k in range(4):
+            steps, pm_dn[k] = products(f_dn, d01_al, k)
+            fill += steps
+        close_turn(y2, 3, r2_ss, r2_so, lambda z, g: z[:].rearrange("p (e x g v l) -> p e g x v l", e=2, x=16, g=4, v=4)[:, g // 4, g % 4],
+                   lambda ps: ps[:].rearrange("p (v l x) -> p x v l", v=4, l=8), 2)
+
+        y2 = {}
+        his = {}
+        todo = [[(4 * c + t, 4 * c + 4 + t) for t in (t0, t0 + 1)] for c in range(0, 8, 2) for t0 in (0, 2)]
+
+        def r3_begin(grp):
+            for b in grp:
+                ps = turn_back(lambda k: 16 * (k // 4 % 2) + 4 * (k % 4) + k // 8, b)
+                y2[b[0]] = placed["lo", b[0]]
+                nc.scalar.copy(out=right(y2[b[0]]), in_=ps[b[0]])
+                his[b[1]] = ps[b[1]]
+
+        r3_begin(todo[0])
+        r3_begin(todo[1])
+        filler(10)
+        for n, grp in enumerate(todo):
+            norm_psum(y2, grp, his, um_r[0], right, replay("hi"))
+            if n + 2 < 8:
+                r3_begin(todo[n + 2])
+
+        for grp in groups(pairs(3)):
+            norm_group(y2, grp, um_r[1], right, replay("s10"), keep)
+
+        wcc = [cons.tile([128, 4, D], U32, tag="zc", name="wcc%d" % k, bufs=2, align_bytes=64) for k in range(2)]
+        wcs = cons.tile([128, 8, D], U8, name="wcs", align_bytes=64)
+        csrc = w_con.rearrange("(c p j) d -> c p j d", p=128, j=4)
+        wr_t, wq_t = {}, {}
+
+        def con_load(n):
+            c, dh = n // 2, n % 2
+            wr_t[n] = work.tile([128, 4, 512], BF16, tag="wide", name="wr", bufs=3, align_bytes=64)
+            nc.sync.dma_start(out=wr_t[n][:], in_=csrc[c][:, :, 512 * dh : 512 * dh + 512])
+
+        def con_weave(n):
+            wq_t[n] = work.tile([128, 2048], BF16, tag="inter", name="wq", bufs=3, align_bytes=64)
+            nc.scalar.copy(out=wq_t[n][:].rearrange("p (d j) -> p d j", j=4), in_=wr_t[n][:].rearrange("p j d -> p d j"))
+
+        def con_quant(n):
+            c, dh = n // 2, n % 2
+            nc.vector.quantize_mx(out=wcc[c // 4][:, c % 4, 512 * dh : 512 * dh + 512].bitcast(FP8X4), scales=wcs[:, c, 512 * dh : 512 * dh + 512], in_=wq_t[n][:])
+
+        con = [0]
+
+        def con_step():
+            n = con[0]
+            if n == 0:
+                con_load(0)
+                con_load(1)
+            if n < 16:
+                if n + 2 < 16:
+                    con_load(n + 2)
+                con_weave(n)
+            if 1 <= n <= 16:
+                con_quant(n - 1)
+            con[0] = n + 1
+
+        y = y1
+        dfree = []
+
+        def dnew(k):
+            return dfree.pop(0)
+
+        his = {}
+
+        def down_middle(c):
+            for t in range(4):
+                b = 4 * c + t
+                ps = bank()
+                nc.tensor.matmul(ps[:], block_matrix(pm_dn[c // 2], b), full(y[b]), start=True, stop=True)
+                dfree.append(y[b])
+                if c % 2 == 0:
+                    y[b] = dnew(b)
+                    nc.scalar.copy(out=full(y[b]), in_=ps[:])
+                else:
+                    his[b] = ps[:]
+
+        def down_nine(c):
+            for t0 in (0, 2):
+                norm_psum(y, [(4 * c + t, 4 * c + 4 + t) for t in (t0, t0 + 1)], his, d9_r[0], full, dnew)
+
+        def down_ten(c):
+            for t0 in (0, 2):
+                norm_group(y, [(4 * c + t, 4 * c + 8 + t) for t in (t0, t0 + 1)], d9_r[1], full, dnew, dfree.append)
+
+        over = turnover(y2, right, replay, keep)
+
+        def over_steps(n):
+            for k in range(n):
+                over.pop(0)()
+
+        filler(len(fill))
+        over_steps(4)
+        con_step()
+        over_steps(4)
+        con_step()
+        over_steps(2)
+        down_middle(0)
+        con_step()
+        over_steps(2)
+        down_middle(4)
+        over_steps(4)
+        con_step()
+        down_middle(1)
+        over_steps(2)
+        down_nine(0)
+        down_middle(5)
+        con_step()
+        over_steps(2)
+        down_nine(4)
+        con_step()
+        down_middle(2)
+        over_steps(4)
+        con_step()
+        down_middle(6)
+        dfree.extend(lfree)
+        con_step()
+        down_middle(3)
+        con_step()
+        down_nine(2)
+        con_step()
+        down_middle(7)
+        down_ten(0)
+        con_step()
+        down_ten(1)
+        con_step()
+        down_nine(6)
+        con_step()
+        con_step()
+        down_ten(4)
+        con_step()
+        con_step()
+        down_ten(5)
+        con_step()
+        con_step()
 
         ht = cons.tile([128, 8, 4, TOK], BF16, tag="fh", name="ht")
-        for c in range(4):
-            for t in range(4):
-                b = (4 * c + t, 4 * c + 16 + t)
-                close_pair(y, b, d_ss, d_so, full, lnew, lfree.append, {b[0]: ht[:, c, t, :], b[1]: ht[:, c + 4, t, :]})
-        orows = out.rearrange("b s d -> (b s) d")
-        acc = [bank(0) for n in range(8)]
-        for n, c in enumerate((0, 4, 1, 5, 2, 6, 3, 7)):
-            hi = work.tile([128, 2048], BF16, tag="inter", name="hi", bufs=3, align_bytes=64)
-            cp = nc.scalar.copy if n % 2 == 0 else nc.vector.tensor_copy
-            cp(out=hi[:].rearrange("p (r t) -> p r t", t=4), in_=ht[:, c].rearrange("p t r -> p r t"))
-            hq = work.tile([128, 512], U32, tag="wc", name="hq", bufs=2, align_bytes=64)
-            hs = work.tile([128, 512], U8, tag="ws", name="hs", bufs=2, align_bytes=64)
-            nc.vector.quantize_mx(out=hq[:].bitcast(FP8X4), scales=hs[:], in_=hi[:])
+        acc = [bank() for n in range(8)]
+        hq_t, hs_t, hi_t = {}, {}, {}
+
+        def h_weave(c, cp):
+            hi_t[c] = work.tile([128, 2048], BF16, tag="inter", name="hi", bufs=3, align_bytes=64)
+            cp(out=hi_t[c][:].rearrange("p (r t) -> p r t", t=4), in_=ht[:, c].rearrange("p t r -> p r t"))
+
+        def h_quant(c):
+            hq_t[c] = work.tile([128, 512], U32, tag="wc", name="hq", bufs=2, align_bytes=64)
+            hs_t[c] = work.tile([128, 512], U8, tag="ws", name="hs", bufs=2, align_bytes=64)
+            nc.vector.quantize_mx(out=hq_t[c][:].bitcast(FP8X4), scales=hs_t[c][:], in_=hi_t[c][:])
+
+        def second_product(c, first, last):
             for k in range(8):
                 i, dh = k // 2, k % 2
-                nc.tensor.matmul_mx(out=acc[k][:], lhsT=hq[:, 128 * i : 128 * i + 128].bitcast(FP8X4), lhsT_scale=hs[:, 128 * i : 128 * i + 128],
+                nc.tensor.matmul_mx(out=acc[k][:], lhsT=hq_t[c][:, 128 * i : 128 * i + 128].bitcast(FP8X4), lhsT_scale=hs_t[c][:, 128 * i : 128 * i + 128],
                                     rhs=wcc[c // 4][:, c % 4, 512 * dh : 512 * dh + 512].bitcast(FP8X4), rhs_scale=wcs[:, c, 512 * dh : 512 * dh + 512],
-                                    start=n == 0, stop=n == 7)
+                                    start=first, stop=last)
+
+        todo = [(4 * c + t, 4 * c + 16 + t) for c in range(4) for t in range(4)]
+        ts = {0: close_scaled(y, todo[0], d_ss, full, dnew)}
+        for k, b in enumerate(todo):
+            c, t = k // 4, k % 4
+            if k + 1 < 16 and len(dfree) >= 2:
+                ts[k + 1] = close_scaled(y, todo[k + 1], d_ss, full, dnew)
+            close_sum(y, b, ts[k], d_so, full, {b[0]: ht[:, c, t, :], b[1]: ht[:, c + 4, t, :]})
+            for q in b:
+                dfree.append(y[q])
+                dfree.append(ts[k][q])
+            if k + 1 < 16 and k + 1 not in ts:
+                ts[k + 1] = close_scaled(y, todo[k + 1], d_ss, full, dnew)
+            if c > 0 and t == 0:
+                h_weave(c - 1, nc.scalar.copy)
+                h_weave(c + 3, nc.vector.tensor_copy)
+                h_quant(c + 3)
+                second_product(c + 3, c == 1, False)
+            if c > 0 and t == 2:
+                h_quant(c - 1)
+                second_product(c - 1, False, False)
+        h_weave(3, nc.scalar.copy)
+        h_weave(7, nc.vector.tensor_copy)
+        h_quant(7)
+        second_product(7, False, False)
+        h_quant(3)
+        second_product(3, False, True)
+        orows = out.rearrange("b s d -> (b s) d")
         for k in range(8):
             i, dh = k // 2, k % 2
-            ot = work.tile([128, 512], F32, tag="wb", name="ot", bufs=3, align_bytes=64)
+            ot = work.tile([128, 512], F32, tag="wide" if k % 2 else "inter", name="ot", bufs=3, align_bytes=64)
             tt(nc.vector, ot[:], acc[k][:], bb[:, 512 * dh : 512 * dh + 512], ALU.add)
             nc.sync.dma_start(out=orows[128 * i : 128 * i + 128, 512 * dh : 512 * dh + 512], in_=ot[:])

@@ -13,17 +13,20 @@ ALU = mybir.AluOpType
 ACT = mybir.ActivationFunctionType
 
 TOK, D, H = 512, 1024, 4096
+A_WIDEN = (3,)
+V_WEAVE = 5
+PLAN_1 = (2, (0, 1, 0, 1), (0, 1, 0, 0), 1)
+PLAN_2 = (4, (1, 1, 0, 1), (0, 1, 0, 1), 3)
+PLAN_3 = (6, 1)
 FLOPS = 2 * 2 * TOK * D * H + 2 * 12 * 3 * TOK * H
 
-N1 = 304
-N2 = TOK - N1
-NFULL = 35
-NEXTRA = 6
-CHUNKS = ((0, N1, 0), (1, 384, 384 - N1))
+
+def pairs(bit, n=32):
+    return [(b, b | (1 << bit)) for b in range(n) if not b & (1 << bit)]
 
 
-def pairs(bit):
-    return [(b, b | (1 << bit)) for b in range(32) if not b & (1 << bit)]
+def groups(todo, n=2):
+    return [todo[k : k + n] for k in range(0, len(todo), n)]
 
 
 def tile_butterflymlp_kernel(tc, x, w_bytes, w_scale, b_exp, up_w, up_bias, down_w, w_con, b_con, down_bias, out):
@@ -39,17 +42,8 @@ def tile_butterflymlp_kernel(tc, x, w_bytes, w_scale, b_exp, up_w, up_bias, down
             ps = psum.tile([128, 512], F32, tag="ps", name="ps")
             return ps
 
-        areas = [cons.tile([128, TOK], F32, name="ar%d" % k) for k in range(NFULL)]
-        areas += [cons.tile([128, N2], F32, name="ax%d" % k) for k in range(NEXTRA)]
-
-        def full(k):
-            return areas[k][:]
-
-        def left(k):
-            return areas[k][:, 0:N1]
-
-        def right(k):
-            return areas[k][:, N1:TOK] if k < NFULL else areas[k][:]
+        def ytile():
+            return work.tile([128, TOK], F32, tag="y", name="y", bufs=38)
 
         def stt(o, in0, s, in1):
             nc.vector.scalar_tensor_tensor(out=o, in0=in0, scalar=s, in1=in1, op0=ALU.mult, op1=ALU.add)
@@ -76,7 +70,7 @@ def tile_butterflymlp_kernel(tc, x, w_bytes, w_scale, b_exp, up_w, up_bias, down
         xrows = x.rearrange("b s d -> (b s) d").rearrange("(i p) d -> p i d", p=128)
         xraw = []
         for h in range(2):
-            xr = work.tile([128, 2, D], BF16, tag="wide", name="xr", bufs=3, align_bytes=64)
+            xr = work.tile([128, 2, D], BF16, tag="wide", name="xr", bufs=4, align_bytes=64)
             nc.sync.dma_start(out=xr[:], in_=xrows[:, 2 * h : 2 * h + 2, :])
             xraw.append(xr)
 
@@ -95,17 +89,28 @@ def tile_butterflymlp_kernel(tc, x, w_bytes, w_scale, b_exp, up_w, up_bias, down
         for k, v in ((0, b_exp), (1, up_bias)):
             nc.sync.dma_start(out=bm_raw[:, k, :].rearrange("p (c t) -> p c t", t=4), in_=v.rearrange("(c p t) -> p c t", p=128, t=4))
         load_wexp(1)
+        load_wexp(2)
 
-        def load_factors(w):
+        r_raw = cons.tile([128, 7, 32], BF16, name="r_raw")
+        for k in range(4):
+            src = flat(up_w, 2 + k).rearrange("(z h u t q) -> z t h u q", z=2, h=32, u=8, t=4)[0]
+            for t in range(4):
+                nc.sync.dma_start(out=r_raw[32 * t : 32 * t + 32, k, :].rearrange("p (u q) -> p u q", q=4), in_=src[t])
+        for k in range(4, 7):
+            src = flat(up_w, 2 + k).rearrange("(z e u l q) -> z e l u q", z=2, e=2, u=8, l=64)[0]
+            for e in range(2):
+                nc.sync.dma_start(out=r_raw[e::2, k, :].rearrange("p (u q) -> p u q", q=4), in_=src[e])
+
+        def load_factors(w, c0, n_c):
             ft = cons.tile([128, 16 * 127 * 8], BF16, tag="fh", name="ft")
             views = []
             off = 0
             for j in range(7):
                 run = 16 << j
-                fj = ft[:, off : off + 8 * run].rearrange("p (c e) -> p c e", c=8)
-                off += 8 * run
+                fj = ft[:, off : off + n_c * run].rearrange("p (c e) -> p c e", c=n_c)
+                off += n_c * run
                 views.append(fj)
-                src = flat(w, 2 + j).rearrange("(c h e) -> h c e", c=8, e=run)
+                src = flat(w, 2 + j).rearrange("(c h e) -> h c e", c=8, e=run)[:, c0 : c0 + n_c, :]
                 n_lo, n_hi = 1 << j, 1 << (6 - j)
                 for i in range(2):
                     if n_lo <= n_hi:
@@ -117,33 +122,28 @@ def tile_butterflymlp_kernel(tc, x, w_bytes, w_scale, b_exp, up_w, up_bias, down
                             nc.sync.dma_start(out=fj[p0 : p0 + n_lo, :, 0 : run - 1], in_=src[h][:, i : i + run - 1].partition_broadcast(n_lo))
             return views
 
-        load_wexp(2)
-        f_up = load_factors(up_w)
-        r1_raw = cons.tile([128, 5, 64], BF16, name="r1_raw")
-        nc.sync.dma_start(out=r1_raw[:], in_=up_w[0:5].rearrange("s k o i -> s (k o i)").rearrange("s (q r) -> q s r", r=64))
-        b2_raw = cons.tile([128, 32], BF16, name="b2_raw")
-        nc.sync.dma_start(out=b2_raw[:], in_=b_exp.rearrange("(q l) -> q l", l=32))
-
         def tt(eng, o, a, b, op):
             eng.tensor_tensor(out=o, in0=a, in1=b, op=op)
 
         def half(a, bit, o):
             return a.rearrange("p (h o l) -> p h o l", o=2, l=1 << bit)[:, :, o, :]
 
-        def coefficients(raw, n, name):
-            wd = cons.tile([128, n, 32], F32, name=name + "_wd")
-            wo = cons.tile([128, n, 32], F32, name=name + "_wo")
-            for k in range(n):
-                lo = 1 << k
+        def coefficients(raw, bits, nb, name):
+            n = len(bits)
+            w = nb * n
+            wd = cons.tile([128, n, nb], F32, name=name + "_wd")
+            wo = cons.tile([128, n, nb], F32, name=name + "_wo")
+            for k, bit in enumerate(bits):
+                lo = 1 << bit
                 src = raw[:, k, :].rearrange("p (h l q) -> p h l q", l=lo, q=4)
                 nc.gpsimd.tensor_copy(out=wd[:, k, :].rearrange("p (h o l) -> p h l o", o=2, l=lo), in_=src[:, :, :, 0:4:3])
                 nc.gpsimd.tensor_copy(out=wo[:, k, :].rearrange("p (h o l) -> p h l o", o=2, l=lo), in_=src[:, :, :, 1:3])
             d = wd[:].rearrange("p k b -> p (k b)")
             o = wo[:].rearrange("p k b -> p (k b)")
-            ta, tb, tk = [right(NFULL - 1 - e)[:, 0 : 32 * n] for e in range(3)]
-            den = cons.tile([128, n, 32], F32, name=name + "_den")
-            inv = cons.tile([128, n, 32], F32, name=name + "_inv")
-            rr = cons.tile([128, n, 32], F32, name=name + "_rr")
+            ta, tb, tk = [tmp.tile([128, 160], F32, tag="t%d" % e, name="tmp")[:, 0:w] for e in range(3)]
+            den = cons.tile([128, n, nb], F32, name=name + "_den")
+            inv = cons.tile([128, n, nb], F32, name=name + "_inv")
+            rr = cons.tile([128, n, nb], F32, name=name + "_rr")
             dn = den[:].rearrange("p k b -> p (k b)")
             iv = inv[:].rearrange("p k b -> p (k b)")
             v, g = nc.vector, nc.gpsimd
@@ -160,48 +160,40 @@ def tile_butterflymlp_kernel(tc, x, w_bytes, w_scale, b_exp, up_w, up_bias, down
                 v.reciprocal(out=iv, in_=dn)
                 tt(g, rr[:].rearrange("p k b -> p (k b)"), o, iv, ALU.mult)
 
-            return dict(wd=wd, wo=wo, den=den, inv=inv, rr=rr), finish
+            return dict(wd=wd, wo=wo, den=den, inv=inv, rr=rr, bits=bits, nb=nb), finish
 
         def partner_mul(o, a, b, bit):
             for i in range(2):
                 tt(nc.gpsimd, half(o, bit, i), half(a, bit, i), half(b, bit, 1 - i), ALU.mult)
 
-        def small(name):
-            return cons.tile([128, 32], F32, name=name)[:]
+        def small(cf, name):
+            return cons.tile([128, cf["nb"]], F32, name=name)[:]
 
         def chain(cf, ks, name):
             rs = [cf["rr"][:, ks[0], :]]
             al, ial = cf["den"][:, ks[0], :], cf["inv"][:, ks[0], :]
             for k in ks[1:]:
-                r = small("%s_r%d" % (name, k))
-                partner_mul(r, cf["rr"][:, k, :], al, k)
+                r = small(cf, "%s_r%d" % (name, k))
+                partner_mul(r, cf["rr"][:, k, :], al, cf["bits"][k])
                 tt(nc.gpsimd, r, r, ial, ALU.mult)
-                a2 = small("%s_a%d" % (name, k))
+                a2 = small(cf, "%s_a%d" % (name, k))
                 tt(nc.gpsimd, a2, al, cf["den"][:, k, :], ALU.mult)
-                rs.append(r)
                 if k != ks[-1]:
-                    i2 = small("%s_i%d" % (name, k))
+                    i2 = small(cf, "%s_i%d" % (name, k))
                     tt(nc.gpsimd, i2, ial, cf["inv"][:, k, :], ALU.mult)
                     ial = i2
+                rs.append(r)
                 al = a2
             return rs, al
 
         def closing(cf, k, al, name):
-            ss = small(name + "_ss")
-            so = small(name + "_so")
+            ss = small(cf, name + "_ss")
+            so = small(cf, name + "_so")
             tt(nc.gpsimd, ss, cf["wd"][:, k, :], al, ALU.mult)
-            partner_mul(so, cf["wo"][:, k, :], al, k)
+            partner_mul(so, cf["wo"][:, k, :], al, cf["bits"][k])
             return ss, so
 
-        def first_bias(cf, b, name):
-            c0 = small(name + "_c")
-            t0 = small(name + "_t")
-            tt(nc.gpsimd, t0, cf["wd"][:, 0, :], b, ALU.mult)
-            partner_mul(c0, cf["wo"][:, 0, :], b, 0)
-            tt(nc.gpsimd, c0, c0, t0, ALU.add)
-            return c0
-
-        def products(f, al, k):
+        def products(eng, f, al, k, c0):
             steps = []
             cur = {}
 
@@ -211,9 +203,9 @@ def tile_butterflymlp_kernel(tc, x, w_bytes, w_scale, b_exp, up_w, up_bias, down
                     cur[j] = tmp.tile([128, 2, 2 * n], F32, tag="p%d" % j, name="pj")
                 else:
                     cur[j] = work.tile([128, 2, 2 * n], F32, tag="pmat", name="pmat", bufs=4)
-                for o in range(2):
-                    other = al[:, 8 * k : 8 * k + 8].rearrange("p (c t) -> p c t", t=4) if j == 0 else cur[j - 1][:]
-                    tt(nc.vector, cur[j][:, :, o * n : o * n + n], other, f[j][:, 2 * k : 2 * k + 2, 2 * o :: 4], ALU.mult)
+                other = al[:, 8 * k : 8 * k + 8].rearrange("p (c t) -> p c t", t=4) if j == 0 else cur[j - 1][:]
+                tt(eng, cur[j][:].rearrange("p c (o n) -> p c o n", o=2), other.unsqueeze(2).to_broadcast([128, 2, 2, n]),
+                   f[j][:, 2 * k - c0 : 2 * k - c0 + 2, :].rearrange("p c (n o i) -> p c o n i", o=2, i=2)[:, :, :, :, 0], ALU.mult)
 
             for j in range(7):
                 steps.append(lambda j=j: step(j))
@@ -222,91 +214,63 @@ def tile_butterflymlp_kernel(tc, x, w_bytes, w_scale, b_exp, up_w, up_bias, down
         def block_matrix(cur, b):
             return cur[6][:, (b // 4) % 2, b % 4 :: 4]
 
-        def norm_group(y, group, r, view, new, done):
+        def norm_group(y, group, r):
             fresh = {}
             for lo, hi in group:
-                fresh[lo] = new(lo)
-                stt(view(fresh[lo]), view(y[hi]), r[:, lo : lo + 1], view(y[lo]))
+                fresh[lo] = ytile()
+                stt(fresh[lo][:], y[hi][:], r[:, lo : lo + 1], y[lo][:])
             for lo, hi in group:
-                stt(view(y[hi]), view(y[lo]), r[:, hi : hi + 1], view(y[hi]))
-                done(y[lo])
+                stt(y[hi][:], y[lo][:], r[:, hi : hi + 1], y[hi][:])
                 y[lo] = fresh[lo]
 
-        def norm_psum(y, group, ps, r, view, new):
+        def norm_psum(y, group, ps, r):
             for lo, hi in group:
-                y[hi] = new(hi)
-                stt(view(y[hi]), view(y[lo]), r[:, hi : hi + 1], ps[hi])
+                y[hi] = ytile()
+                stt(y[hi][:], y[lo][:], r[:, hi : hi + 1], ps[hi][:])
             for lo, hi in group:
-                stt(view(y[lo]), ps[hi], r[:, lo : lo + 1], view(y[lo]))
+                stt(y[lo][:], ps[hi][:], r[:, lo : lo + 1], y[lo][:])
 
-        def first_scaled(y, ps, cf, c0, b, view, new):
-            for k in b:
-                y[k] = new(k)
-                scaled(view(y[k]), ps[k], cf["wd"][:, 0, k : k + 1], c0[:, k : k + 1])
+        def low_copy(y, b, ps):
+            y[b] = ytile()
+            nc.scalar.copy(out=y[b][:], in_=ps[:])
 
-        def first_sum(y, ps, cf, b, view):
-            for k in b:
-                stt(view(y[k]), ps[k ^ 1], cf["wo"][:, 0, k : k + 1], view(y[k]))
-
-        def close_scaled(y, b, ss, view, new):
+        def close_scaled(y, b, ss):
             ts = {}
             for k in b:
-                ts[k] = new(k)
-                scaled(view(ts[k]), view(y[k]), ss[:, k : k + 1])
+                ts[k] = ytile()
+                scaled(ts[k][:], y[k][:], ss[:, k : k + 1])
             return ts
 
-        def close_sum(y, b, ts, so, view, dst):
+        def close_sum(y, b, ts, so, dst=None):
             for k in b:
                 other = b[0] + b[1] - k
-                stt(dst[k], view(y[other]), so[:, k : k + 1], view(ts[k]))
-
-        def groups(todo, n=2):
-            return [todo[k : k + n] for k in range(0, len(todo), n)]
-
-        lfree = list(range(NFULL))
-        rfree = list(range(NFULL + NEXTRA))
-        placed = {}
-
-        def lnew(k):
-            return lfree.pop(0)
-
-        def rnew(k):
-            return rfree.pop(0)
-
-        def logged(step):
-            def new(k):
-                placed[step, k] = lfree.pop(0)
-                return placed[step, k]
-            return new
-
-        def replay(step):
-            return lambda k: placed[step, k]
-
-        def keep(a):
-            return None
+                stt(ts[k][:] if dst is None else dst[k], y[other][:], so[:, k : k + 1], ts[k][:])
+            if dst is None:
+                y.update(ts)
 
         xc = cons.tile([128, 2, TOK], U32, name="xc", align_bytes=64)
         xs = cons.tile([128, 2, TOK], U8, name="xs", align_bytes=64)
-        xc2 = cons.tile([128, 2, 128], U32, name="xc2", align_bytes=64)
-        xs2 = cons.tile([128, 2, 128], U8, name="xs2", align_bytes=64)
         wd_t, wi_t, wc_t, ws_t = {}, {}, {}, {}
 
-        def widen(c, g):
-            wd_t[c, g] = work.tile([128, 4, 512], BF16, tag="wide", name="wd", bufs=3, align_bytes=64)
+        def widen(c, g, on_vector=()):
+            wd_t[c, g] = work.tile([128, 4, 512], BF16, tag="wide", name="wd", bufs=4, align_bytes=64)
             for j in range(4):
-                nc.scalar.activation(out=wd_t[c, g][:, j, :], in_=wbs[c][:, g, j, :].bitcast(FP8), func=ACT.Copy, scale=wsc[:, g, j : j + 1])
+                if j in on_vector:
+                    nc.vector.tensor_scalar(out=wd_t[c, g][:, j, :], in0=wbs[c][:, g, j, :].bitcast(FP8), scalar1=wsc[:, g, j : j + 1], scalar2=None, op0=ALU.mult)
+                else:
+                    nc.scalar.activation(out=wd_t[c, g][:, j, :], in_=wbs[c][:, g, j, :].bitcast(FP8), func=ACT.Copy, scale=wsc[:, g, j : j + 1])
             wi_t[c, g] = work.tile([128, 2048], BF16, tag="inter", name="wi", bufs=3, align_bytes=64)
 
-        def weave(c, g, cp, ts):
-            for t in ts:
-                cp(out=wi_t[c, g][:, 512 * t : 512 * t + 512].rearrange("p (m j) -> p m j", j=4),
-                   in_=wd_t[c, g][:].rearrange("p j (m t) -> p t m j", t=4)[:, t])
+        def weave(c, g, cp):
+            cp(out=wi_t[c, g][:].rearrange("p (t m j) -> p t m j", t=4, j=4), in_=wd_t[c, g][:].rearrange("p j (m t) -> p t m j", t=4))
 
         def quant(c, g):
             if g == 0:
                 wc_t[c] = work.tile([128, 2, 512], U32, tag="wc", name="wc", bufs=2, align_bytes=64)
                 ws_t[c] = work.tile([128, 2, 512], U8, tag="ws", name="ws", bufs=2, align_bytes=64)
             nc.vector.quantize_mx(out=wc_t[c][:, g, :].bitcast(FP8X4), scales=ws_t[c][:, g, :], in_=wi_t[c, g][:])
+
+        von, sca = nc.vector.tensor_copy, nc.scalar.copy
 
         widen(0, 0)
         for g in range(2):
@@ -321,294 +285,253 @@ def tile_butterflymlp_kernel(tc, x, w_bytes, w_scale, b_exp, up_w, up_bias, down
                 nc.vector.tensor_copy(out=xg[:].bitcast(F32)[:, 512 * h : 512 * h + 512].rearrange("p (i r u) -> p i r u", i=2, u=2),
                                       in_=ps[:].rearrange("p (i u r) -> p i r u", i=2, u=2))
             nc.vector.quantize_mx(out=xc[:, g, :].bitcast(FP8X4), scales=xs[:, g, :], in_=xg[:])
-            nc.vector.quantize_mx(out=xc2[:, g, :].bitcast(FP8X4), scales=xs2[:, g, :], in_=xg[:, 4 * N1 : 4 * N1 + 512])
             if g == 0:
-                weave(0, 0, nc.vector.tensor_copy, range(4))
+                weave(0, 0, von)
         quant(0, 0)
-        um, um_finish = coefficients(um_raw, 5, "um")
+        um, um_finish = coefficients(um_raw, (0, 1, 2, 3, 4), 32, "um")
         widen(0, 1)
-        weave(0, 1, nc.vector.tensor_copy, range(2))
-        weave(0, 1, nc.scalar.copy, range(2, 4))
+        weave(0, 1, von)
         um_finish()
         bm = cons.tile([128, 2, 32], F32, name="bm")
         nc.gpsimd.tensor_copy(out=bm[:], in_=bm_raw[:])
-        c_main = first_bias(um, bm[:, 0, :], "um")
-        um_r, um_al = chain(um, (2, 3, 4), "um")
+        c_main = small(um, "um_c")
+        t_main = small(um, "um_t")
+        tt(nc.gpsimd, t_main, um["wd"][:, 0, :], bm[:, 0, :], ALU.mult)
+        partner_mul(c_main, um["wo"][:, 0, :], bm[:, 0, :], 0)
+        tt(nc.gpsimd, c_main, c_main, t_main, ALU.add)
         upb = bm[:, 1, :]
         quant(0, 1)
 
-        zt = [cons.tile([128, H], F32, tag="zc", name="zt%d" % k, bufs=2, align_bytes=64) for k in range(2)]
+        zt = [cons.tile([128, 2048], F32, tag="zc%d" % (k // 2), name="zt%d" % k, bufs=2, align_bytes=64) for k in range(4)]
 
-        def first_product(c, t):
+        def first_product(y, c, ts):
+            pss = {}
+            for t in ts:
+                b = 4 * c + t
+                pss[b] = bank()
+                for g in range(2):
+                    nc.tensor.matmul_mx(out=pss[b][:], lhsT=wc_t[c][:, g, 128 * t : 128 * t + 128].bitcast(FP8X4), lhsT_scale=ws_t[c][:, g, 128 * t : 128 * t + 128],
+                                        rhs=xc[:, g, :].bitcast(FP8X4), rhs_scale=xs[:, g, :], start=g == 0, stop=g == 1)
+            for b in pss:
+                y[b] = ytile()
+                scaled(y[b][:], pss[b][:], um["wd"][:, 0, b : b + 1], c_main[:, b : b + 1])
+            return pss
+
+        def first_sum(y, pss):
+            for b in pss:
+                stt(y[b][:], pss[b ^ 1][:], um["wo"][:, 0, b : b + 1], y[b][:])
+
+        def turn_out(y, blocks, to, frm):
+            for k in range(4):
+                ps = bank()
+                for e, b in enumerate(blocks):
+                    nc.tensor.transpose(ps[:, 128 * e : 128 * e + 128], y[b][:, 128 * k : 128 * k + 128], ident[:])
+                nc.scalar.copy(out=to(zt[k]), in_=frm(ps))
+
+        def turn_back(place):
             ps = bank()
-            for g in range(2):
-                nc.tensor.matmul_mx(out=ps[:], lhsT=wc_t[c][:, g, 128 * t : 128 * t + 128].bitcast(FP8X4), lhsT_scale=ws_t[c][:, g, 128 * t : 128 * t + 128],
-                                    rhs=xc[:, g, :].bitcast(FP8X4), rhs_scale=xs[:, g, :], start=g == 0, stop=g == 1)
-            return ps[:, 0:N1]
+            for k in range(4):
+                nc.tensor.transpose(ps[:, 128 * k : 128 * k + 128], zt[k][:, 128 * place : 128 * place + 128], ident[:])
+            return ps
 
-        def token_product(c, k, tok):
-            ps = bank()
-            for g in range(2):
-                lc = xc2[:, g, :] if k == 0 else xc[:, g, tok : tok + 128]
-                ls = xs2[:, g, :] if k == 0 else xs[:, g, tok : tok + 128]
-                nc.tensor.matmul_mx(out=ps[:], lhsT=lc.bitcast(FP8X4), lhsT_scale=ls, rhs=wc_t[c][:, g, :].bitcast(FP8X4), rhs_scale=ws_t[c][:, g, :],
-                                    start=g == 0, stop=g == 1)
-            nc.scalar.copy(out=zt[k][:].rearrange("p (t l c h) -> p c t l h", t=4, l=8, c=8)[:, c], in_=ps[:].rearrange("p (t h l) -> p t l h", t=4, l=8))
+        y = {}
 
-        y1 = {}
+        def turn_first(c):
+            turn_out(y, range(4 * c, 4 * c + 4),
+                     lambda z: z[:].rearrange("p (v t c h) -> p c v t h", v=16, t=4, c=4)[:, c],
+                     lambda ps: ps[:].rearrange("p (t h v) -> p v t h", t=4, h=8))
+
         pm_up = {}
-        psu = {}
         steps_up = []
-        for k in range(4):
-            steps, pm_up[k] = products(f_up, um["den"][:, 1, :], k)
-            steps_up += steps
 
         def matrix_steps(n):
             for k in range(min(n, len(steps_up))):
                 steps_up.pop(0)()
 
-        def middle(c):
-            for t in range(4):
-                b = 4 * c + t
-                ps = bank()
-                nc.tensor.matmul(ps[:, 0:N1], block_matrix(pm_up[c // 2], b), left(y1[b]), start=True, stop=True)
-                lfree.append(y1[b])
-                psu[b] = ps[:, 0:N1]
-                if c % 2 == 0:
-                    y1[b] = logged("lo")(b)
-                    nc.scalar.copy(out=left(y1[b]), in_=psu[b])
-
-        def upper(c):
-            for t0 in (0, 2):
-                norm_psum(y1, [(4 * c - 4 + t, 4 * c + t) for t in (t0, t0 + 1)], psu, um_r[0], left, logged("hi"))
-
         widen(1, 0)
         widen(1, 1)
-        for c in range(8):
-            if c + 3 < 8:
-                load_wexp(c + 3)
-            pss = {4 * c + t: first_product(c, t) for t in range(4)}
-            for t0 in (0, 2):
-                first_scaled(y1, pss, um, c_main, (4 * c + t0, 4 * c + t0 + 1), left, lnew)
-            if c + 2 < 8:
-                widen(c + 2, 0)
-            if c + 1 < 8:
-                weave(c + 1, 0, nc.vector.tensor_copy, range(4))
-            matrix_steps(1)
-            first_sum(y1, pss, um, (4 * c, 4 * c + 1), left)
-            matrix_steps(1)
-            if c + 1 < 8:
-                quant(c + 1, 0)
-            first_sum(y1, pss, um, (4 * c + 2, 4 * c + 3), left)
-            for k, tok, loc in CHUNKS:
-                token_product(c, k, tok)
-            if c + 1 < 8:
-                weave(c + 1, 1, nc.vector.tensor_copy, range(3))
-                weave(c + 1, 1, nc.scalar.copy, range(3, 4))
-            matrix_steps(1)
-            norm_group(y1, [(4 * c + t, 4 * c + t + 2) for t in (0, 1)], um["rr"][:, 1, :], left, lnew, lfree.append)
+        for c in range(4):
+            load_wexp(c + 3)
+            p0 = first_product(y, c, (0, 1))
+            p1 = first_product(y, c, (2, 3))
+            weave(c + 1, 0, von)
+            if c >= 2:
+                matrix_steps(3)
+            first_sum(y, p0)
+            quant(c + 1, 0)
+            first_sum(y, p1)
+            ts = [(b, close_scaled(y, b, um["wd"][:, 1, :])) for b in ((4 * c, 4 * c + 2), (4 * c + 1, 4 * c + 3))]
+            widen(c + 2, 0, A_WIDEN)
+            weave(c + 1, 1, von)
+            for b, t in ts:
+                close_sum(y, b, t, um["wo"][:, 1, :])
+            if c >= 2:
+                matrix_steps(3)
+            quant(c + 1, 1)
+            turn_first(c)
+            widen(c + 2, 1, A_WIDEN)
             if c == 0:
-                matrix_steps(4)
-            middle(c)
-            if c + 2 < 8:
-                widen(c + 2, 1)
-            if c + 1 < 8:
-                quant(c + 1, 1)
-            matrix_steps(1)
-            if c >= 2 and c % 2 == 0:
-                upper(c - 1)
-            if c == 2:
-                r1, r1_finish = coefficients(r1_raw, 5, "r1")
-                r2_raw = cons.tile([128, 4, 64], BF16, name="r2_raw")
-                for k in range(4):
-                    src = flat(up_w, 5 + k).rearrange("(h u l q) -> h l u q", h=4, u=16, l=32)
-                    for h in range(4):
-                        nc.sync.dma_start(out=r2_raw[h::4, k, :].rearrange("p (u q) -> p u q", q=4), in_=src[h])
-            if c == 3:
+                f_up = load_factors(up_w, 4, 4)
+                for k in (2, 3):
+                    steps, pm_up[k] = products(nc.vector, f_up, um["den"][:, 1, :], k, 4)
+                    steps_up += steps
+                r1, r1_finish = coefficients(r_raw[:, 0:4, :], (0, 1, 2, 3), 16, "r1")
+            if c == 1:
                 r1_finish()
-                b2 = cons.tile([128, 32], F32, name="b2")
-                nc.gpsimd.tensor_copy(out=b2[:], in_=b2_raw[:])
-                c_r1 = first_bias(r1, b2[:], "r1")
-                r1_r, r1_al = chain(r1, (1, 2, 3), "r1")
-                r1_ss, r1_so = closing(r1, 4, r1_al, "r1")
+                r1_r, r1_al = chain(r1, (0, 1, 2), "r1")
+                r1_ss, r1_so = closing(r1, 3, r1_al, "r1")
                 dm_raw = load_main(down_w, "dm_raw")
-            if c == 4:
-                r2, r2_finish = coefficients(r2_raw, 4, "r2")
-            if c == 5:
+                r2, r2_finish = coefficients(r_raw[:, 4:7, :], (0, 1, 2), 16, "r2")
+            if c == 2:
                 r2_finish()
-                r2_r, r2_al = chain(r2, (0, 1, 2), "r2")
-                r2_ss, r2_so = closing(r2, 3, r2_al, "r2")
-                dm, dm_finish = coefficients(dm_raw, 5, "dm")
-            if c == 6:
+                r2_r, r2_al = chain(r2, (0, 1), "r2")
+                r2_ss, r2_so = closing(r2, 2, r2_al, "r2")
+                um_r, um_al = chain(um, (2, 3, 4), "um")
+                dm, dm_finish = coefficients(dm_raw, (0, 1, 2, 3, 4), 32, "dm")
+            if c == 3:
                 dm_finish()
                 d01_r, d01_al = chain(dm, (0, 1), "d0")
                 d9_r, d9_al = chain(dm, (2, 3), "d9")
                 d_ss, d_so = closing(dm, 4, d9_al, "d11")
 
         fill = []
+        psu = {}
+        held = {}
 
         def filler(n):
             for k in range(min(n, len(fill))):
                 fill.pop(0)()
 
-        def gelu(y, b, view):
-            nc.scalar.activation(out=view(y[b]), in_=view(y[b]), func=ACT.Gelu, scale=um_al[:, b : b + 1], bias=upb[:, b : b + 1])
+        def s_product(c, ts):
+            held[c, ts] = first_product(y, c, ts)
 
-        def last_stage(y, grp, view, new, done):
-            norm_group(y, grp, um_r[2], view, new("s11"), done)
-            for p in grp:
-                for b in p:
-                    gelu(y, b, view)
+        def s0(c):
+            s_product(c, (0, 1))
+            if c + 3 < 8:
+                load_wexp(c + 3)
+            if c + 2 < 8:
+                widen(c + 2, 0)
 
-        def down_stage(y, grp, bit, view, new, done):
-            norm_group(y, grp, d01_r[bit], view, new("d%d" % bit), done)
+        def s1(c):
+            first_sum(y, held[c, (0, 1)])
+            s_product(c, (2, 3))
+            if c + 1 < 8:
+                weave(c + 1, 0, von if c < V_WEAVE else sca)
 
-        def turnover(y, view, new, done):
-            steps = []
-            for kind, c in ((11, 0), (11, 1), (0, 0), (11, 2), (1, 0), (0, 1), (11, 3), (1, 1), (0, 2), (1, 2), (0, 3), (1, 3)):
-                if kind == 11:
-                    for grp in groups([(4 * c + t, 4 * c + 16 + t) for t in range(4)]):
-                        steps.append(lambda grp=grp: last_stage(y, grp, view, new, done))
-                else:
-                    for cc in (c, c + 4):
-                        grp = [(4 * cc + p[0], 4 * cc + p[1]) for p in pairs(kind)[0:2]]
-                        steps.append(lambda grp=grp, kind=kind: down_stage(y, grp, kind, view, new, done))
-            return steps
+        def s2(c):
+            first_sum(y, held[c, (2, 3)])
+            if c + 2 < 8:
+                widen(c + 2, 1)
+            if c + 1 < 8:
+                quant(c + 1, 0)
 
-        bb = work.tile([128, D], F32, tag="wb", name="bb", bufs=3, align_bytes=64)
-        braw = []
-        for v in (b_con, down_bias):
-            br = work.tile([128, D], BF16, tag="wb", name="br", bufs=3, align_bytes=64)
-            nc.sync.dma_start(out=br[:], in_=v.partition_broadcast(128))
-            braw.append(br)
-        tt(nc.gpsimd, bb[:], braw[0][:], braw[1][:], ALU.add)
-        f_dn = load_factors(down_w)
+        def s3(c):
+            norm_group(y, [(4 * c, 4 * c + 2), (4 * c + 1, 4 * c + 3)], um["rr"][:, 1, :])
+            if c + 1 < 8:
+                weave(c + 1, 1, von if c < V_WEAVE - 1 else sca)
+            if c == 4:
+                matrix_steps(len(steps_up))
 
-        def turn_back(place, b):
-            ps = bank()
-            for e in range(2):
-                for k, tok, loc in CHUNKS:
-                    z0 = 128 * place(b[e])
-                    nc.tensor.transpose(ps[:, 256 * e + loc : 256 * e + loc + 128], zt[k][:, z0 : z0 + 128], ident[:])
-            return {b[0]: ps[:, 0:N2], b[1]: ps[:, 256 : 256 + N2]}
+        def s4(c):
+            for t in range(4):
+                b = 4 * c + t
+                psu[b] = bank()
+                nc.tensor.matmul(psu[b][:], block_matrix(pm_up[c // 2], b), y[b][:], start=True, stop=True)
+                if c % 2 == 0:
+                    low_copy(y, b, psu[b])
+            if c + 1 < 8:
+                quant(c + 1, 1)
 
-        def turn_out(y, g, to, frm):
-            for k, tok, loc in CHUNKS:
-                ps = bank()
-                for e in range(4):
-                    nc.tensor.transpose(ps[:, 128 * e : 128 * e + 128], right(y[4 * g + e])[:, loc : loc + 128], ident[:])
-                nc.scalar.copy(out=to(zt[k], g), in_=frm(ps))
-            for e in range(4):
-                rfree.append(y[4 * g + e])
+        def s5(c, t0):
+            norm_psum(y, [(4 * c - 4 + t, 4 * c + t) for t in (t0, t0 + 1)], psu, um_r[0])
 
-        def turn_start(y, place, cf, c0, ahead, n_fill):
-            todo = pairs(0)
-            pss = {}
+        for c in range(4, 8):
+            fill += [lambda c=c: s0(c), lambda c=c: s1(c), lambda c=c: s2(c), lambda c=c: s3(c), lambda c=c: s4(c)]
+            if c % 2 == 1:
+                fill += [lambda c=c: s5(c, 0), lambda c=c: s5(c, 2)]
+        fill += [lambda grp=grp: norm_group(y, grp, um_r[1]) for grp in groups([p for p in pairs(3) if p[0] >= 16])]
 
-            def begin(b):
-                pss.update(turn_back(place, b))
-                first_scaled(y, pss, cf, c0, b, right, rnew)
+        def turned(z, coefs, place, bit, ss, so, to, frm, plan, beside):
+            todo = groups(pairs(0, 16))
+            his = {}
 
-            for b in todo[0:ahead]:
-                begin(b)
-            filler(n_fill)
-            for k, b in enumerate(todo):
-                first_sum(y, pss, cf, b, right)
-                if k + ahead < 16:
-                    begin(todo[k + ahead])
+            def begin(grp):
+                for lo, hi in grp:
+                    low_copy(z, lo, turn_back(place(lo)))
+                    his[hi] = turn_back(place(hi))
 
-        def close_turn(y, bit, ss, so, to, frm, n_fill):
-            todo = pairs(bit)
-            step = 1 << (bit - 2)
-            ts = {}
-            ts[0] = close_scaled(y, todo[0], ss, right, rnew)
-            ts[1] = close_scaled(y, todo[1], ss, right, rnew)
+            begin(todo[0])
+            filler(plan[0])
+            for n, grp in enumerate(todo):
+                norm_psum(z, grp, his, coefs[0])
+                if n == 0:
+                    beside(z[grp[0][1]])
+                if n + 1 < 4:
+                    begin(todo[n + 1])
+                filler(plan[1][n])
+            for k in range(1, bit):
+                for n, grp in enumerate(groups(pairs(k, 16))):
+                    norm_group(z, grp, coefs[k])
+                    filler(plan[2][n])
+            todo = pairs(bit, 16)
+            ts = {0: close_scaled(z, todo[0], ss), 1: close_scaled(z, todo[1], ss)}
             ready = []
-            for k, b in enumerate(todo):
-                if k + 2 < 16:
-                    ts[k + 2] = close_scaled(y, todo[k + 2], ss, right, rnew)
-                close_sum(y, b, ts[k], so, right, {q: right(ts[k][q]) for q in b})
-                for q in b:
-                    rfree.append(y[q])
-                    y[q] = ts[k][q]
-                if k % 4 == 3:
-                    ready += [b[0] // 4, b[1] // 4]
-                    filler(n_fill)
-                elif k % 4 in (0, 1) and ready:
-                    turn_out(y, ready.pop(0), to, frm)
-            for g in ready:
-                turn_out(y, g, to, frm)
+            for n, b in enumerate(todo):
+                if n + 2 < 8:
+                    ts[n + 2] = close_scaled(z, todo[n + 2], ss)
+                close_sum(z, b, ts[n], so)
+                if n % 4 == 3:
+                    for e in b:
+                        g = e // 4
+                        turn_out(z, range(4 * g, 4 * g + 4), lambda q: to(q, g), frm)
+                    filler(plan[3])
 
-        upper(7)
-        y2 = {}
-        fill += [lambda grp=grp: norm_group(y1, grp, um_r[1], left, logged("s10"), lfree.append) for grp in groups(pairs(3))]
-        fill += turnover(y1, left, logged, lfree.append)
-        turn_start(y2, lambda l: 8 * (l % 4) + l // 4, r1, c_r1, 3, 3)
-        for bit in (1, 2, 3):
-            for n, grp in enumerate(groups(pairs(bit))):
-                norm_group(y2, grp, r1_r[bit - 1], right, rnew, rfree.append)
-                if n % 4 != 3:
-                    filler(1)
-        close_turn(y2, 4, r1_ss, r1_so, lambda z, g: z[:].rearrange("p (v g l h) -> p g v l h", v=32, g=8, l=4)[:, g],
-                   lambda ps: ps[:].rearrange("p (l h v) -> p v l h", l=4, h=4), 2)
-        y2 = {}
-        his = {}
-        todo = groups(pairs(0))
-
-        def r2_begin(grp):
-            for b in grp:
-                ps = turn_back(lambda v: v, b)
-                y2[b[0]] = rnew(b[0])
-                nc.scalar.copy(out=right(y2[b[0]]), in_=ps[b[0]])
-                his[b[1]] = ps[b[1]]
-
-        r2_begin(todo[0])
-        r2_begin(todo[1])
-        filler(2)
-        for n, grp in enumerate(todo):
-            norm_psum(y2, grp, his, r2_r[0], right, rnew)
-            if n + 2 < 8:
-                r2_begin(todo[n + 2])
-        for bit in (1, 2):
-            for grp in groups(pairs(bit)):
-                norm_group(y2, grp, r2_r[bit], right, rnew, rfree.append)
         pm_dn = {}
-        for k in range(4):
-            steps, pm_dn[k] = products(f_dn, d01_al, k)
-            fill += steps
-        close_turn(y2, 3, r2_ss, r2_so, lambda z, g: z[:].rearrange("p (e x g v l) -> p e g x v l", e=2, x=16, g=4, v=4)[:, g // 4, g % 4],
-                   lambda ps: ps[:].rearrange("p (v l x) -> p x v l", v=4, l=8), 2)
+        gate = cons.tile([128, 2], F32, name="gate")
 
-        y2 = {}
+        def down_matrices(t, ks):
+            nc.gpsimd.tensor_copy(out=gate[:, ks[0] // 2 : ks[0] // 2 + 1], in_=t[:, 0:1])
+            for k in ks:
+                steps, pm_dn[k] = products(nc.gpsimd, f_dn, d01_al, k, 0)
+                for st in steps:
+                    st()
+
+        turned({}, r1_r, lambda v: v, 3, r1_ss, r1_so,
+               lambda q, g: q[:].rearrange("p (w g v r) -> p g w v r", w=16, g=4, v=4)[:, g],
+               lambda ps: ps[:].rearrange("p (v r w) -> p w v r", v=4, r=8), PLAN_1, lambda t: None)
+        f_dn = load_factors(down_w, 0, 8)
+        turned({}, r2_r, lambda s: s, 2, r2_ss, r2_so,
+               lambda q, g: q[:].rearrange("p (c x e h v) -> p c e x h v", c=2, x=8, e=2, h=4)[:, g // 2, g % 2],
+               lambda ps: ps[:].rearrange("p (h v x) -> p x h v", h=4, v=16), PLAN_2, lambda t: down_matrices(t, (0, 1)))
         his = {}
-        todo = [[(4 * c + t, 4 * c + 4 + t) for t in (t0, t0 + 1)] for c in range(0, 8, 2) for t0 in (0, 2)]
+        todo = groups([(4 * c + t, 4 * c + 4 + t) for c in (0, 2) for t in range(4)])
 
-        def r3_begin(grp):
-            for b in grp:
-                ps = turn_back(lambda k: 16 * (k // 4 % 2) + 4 * (k % 4) + k // 8, b)
-                y2[b[0]] = placed["lo", b[0]]
-                nc.scalar.copy(out=right(y2[b[0]]), in_=ps[b[0]])
-                his[b[1]] = ps[b[1]]
+        def nine_begin(grp):
+            for lo, hi in grp:
+                low_copy(y, lo, turn_back(8 * (lo // 4 % 2) + 2 * (lo % 4) + lo // 8))
+                his[hi] = turn_back(8 * (hi // 4 % 2) + 2 * (hi % 4) + hi // 8)
 
-        r3_begin(todo[0])
-        r3_begin(todo[1])
-        filler(10)
+        nine_begin(todo[0])
+        filler(PLAN_3[0])
         for n, grp in enumerate(todo):
-            norm_psum(y2, grp, his, um_r[0], right, replay("hi"))
-            if n + 2 < 8:
-                r3_begin(todo[n + 2])
+            norm_psum(y, grp, his, um_r[0])
+            if n == 0:
+                down_matrices(y[grp[0][1]], (2, 3))
+            if n + 1 < 4:
+                nine_begin(todo[n + 1])
+            filler(PLAN_3[1])
+        for grp in groups([p for p in pairs(3) if p[0] < 16]):
+            norm_group(y, grp, um_r[1])
+        filler(len(fill))
 
-        for grp in groups(pairs(3)):
-            norm_group(y2, grp, um_r[1], right, replay("s10"), keep)
-
-        wcc = [cons.tile([128, 4, D], U32, tag="zc", name="wcc%d" % k, bufs=2, align_bytes=64) for k in range(2)]
+        wcc = [cons.tile([128, 2, D], U32, tag="zc%d" % (k // 2), name="wcc%d" % k, bufs=2, align_bytes=64) for k in range(4)]
         wcs = cons.tile([128, 8, D], U8, name="wcs", align_bytes=64)
         csrc = w_con.rearrange("(c p j) d -> c p j d", p=128, j=4)
         wr_t, wq_t = {}, {}
 
         def con_load(n):
             c, dh = n // 2, n % 2
-            wr_t[n] = work.tile([128, 4, 512], BF16, tag="wide", name="wr", bufs=3, align_bytes=64)
+            wr_t[n] = work.tile([128, 4, 512], BF16, tag="wide", name="wr", bufs=4, align_bytes=64)
             nc.sync.dma_start(out=wr_t[n][:], in_=csrc[c][:, :, 512 * dh : 512 * dh + 512])
 
         def con_weave(n):
@@ -617,7 +540,7 @@ def tile_butterflymlp_kernel(tc, x, w_bytes, w_scale, b_exp, up_w, up_bias, down
 
         def con_quant(n):
             c, dh = n // 2, n % 2
-            nc.vector.quantize_mx(out=wcc[c // 4][:, c % 4, 512 * dh : 512 * dh + 512].bitcast(FP8X4), scales=wcs[:, c, 512 * dh : 512 * dh + 512], in_=wq_t[n][:])
+            nc.vector.quantize_mx(out=wcc[c // 2][:, c % 2, 512 * dh : 512 * dh + 512].bitcast(FP8X4), scales=wcs[:, c, 512 * dh : 512 * dh + 512], in_=wq_t[n][:])
 
         con = [0]
 
@@ -634,66 +557,65 @@ def tile_butterflymlp_kernel(tc, x, w_bytes, w_scale, b_exp, up_w, up_bias, down
                 con_quant(n - 1)
             con[0] = n + 1
 
-        y = y1
-        dfree = []
-
-        def dnew(k):
-            return dfree.pop(0)
-
         his = {}
+
+        def last_stage(c):
+            for grp in groups([(4 * c + t, 4 * c + 16 + t) for t in range(4)]):
+                norm_group(y, grp, um_r[2])
+                for p in grp:
+                    for b in p:
+                        nc.scalar.activation(out=y[b][:], in_=y[b][:], func=ACT.Gelu, scale=um_al[:, b : b + 1], bias=upb[:, b : b + 1])
+
+        def down_first(c, bit):
+            for cc in (c, c + 4):
+                norm_group(y, [(4 * cc + p[0], 4 * cc + p[1]) for p in pairs(bit)[0:2]], d01_r[bit])
 
         def down_middle(c):
             for t in range(4):
                 b = 4 * c + t
                 ps = bank()
-                nc.tensor.matmul(ps[:], block_matrix(pm_dn[c // 2], b), full(y[b]), start=True, stop=True)
-                dfree.append(y[b])
+                nc.tensor.matmul(ps[:], block_matrix(pm_dn[c // 2], b), y[b][:], start=True, stop=True)
                 if c % 2 == 0:
-                    y[b] = dnew(b)
-                    nc.scalar.copy(out=full(y[b]), in_=ps[:])
+                    low_copy(y, b, ps)
                 else:
-                    his[b] = ps[:]
+                    his[b] = ps
 
         def down_nine(c):
             for t0 in (0, 2):
-                norm_psum(y, [(4 * c + t, 4 * c + 4 + t) for t in (t0, t0 + 1)], his, d9_r[0], full, dnew)
+                norm_psum(y, [(4 * c + t, 4 * c + 4 + t) for t in (t0, t0 + 1)], his, d9_r[0])
 
         def down_ten(c):
             for t0 in (0, 2):
-                norm_group(y, [(4 * c + t, 4 * c + 8 + t) for t in (t0, t0 + 1)], d9_r[1], full, dnew, dfree.append)
+                norm_group(y, [(4 * c + t, 4 * c + 8 + t) for t in (t0, t0 + 1)], d9_r[1])
 
-        over = turnover(y2, right, replay, keep)
-
-        def over_steps(n):
-            for k in range(n):
-                over.pop(0)()
-
-        filler(len(fill))
-        over_steps(4)
+        last_stage(0)
         con_step()
-        over_steps(4)
+        last_stage(1)
+        down_first(0, 0)
         con_step()
-        over_steps(2)
+        last_stage(2)
+        down_first(0, 1)
         down_middle(0)
         con_step()
-        over_steps(2)
+        down_first(1, 0)
         down_middle(4)
-        over_steps(4)
         con_step()
+        last_stage(3)
+        down_first(1, 1)
         down_middle(1)
-        over_steps(2)
+        con_step()
+        down_first(2, 0)
         down_nine(0)
         down_middle(5)
         con_step()
-        over_steps(2)
+        down_first(2, 1)
         down_nine(4)
-        con_step()
         down_middle(2)
-        over_steps(4)
         con_step()
+        down_first(3, 0)
         down_middle(6)
-        dfree.extend(lfree)
         con_step()
+        down_first(3, 1)
         down_middle(3)
         con_step()
         down_nine(2)
@@ -711,7 +633,14 @@ def tile_butterflymlp_kernel(tc, x, w_bytes, w_scale, b_exp, up_w, up_bias, down
         con_step()
         down_ten(5)
         con_step()
-        con_step()
+
+        bb = work.tile([128, D], F32, tag="wb", name="bb", bufs=3, align_bytes=64)
+        braw = []
+        for v in (b_con, down_bias):
+            br = work.tile([128, D], BF16, tag="wb", name="br", bufs=3, align_bytes=64)
+            nc.sync.dma_start(out=br[:], in_=v.partition_broadcast(128))
+            braw.append(br)
+        tt(nc.vector, bb[:], braw[0][:], braw[1][:], ALU.add)
 
         ht = cons.tile([128, 8, 4, TOK], BF16, tag="fh", name="ht")
         acc = [bank() for n in range(8)]
@@ -730,31 +659,26 @@ def tile_butterflymlp_kernel(tc, x, w_bytes, w_scale, b_exp, up_w, up_bias, down
             for k in range(8):
                 i, dh = k // 2, k % 2
                 nc.tensor.matmul_mx(out=acc[k][:], lhsT=hq_t[c][:, 128 * i : 128 * i + 128].bitcast(FP8X4), lhsT_scale=hs_t[c][:, 128 * i : 128 * i + 128],
-                                    rhs=wcc[c // 4][:, c % 4, 512 * dh : 512 * dh + 512].bitcast(FP8X4), rhs_scale=wcs[:, c, 512 * dh : 512 * dh + 512],
+                                    rhs=wcc[c // 2][:, c % 2, 512 * dh : 512 * dh + 512].bitcast(FP8X4), rhs_scale=wcs[:, c, 512 * dh : 512 * dh + 512],
                                     start=first, stop=last)
 
         todo = [(4 * c + t, 4 * c + 16 + t) for c in range(4) for t in range(4)]
-        ts = {0: close_scaled(y, todo[0], d_ss, full, dnew)}
+        ts = {0: close_scaled(y, todo[0], d_ss), 1: close_scaled(y, todo[1], d_ss)}
         for k, b in enumerate(todo):
             c, t = k // 4, k % 4
-            if k + 1 < 16 and len(dfree) >= 2:
-                ts[k + 1] = close_scaled(y, todo[k + 1], d_ss, full, dnew)
-            close_sum(y, b, ts[k], d_so, full, {b[0]: ht[:, c, t, :], b[1]: ht[:, c + 4, t, :]})
-            for q in b:
-                dfree.append(y[q])
-                dfree.append(ts[k][q])
-            if k + 1 < 16 and k + 1 not in ts:
-                ts[k + 1] = close_scaled(y, todo[k + 1], d_ss, full, dnew)
+            if k + 2 < 16:
+                ts[k + 2] = close_scaled(y, todo[k + 2], d_ss)
+            close_sum(y, b, ts[k], d_so, {b[0]: ht[:, c, t, :], b[1]: ht[:, c + 4, t, :]})
             if c > 0 and t == 0:
-                h_weave(c - 1, nc.scalar.copy)
-                h_weave(c + 3, nc.vector.tensor_copy)
+                h_weave(c - 1, sca)
+                h_weave(c + 3, von)
                 h_quant(c + 3)
                 second_product(c + 3, c == 1, False)
             if c > 0 and t == 2:
                 h_quant(c - 1)
                 second_product(c - 1, False, False)
-        h_weave(3, nc.scalar.copy)
-        h_weave(7, nc.vector.tensor_copy)
+        h_weave(3, sca)
+        h_weave(7, von)
         h_quant(7)
         second_product(7, False, False)
         h_quant(3)
@@ -762,6 +686,6 @@ def tile_butterflymlp_kernel(tc, x, w_bytes, w_scale, b_exp, up_w, up_bias, down
         orows = out.rearrange("b s d -> (b s) d")
         for k in range(8):
             i, dh = k // 2, k % 2
-            ot = work.tile([128, 512], F32, tag="wide" if k % 2 else "inter", name="ot", bufs=3, align_bytes=64)
+            ot = work.tile([128, 512], F32, tag="wide" if k % 2 else "inter", name="ot", bufs=4 if k % 2 else 3, align_bytes=64)
             tt(nc.vector, ot[:], acc[k][:], bb[:, 512 * dh : 512 * dh + 512], ALU.add)
             nc.sync.dma_start(out=orows[128 * i : 128 * i + 128, 512 * dh : 512 * dh + 512], in_=ot[:])

@@ -13,10 +13,12 @@ ALU = mybir.AluOpType
 ACT = mybir.ActivationFunctionType
 
 TOK, D, H = 512, 1024, 4096
-A_WIDEN = (3,)
+A_WIDEN = ()
 V_WEAVE = 5
-PLAN_1 = (2, (0, 1, 0, 1), (0, 1, 0, 0), 1)
-PLAN_2 = (4, (1, 1, 0, 1), (0, 1, 0, 1), 3)
+H_ON_V = (4, 5, 6, 7)
+ACT_KINDS = ()
+PLAN_1 = (2, (0, 1, 0, 1), (0, 1, 0, 1), 2)
+PLAN_2 = (4, (1, 1, 1, 1), (0, 1, 0, 1), 2)
 PLAN_3 = (6, 1)
 FLOPS = 2 * 2 * TOK * D * H + 2 * 12 * 3 * TOK * H
 
@@ -101,6 +103,10 @@ def tile_butterflymlp_kernel(tc, x, w_bytes, w_scale, b_exp, up_w, up_bias, down
             for e in range(2):
                 nc.sync.dma_start(out=r_raw[e::2, k, :].rearrange("p (u q) -> p u q", q=4), in_=src[e])
 
+        s_raw = cons.tile([128, 16, 8], BF16, name="s_raw")
+        for t in range(4):
+            nc.sync.dma_start(out=s_raw[32 * t : 32 * t + 32, :, :], in_=flat(up_w, 1).rearrange("(z h v e) -> z h v e", z=2, h=32, v=16)[0])
+
         def load_factors(w, c0, n_c):
             ft = cons.tile([128, 16 * 127 * 8], BF16, tag="fh", name="ft")
             views = []
@@ -128,8 +134,8 @@ def tile_butterflymlp_kernel(tc, x, w_bytes, w_scale, b_exp, up_w, up_bias, down
         def half(a, bit, o):
             return a.rearrange("p (h o l) -> p h o l", o=2, l=1 << bit)[:, :, o, :]
 
-        def coefficients(raw, bits, nb, name):
-            n = len(bits)
+        def coefficients(raw, bits, nb, name, before=None):
+            n = len(bits) + (0 if before is None else 1)
             w = nb * n
             wd = cons.tile([128, n, nb], F32, name=name + "_wd")
             wo = cons.tile([128, n, nb], F32, name=name + "_wo")
@@ -138,6 +144,8 @@ def tile_butterflymlp_kernel(tc, x, w_bytes, w_scale, b_exp, up_w, up_bias, down
                 src = raw[:, k, :].rearrange("p (h l q) -> p h l q", l=lo, q=4)
                 nc.gpsimd.tensor_copy(out=wd[:, k, :].rearrange("p (h o l) -> p h l o", o=2, l=lo), in_=src[:, :, :, 0:4:3])
                 nc.gpsimd.tensor_copy(out=wo[:, k, :].rearrange("p (h o l) -> p h l o", o=2, l=lo), in_=src[:, :, :, 1:3])
+            if before is not None:
+                before(wd[:, n - 1, :], wo[:, n - 1, :])
             d = wd[:].rearrange("p k b -> p (k b)")
             o = wo[:].rearrange("p k b -> p (k b)")
             ta, tb, tk = [tmp.tile([128, 160], F32, tag="t%d" % e, name="tmp")[:, 0:w] for e in range(3)]
@@ -169,10 +177,11 @@ def tile_butterflymlp_kernel(tc, x, w_bytes, w_scale, b_exp, up_w, up_bias, down
         def small(cf, name):
             return cons.tile([128, cf["nb"]], F32, name=name)[:]
 
-        def chain(cf, ks, name):
-            rs = [cf["rr"][:, ks[0], :]]
-            al, ial = cf["den"][:, ks[0], :], cf["inv"][:, ks[0], :]
-            for k in ks[1:]:
+        def chain(cf, ks, name, k0=None):
+            rs = [] if k0 is not None else [cf["rr"][:, ks[0], :]]
+            k1 = ks[0] if k0 is None else k0
+            al, ial = cf["den"][:, k1, :], cf["inv"][:, k1, :]
+            for k in ks[len(rs) :]:
                 r = small(cf, "%s_r%d" % (name, k))
                 partner_mul(r, cf["rr"][:, k, :], al, cf["bits"][k])
                 tt(nc.gpsimd, r, r, ial, ALU.mult)
@@ -223,10 +232,12 @@ def tile_butterflymlp_kernel(tc, x, w_bytes, w_scale, b_exp, up_w, up_bias, down
                 stt(y[hi][:], y[lo][:], r[:, hi : hi + 1], y[hi][:])
                 y[lo] = fresh[lo]
 
-        def norm_psum(y, group, ps, r):
-            for lo, hi in group:
+        def norm_psum(y, group, ps, r, beside=None):
+            for n, (lo, hi) in enumerate(group):
                 y[hi] = ytile()
                 stt(y[hi][:], y[lo][:], r[:, hi : hi + 1], ps[hi][:])
+                if n == 0 and beside is not None:
+                    beside(y[hi])
             for lo, hi in group:
                 stt(y[lo][:], ps[hi][:], r[:, lo : lo + 1], y[lo][:])
 
@@ -247,6 +258,49 @@ def tile_butterflymlp_kernel(tc, x, w_bytes, w_scale, b_exp, up_w, up_bias, down
                 stt(ts[k][:] if dst is None else dst[k], y[other][:], so[:, k : k + 1], ts[k][:])
             if dst is None:
                 y.update(ts)
+
+        def stage_one(wd, wo):
+            for t in range(4):
+                q = slice(32 * t, 32 * t + 32)
+                e = 4 * (t % 2)
+                nc.gpsimd.tensor_copy(out=wd[q, :], in_=s_raw[q, :, e + 3 * (t // 2)])
+                nc.gpsimd.tensor_copy(out=wo[q, :], in_=s_raw[q, :, e + 1 + t // 2])
+
+        gate = cons.tile([128, 1], F32, name="gate")
+
+        def wait_for(t):
+            nc.gpsimd.tensor_copy(out=gate[:], in_=t[:, 0:1])
+
+        def pool_begin(y, group, r):
+            ts = {}
+            for p in group:
+                for k in p:
+                    ts[k] = ytile()
+                    scaled(ts[k][:], y[p[0] + p[1] - k][:], r[:, k : k + 1])
+            return ts
+
+        def pool_sum(y, ts, t):
+            wait_for(t)
+            for k in ts:
+                tt(nc.gpsimd, ts[k][:], ts[k][:], y[k][:], ALU.add)
+            y.update(ts)
+
+        def stage_group(y, group, r, kind):
+            if kind in ACT_KINDS and len(group) == 2:
+                acts_group(y, group, r)
+            else:
+                norm_group(y, group, r)
+
+        def acts_group(y, group, r):
+            p, q = group
+            ts = {}
+            for k in p:
+                ts[k] = ytile()
+                scaled(ts[k][:], y[p[0] + p[1] - k][:], r[:, k : k + 1])
+            norm_group(y, [q], r)
+            for k in p:
+                tt(nc.vector, ts[k][:], ts[k][:], y[k][:], ALU.add)
+            y.update(ts)
 
         xc = cons.tile([128, 2, TOK], U32, name="xc", align_bytes=64)
         xs = cons.tile([128, 2, TOK], U8, name="xs", align_bytes=64)
@@ -272,7 +326,7 @@ def tile_butterflymlp_kernel(tc, x, w_bytes, w_scale, b_exp, up_w, up_bias, down
 
         von, sca = nc.vector.tensor_copy, nc.scalar.copy
 
-        widen(0, 0)
+        widen(0, 0, (2, 3))
         for g in range(2):
             xg = work.tile([128, TOK * 4], BF16, tag="inter", name="xg", bufs=3, align_bytes=64)
             for h in range(2):
@@ -289,7 +343,7 @@ def tile_butterflymlp_kernel(tc, x, w_bytes, w_scale, b_exp, up_w, up_bias, down
                 weave(0, 0, von)
         quant(0, 0)
         um, um_finish = coefficients(um_raw, (0, 1, 2, 3, 4), 32, "um")
-        widen(0, 1)
+        widen(0, 1, (2, 3))
         weave(0, 1, von)
         um_finish()
         bm = cons.tile([128, 2, 32], F32, name="bm")
@@ -360,11 +414,9 @@ def tile_butterflymlp_kernel(tc, x, w_bytes, w_scale, b_exp, up_w, up_bias, down
             first_sum(y, p0)
             quant(c + 1, 0)
             first_sum(y, p1)
-            ts = [(b, close_scaled(y, b, um["wd"][:, 1, :])) for b in ((4 * c, 4 * c + 2), (4 * c + 1, 4 * c + 3))]
             widen(c + 2, 0, A_WIDEN)
             weave(c + 1, 1, von)
-            for b, t in ts:
-                close_sum(y, b, t, um["wo"][:, 1, :])
+            norm_group(y, [(4 * c, 4 * c + 2), (4 * c + 1, 4 * c + 3)], um["rr"][:, 1, :])
             if c >= 2:
                 matrix_steps(3)
             quant(c + 1, 1)
@@ -375,10 +427,10 @@ def tile_butterflymlp_kernel(tc, x, w_bytes, w_scale, b_exp, up_w, up_bias, down
                 for k in (2, 3):
                     steps, pm_up[k] = products(nc.vector, f_up, um["den"][:, 1, :], k, 4)
                     steps_up += steps
-                r1, r1_finish = coefficients(r_raw[:, 0:4, :], (0, 1, 2, 3), 16, "r1")
+                r1, r1_finish = coefficients(r_raw[:, 0:4, :], (0, 1, 2, 3), 16, "r1", stage_one)
             if c == 1:
                 r1_finish()
-                r1_r, r1_al = chain(r1, (0, 1, 2), "r1")
+                r1_r, r1_al = chain(r1, (0, 1, 2), "r1", 4)
                 r1_ss, r1_so = closing(r1, 3, r1_al, "r1")
                 dm_raw = load_main(down_w, "dm_raw")
                 r2, r2_finish = coefficients(r_raw[:, 4:7, :], (0, 1, 2), 16, "r2")
@@ -449,7 +501,7 @@ def tile_butterflymlp_kernel(tc, x, w_bytes, w_scale, b_exp, up_w, up_bias, down
             fill += [lambda c=c: s0(c), lambda c=c: s1(c), lambda c=c: s2(c), lambda c=c: s3(c), lambda c=c: s4(c)]
             if c % 2 == 1:
                 fill += [lambda c=c: s5(c, 0), lambda c=c: s5(c, 2)]
-        fill += [lambda grp=grp: norm_group(y, grp, um_r[1]) for grp in groups([p for p in pairs(3) if p[0] >= 16])]
+        fill += [lambda grp=grp: stage_group(y, grp, um_r[1], "u10f") for grp in groups([p for p in pairs(3) if p[0] >= 16])]
 
         def turned(z, coefs, place, bit, ss, so, to, frm, plan, beside):
             todo = groups(pairs(0, 16))
@@ -463,15 +515,13 @@ def tile_butterflymlp_kernel(tc, x, w_bytes, w_scale, b_exp, up_w, up_bias, down
             begin(todo[0])
             filler(plan[0])
             for n, grp in enumerate(todo):
-                norm_psum(z, grp, his, coefs[0])
-                if n == 0:
-                    beside(z[grp[0][1]])
+                norm_psum(z, grp, his, coefs[0], beside if n == 0 else None)
                 if n + 1 < 4:
                     begin(todo[n + 1])
                 filler(plan[1][n])
             for k in range(1, bit):
                 for n, grp in enumerate(groups(pairs(k, 16))):
-                    norm_group(z, grp, coefs[k])
+                    stage_group(z, grp, coefs[k], "t%d%d" % (bit, k))
                     filler(plan[2][n])
             todo = pairs(bit, 16)
             ts = {0: close_scaled(z, todo[0], ss), 1: close_scaled(z, todo[1], ss)}
@@ -487,10 +537,9 @@ def tile_butterflymlp_kernel(tc, x, w_bytes, w_scale, b_exp, up_w, up_bias, down
                     filler(plan[3])
 
         pm_dn = {}
-        gate = cons.tile([128, 2], F32, name="gate")
 
         def down_matrices(t, ks):
-            nc.gpsimd.tensor_copy(out=gate[:, ks[0] // 2 : ks[0] // 2 + 1], in_=t[:, 0:1])
+            wait_for(t)
             for k in ks:
                 steps, pm_dn[k] = products(nc.gpsimd, f_dn, d01_al, k, 0)
                 for st in steps:
@@ -498,7 +547,7 @@ def tile_butterflymlp_kernel(tc, x, w_bytes, w_scale, b_exp, up_w, up_bias, down
 
         turned({}, r1_r, lambda v: v, 3, r1_ss, r1_so,
                lambda q, g: q[:].rearrange("p (w g v r) -> p g w v r", w=16, g=4, v=4)[:, g],
-               lambda ps: ps[:].rearrange("p (v r w) -> p w v r", v=4, r=8), PLAN_1, lambda t: None)
+               lambda ps: ps[:].rearrange("p (v r w) -> p w v r", v=4, r=8), PLAN_1, None)
         f_dn = load_factors(down_w, 0, 8)
         turned({}, r2_r, lambda s: s, 2, r2_ss, r2_so,
                lambda q, g: q[:].rearrange("p (c x e h v) -> p c e x h v", c=2, x=8, e=2, h=4)[:, g // 2, g % 2],
@@ -514,14 +563,12 @@ def tile_butterflymlp_kernel(tc, x, w_bytes, w_scale, b_exp, up_w, up_bias, down
         nine_begin(todo[0])
         filler(PLAN_3[0])
         for n, grp in enumerate(todo):
-            norm_psum(y, grp, his, um_r[0])
-            if n == 0:
-                down_matrices(y[grp[0][1]], (2, 3))
+            norm_psum(y, grp, his, um_r[0], (lambda t: down_matrices(t, (2, 3))) if n == 0 else None)
             if n + 1 < 4:
                 nine_begin(todo[n + 1])
             filler(PLAN_3[1])
         for grp in groups([p for p in pairs(3) if p[0] < 16]):
-            norm_group(y, grp, um_r[1])
+            stage_group(y, grp, um_r[1], "u10")
         filler(len(fill))
 
         wcc = [cons.tile([128, 2, D], U32, tag="zc%d" % (k // 2), name="wcc%d" % k, bufs=2, align_bytes=64) for k in range(4)]
@@ -561,14 +608,17 @@ def tile_butterflymlp_kernel(tc, x, w_bytes, w_scale, b_exp, up_w, up_bias, down
 
         def last_stage(c):
             for grp in groups([(4 * c + t, 4 * c + 16 + t) for t in range(4)]):
-                norm_group(y, grp, um_r[2])
+                stage_group(y, grp, um_r[2], "u11")
                 for p in grp:
                     for b in p:
                         nc.scalar.activation(out=y[b][:], in_=y[b][:], func=ACT.Gelu, scale=um_al[:, b : b + 1], bias=upb[:, b : b + 1])
 
+        def two_pairs(c, bit):
+            return [(4 * c + p[0], 4 * c + p[1]) for p in pairs(bit)[0:2]]
+
         def down_first(c, bit):
             for cc in (c, c + 4):
-                norm_group(y, [(4 * cc + p[0], 4 * cc + p[1]) for p in pairs(bit)[0:2]], d01_r[bit])
+                stage_group(y, two_pairs(cc, bit), d01_r[bit], "d%d" % bit)
 
         def down_middle(c):
             for t in range(4):
@@ -580,13 +630,20 @@ def tile_butterflymlp_kernel(tc, x, w_bytes, w_scale, b_exp, up_w, up_bias, down
                 else:
                     his[b] = ps
 
-        def down_nine(c):
+        def down_nine(c, group=None, r=None):
+            beside = None
+            if group is not None:
+                ts = pool_begin(y, group, r)
+                beside = lambda t: pool_sum(y, ts, t)
             for t0 in (0, 2):
-                norm_psum(y, [(4 * c + t, 4 * c + 4 + t) for t in (t0, t0 + 1)], his, d9_r[0])
+                norm_psum(y, [(4 * c + t, 4 * c + 4 + t) for t in (t0, t0 + 1)], his, d9_r[0], beside if t0 == 0 else None)
 
-        def down_ten(c):
-            for t0 in (0, 2):
-                norm_group(y, [(4 * c + t, 4 * c + 8 + t) for t in (t0, t0 + 1)], d9_r[1])
+        def ten_pairs(c, t0):
+            return [(4 * c + t, 4 * c + 8 + t) for t in (t0, t0 + 1)]
+
+        def down_ten(c, t0s=(0, 2)):
+            for t0 in t0s:
+                stage_group(y, ten_pairs(c, t0), d9_r[1], "d10")
 
         last_stage(0)
         con_step()
@@ -605,17 +662,17 @@ def tile_butterflymlp_kernel(tc, x, w_bytes, w_scale, b_exp, up_w, up_bias, down
         down_middle(1)
         con_step()
         down_first(2, 0)
-        down_nine(0)
+        down_nine(0, two_pairs(2, 1), d01_r[1])
         down_middle(5)
         con_step()
-        down_first(2, 1)
-        down_nine(4)
+        stage_group(y, two_pairs(6, 1), d01_r[1], "d1")
+        down_first(3, 0)
+        down_nine(4, two_pairs(3, 1), d01_r[1])
         down_middle(2)
         con_step()
-        down_first(3, 0)
         down_middle(6)
         con_step()
-        down_first(3, 1)
+        stage_group(y, two_pairs(7, 1), d01_r[1], "d1")
         down_middle(3)
         con_step()
         down_nine(2)
@@ -623,15 +680,17 @@ def tile_butterflymlp_kernel(tc, x, w_bytes, w_scale, b_exp, up_w, up_bias, down
         down_middle(7)
         down_ten(0)
         con_step()
-        down_ten(1)
+        down_nine(6, ten_pairs(1, 0), d9_r[1])
         con_step()
-        down_nine(6)
+        down_ten(1, (2,))
         con_step()
         con_step()
         down_ten(4)
         con_step()
         con_step()
         down_ten(5)
+        con_step()
+        con_step()
         con_step()
 
         bb = work.tile([128, D], F32, tag="wb", name="bb", bufs=3, align_bytes=64)
@@ -671,14 +730,14 @@ def tile_butterflymlp_kernel(tc, x, w_bytes, w_scale, b_exp, up_w, up_bias, down
             close_sum(y, b, ts[k], d_so, {b[0]: ht[:, c, t, :], b[1]: ht[:, c + 4, t, :]})
             if c > 0 and t == 0:
                 h_weave(c - 1, sca)
-                h_weave(c + 3, von)
+                h_weave(c + 3, von if c + 3 in H_ON_V else sca)
                 h_quant(c + 3)
                 second_product(c + 3, c == 1, False)
             if c > 0 and t == 2:
                 h_quant(c - 1)
                 second_product(c - 1, False, False)
         h_weave(3, sca)
-        h_weave(7, von)
+        h_weave(7, von if 7 in H_ON_V else sca)
         h_quant(7)
         second_product(7, False, False)
         h_quant(3)

from contextlib import ExitStack

import concourse.mybir as mybir
from concourse.masks import make_identity

F32 = mybir.dt.float32
BF16 = mybir.dt.bfloat16
U32 = mybir.dt.uint32
U8 = mybir.dt.uint8
FP8 = mybir.dt.float8_e4m3fn
FP8X4 = mybir.dt.float8_e4m3fn_x4
ALU = mybir.AluOpType
ACT = mybir.ActivationFunctionType

TOK, D, H = 512, 1024, 4096
A_WIDEN = ()
V_WEAVE = 5
H_ON_V = (4, 5, 6, 7)
ACT_KINDS = ()
PLAN_1 = (2, (0, 1, 0, 1), (0, 1, 0, 1), 2)
PLAN_2 = (4, (1, 1, 1, 1), (0, 1, 0, 1), 2)
PLAN_3 = (6, 1)
FLOPS = 2 * 2 * TOK * D * H + 2 * 12 * 3 * TOK * H


def pairs(bit, n=32):
    return [(b, b | (1 << bit)) for b in range(n) if not b & (1 << bit)]


def groups(todo, n=2):
    return [todo[k : k + n] for k in range(0, len(todo), n)]


def tile_butterflymlp_kernel(tc, x, w_bytes, w_scale, b_exp, up_w, up_bias, down_w, w_con, b_con, down_bias, out):
    nc = tc.nc
    with ExitStack() as ctx:
        cons = ctx.enter_context(tc.tile_pool(name="cons", bufs=1))
        tmp = ctx.enter_context(tc.tile_pool(name="tmp", bufs=1))
        work = ctx.enter_context(tc.tile_pool(name="work", bufs=2))
        psum = ctx.enter_context(tc.psum_pool(name="psum", bufs=8))
        ctx.enter_context(tc.manual_schedule())

        def bank():
            ps = psum.tile([128, 512], F32, tag="ps", name="ps")
            return ps

        def ytile():
            return work.tile([128, TOK], F32, tag="y", name="y", bufs=38)

        def stt(o, in0, s, in1):
            nc.vector.scalar_tensor_tensor(out=o, in0=in0, scalar=s, in1=in1, op0=ALU.mult, op1=ALU.add)

        def scaled(o, i, s, b=None):
            if b is None:
                nc.scalar.activation(out=o, in_=i, func=ACT.Copy, scale=s)
            else:
                nc.scalar.activation(out=o, in_=i, func=ACT.Identity, scale=s, bias=b)

        ident = cons.tile([128, 128], F32, name="ident")
        make_identity(nc, ident[:])
        wsrc = w_bytes.rearrange("(g p t) n -> g p t n", g=2, t=4)
        wsc = cons.tile([128, 2, 4], F32, name="wsc")
        nc.sync.dma_start(out=wsc[:], in_=w_scale.rearrange("(g p t) o -> p g (t o)", g=2, t=4))
        wbs = {}

        def load_wexp(c):
            wbs[c] = work.tile([128, 2, 4, 512], U8, tag="wb", name="wb", bufs=3, align_bytes=64)
            for g in range(2):
                nc.sync.dma_start(out=wbs[c][:, g, :, :], in_=wsrc[g][:, :, 512 * c : 512 * c + 512])

        load_wexp(0)
        xrows = x.rearrange("b s d -> (b s) d").rearrange("(i p) d -> p i d", p=128)
        xraw = []
        for h in range(2):
            xr = work.tile([128, 2, D], BF16, tag="wide", name="xr", bufs=4, align_bytes=64)
            nc.sync.dma_start(out=xr[:], in_=xrows[:, 2 * h : 2 * h + 2, :])
            xraw.append(xr)

        def flat(w, s):
            return w[s].rearrange("k o i -> (k o i)")

        def load_main(w, name):
            raw = cons.tile([128, 5, 64], BF16, name=name)
            for k, s in enumerate((0, 1, 9, 10, 11)):
                n = 8 if k < 2 else 4
                nc.sync.dma_start(out=raw[:, k, :].rearrange("p (c r) -> p c r", c=n), in_=flat(w, s).rearrange("(c p r) -> p c r", c=n, p=128))
            return raw

        um_raw = load_main(up_w, "um_raw")
        bm_raw = cons.tile([128, 2, 32], BF16, name="bm_raw")
        for k, v in ((0, b_exp), (1, up_bias)):
            nc.sync.dma_start(out=bm_raw[:, k, :].rearrange("p (c t) -> p c t", t=4), in_=v.rearrange("(c p t) -> p c t", p=128, t=4))
        load_wexp(1)
        load_wexp(2)

        r_raw = cons.tile([128, 7, 32], BF16, name="r_raw")
        for k in range(4):
            src = flat(up_w, 2 + k).rearrange("(z h u t q) -> z t h u q", z=2, h=32, u=8, t=4)[0]
            for t in range(4):
                nc.sync.dma_start(out=r_raw[32 * t : 32 * t + 32, k, :].rearrange("p (u q) -> p u q", q=4), in_=src[t])
        for k in range(4, 7):
            src = flat(up_w, 2 + k).rearrange("(z e u l q) -> z e l u q", z=2, e=2, u=8, l=64)[0]
            for e in range(2):
                nc.sync.dma_start(out=r_raw[e::2, k, :].rearrange("p (u q) -> p u q", q=4), in_=src[e])

        s_raw = cons.tile([128, 16, 8], BF16, name="s_raw")
        for t in range(4):
            nc.sync.dma_start(out=s_raw[32 * t : 32 * t + 32, :, :], in_=flat(up_w, 1).rearrange("(z h v e) -> z h v e", z=2, h=32, v=16)[0])

        def load_factors(w, c0, n_c):
            ft = cons.tile([128, 16 * 127 * 8], BF16, tag="fh", name="ft")
            views = []
            off = 0
            for j in range(7):
                run = 16 << j
                fj = ft[:, off : off + n_c * run].rearrange("p (c e) -> p c e", c=n_c)
                off += n_c * run
                views.append(fj)
                src = flat(w, 2 + j).rearrange("(c h e) -> h c e", c=8, e=run)[:, c0 : c0 + n_c, :]
                n_lo, n_hi = 1 << j, 1 << (6 - j)
                for i in range(2):
                    if n_lo <= n_hi:
                        for lo in range(n_lo):
                            nc.sync.dma_start(out=fj[i * n_lo + lo :: 2 * n_lo, :, 0 : run - 1], in_=src[:, :, i : i + run - 1])
                    else:
                        for h in range(n_hi):
                            p0 = h * 2 * n_lo + i * n_lo
                            nc.sync.dma_start(out=fj[p0 : p0 + n_lo, :, 0 : run - 1], in_=src[h][:, i : i + run - 1].partition_broadcast(n_lo))
            return views

        def tt(eng, o, a, b, op):
            eng.tensor_tensor(out=o, in0=a, in1=b, op=op)

        def half(a, bit, o):
            return a.rearrange("p (h o l) -> p h o l", o=2, l=1 << bit)[:, :, o, :]

        def coefficients(raw, bits, nb, name, before=None):
            n = len(bits) + (0 if before is None else 1)
            w = nb * n
            wd = cons.tile([128, n, nb], F32, name=name + "_wd")
            wo = cons.tile([128, n, nb], F32, name=name + "_wo")
            for k, bit in enumerate(bits):
                lo = 1 << bit
                src = raw[:, k, :].rearrange("p (h l q) -> p h l q", l=lo, q=4)
                nc.gpsimd.tensor_copy(out=wd[:, k, :].rearrange("p (h o l) -> p h l o", o=2, l=lo), in_=src[:, :, :, 0:4:3])
                nc.gpsimd.tensor_copy(out=wo[:, k, :].rearrange("p (h o l) -> p h l o", o=2, l=lo), in_=src[:, :, :, 1:3])
            if before is not None:
                before(wd[:, n - 1, :], wo[:, n - 1, :])
            d = wd[:].rearrange("p k b -> p (k b)")
            o = wo[:].rearrange("p k b -> p (k b)")
            ta, tb, tk = [tmp.tile([128, 160], F32, tag="t%d" % e, name="tmp")[:, 0:w] for e in range(3)]
            den = cons.tile([128, n, nb], F32, name=name + "_den")
            inv = cons.tile([128, n, nb], F32, name=name + "_inv")
            rr = cons.tile([128, n, nb], F32, name=name + "_rr")
            dn = den[:].rearrange("p k b -> p (k b)")
            iv = inv[:].rearrange("p k b -> p (k b)")
            v, g = nc.vector, nc.gpsimd
            v.scalar_tensor_tensor(out=tb, in0=o, scalar=-1.0, in1=o, op0=ALU.mult, op1=ALU.max)
            v.scalar_tensor_tensor(out=ta, in0=d, scalar=-1.0, in1=d, op0=ALU.mult, op1=ALU.max)
            v.tensor_scalar(out=tb, in0=tb, scalar1=2.0**-20, scalar2=2.0**-40, op0=ALU.mult, op1=ALU.max)
            tt(v, tk, ta, tb, ALU.is_ge)
            tt(g, ta, tk, d, ALU.mult)
            g.tensor_scalar(out=tk, in0=tk, scalar1=-1.0, scalar2=1.0, op0=ALU.mult, op1=ALU.add)
            tt(g, tb, tk, tb, ALU.mult)
            tt(g, dn, ta, tb, ALU.add)

            def finish():
                v.reciprocal(out=iv, in_=dn)
                tt(g, rr[:].rearrange("p k b -> p (k b)"), o, iv, ALU.mult)

            return dict(wd=wd, wo=wo, den=den, inv=inv, rr=rr, bits=bits, nb=nb), finish

        def partner_mul(o, a, b, bit):
            for i in range(2):
                tt(nc.gpsimd, half(o, bit, i), half(a, bit, i), half(b, bit, 1 - i), ALU.mult)

        def small(cf, name):
            return cons.tile([128, cf["nb"]], F32, name=name)[:]

        def chain(cf, ks, name, k0=None):
            rs = [] if k0 is not None else [cf["rr"][:, ks[0], :]]
            k1 = ks[0] if k0 is None else k0
            al, ial = cf["den"][:, k1, :], cf["inv"][:, k1, :]
            for k in ks[len(rs) :]:
                r = small(cf, "%s_r%d" % (name, k))
                partner_mul(r, cf["rr"][:, k, :], al, cf["bits"][k])
                tt(nc.gpsimd, r, r, ial, ALU.mult)
                a2 = small(cf, "%s_a%d" % (name, k))
                tt(nc.gpsimd, a2, al, cf["den"][:, k, :], ALU.mult)
                if k != ks[-1]:
                    i2 = small(cf, "%s_i%d" % (name, k))
                    tt(nc.gpsimd, i2, ial, cf["inv"][:, k, :], ALU.mult)
                    ial = i2
                rs.append(r)
                al = a2
            return rs, al

        def closing(cf, k, al, name):
            ss = small(cf, name + "_ss")
            so = small(cf, name + "_so")
            tt(nc.gpsimd, ss, cf["wd"][:, k, :], al, ALU.mult)
            partner_mul(so, cf["wo"][:, k, :], al, cf["bits"][k])
            return ss, so

        def products(eng, f, al, k, c0):
            steps = []
            cur = {}

            def step(j):
                n = 4 << j
                if j < 6:
                    cur[j] = tmp.tile([128, 2, 2 * n], F32, tag="p%d" % j, name="pj")
                else:
                    cur[j] = work.tile([128, 2, 2 * n], F32, tag="pmat", name="pmat", bufs=4)
                other = al[:, 8 * k : 8 * k + 8].rearrange("p (c t) -> p c t", t=4) if j == 0 else cur[j - 1][:]
                tt(eng, cur[j][:].rearrange("p c (o n) -> p c o n", o=2), other.unsqueeze(2).to_broadcast([128, 2, 2, n]),
                   f[j][:, 2 * k - c0 : 2 * k - c0 + 2, :].rearrange("p c (n o i) -> p c o n i", o=2, i=2)[:, :, :, :, 0], ALU.mult)

            for j in range(7):
                steps.append(lambda j=j: step(j))
            return steps, cur

        def block_matrix(cur, b):
            return cur[6][:, (b // 4) % 2, b % 4 :: 4]

        def norm_group(y, group, r):
            fresh = {}
            for lo, hi in group:
                fresh[lo] = ytile()
                stt(fresh[lo][:], y[hi][:], r[:, lo : lo + 1], y[lo][:])
            for lo, hi in group:
                stt(y[hi][:], y[lo][:], r[:, hi : hi + 1], y[hi][:])
                y[lo] = fresh[lo]

        def norm_psum(y, group, ps, r, beside=None):
            for n, (lo, hi) in enumerate(group):
                y[hi] = ytile()
                stt(y[hi][:], y[lo][:], r[:, hi : hi + 1], ps[hi][:])
                if n == 0 and beside is not None:
                    beside(y[hi])
            for lo, hi in group:
                stt(y[lo][:], ps[hi][:], r[:, lo : lo + 1], y[lo][:])

        def low_copy(y, b, ps):
            y[b] = ytile()
            nc.scalar.copy(out=y[b][:], in_=ps[:])

        def close_scaled(y, b, ss):
            ts = {}
            for k in b:
                ts[k] = ytile()
                scaled(ts[k][:], y[k][:], ss[:, k : k + 1])
            return ts

        def close_sum(y, b, ts, so, dst=None):
            for k in b:
                other = b[0] + b[1] - k
                stt(ts[k][:] if dst is None else dst[k], y[other][:], so[:, k : k + 1], ts[k][:])
            if dst is None:
                y.update(ts)

        def stage_one(wd, wo):
            for t in range(4):
                q = slice(32 * t, 32 * t + 32)
                e = 4 * (t % 2)
                nc.gpsimd.tensor_copy(out=wd[q, :], in_=s_raw[q, :, e + 3 * (t // 2)])
                nc.gpsimd.tensor_copy(out=wo[q, :], in_=s_raw[q, :, e + 1 + t // 2])

        gate = cons.tile([128, 1], F32, name="gate")

        def wait_for(t):
            nc.gpsimd.tensor_copy(out=gate[:], in_=t[:, 0:1])

        def pool_begin(y, group, r):
            ts = {}
            for p in group:
                for k in p:
                    ts[k] = ytile()
                    scaled(ts[k][:], y[p[0] + p[1] - k][:], r[:, k : k + 1])
            return ts

        def pool_sum(y, ts, t):
            wait_for(t)
            for k in ts:
                tt(nc.gpsimd, ts[k][:], ts[k][:], y[k][:], ALU.add)
            y.update(ts)

        def stage_group(y, group, r, kind):
            if kind in ACT_KINDS and len(group) == 2:
                acts_group(y, group, r)
            else:
                norm_group(y, group, r)

        def acts_group(y, group, r):
            p, q = group
            ts = {}
            for k in p:
                ts[k] = ytile()
                scaled(ts[k][:], y[p[0] + p[1] - k][:], r[:, k : k + 1])
            norm_group(y, [q], r)
            for k in p:
                tt(nc.vector, ts[k][:], ts[k][:], y[k][:], ALU.add)
            y.update(ts)

        xc = cons.tile([128, 2, TOK], U32, name="xc", align_bytes=64)
        xs = cons.tile([128, 2, TOK], U8, name="xs", align_bytes=64)
        wd_t, wi_t, wc_t, ws_t = {}, {}, {}, {}

        def widen(c, g, on_vector=()):
            wd_t[c, g] = work.tile([128, 4, 512], BF16, tag="wide", name="wd", bufs=4, align_bytes=64)
            for j in range(4):
                if j in on_vector:
                    nc.vector.tensor_scalar(out=wd_t[c, g][:, j, :], in0=wbs[c][:, g, j, :].bitcast(FP8), scalar1=wsc[:, g, j : j + 1], scalar2=None, op0=ALU.mult)
                else:
                    nc.scalar.activation(out=wd_t[c, g][:, j, :], in_=wbs[c][:, g, j, :].bitcast(FP8), func=ACT.Copy, scale=wsc[:, g, j : j + 1])
            wi_t[c, g] = work.tile([128, 2048], BF16, tag="inter", name="wi", bufs=3, align_bytes=64)

        def weave(c, g, cp):
            cp(out=wi_t[c, g][:].rearrange("p (t m j) -> p t m j", t=4, j=4), in_=wd_t[c, g][:].rearrange("p j (m t) -> p t m j", t=4))

        def quant(c, g):
            if g == 0:
                wc_t[c] = work.tile([128, 2, 512], U32, tag="wc", name="wc", bufs=2, align_bytes=64)
                ws_t[c] = work.tile([128, 2, 512], U8, tag="ws", name="ws", bufs=2, align_bytes=64)
            nc.vector.quantize_mx(out=wc_t[c][:, g, :].bitcast(FP8X4), scales=ws_t[c][:, g, :], in_=wi_t[c, g][:])

        von, sca = nc.vector.tensor_copy, nc.scalar.copy

        widen(0, 0, (2, 3))
        for g in range(2):
            xg = work.tile([128, TOK * 4], BF16, tag="inter", name="xg", bufs=3, align_bytes=64)
            for h in range(2):
                ps = bank()
                words = xraw[h][:].rearrange("p i d -> p (i d)").bitcast(F32)
                for i in range(2):
                    for u in range(2):
                        w0 = 512 * i + 256 * g
                        nc.tensor.transpose(ps[:, 256 * i + 128 * u : 256 * i + 128 * u + 128], words[:, w0 + u : w0 + 256 : 2], ident[:])
                nc.vector.tensor_copy(out=xg[:].bitcast(F32)[:, 512 * h : 512 * h + 512].rearrange("p (i r u) -> p i r u", i=2, u=2),
                                      in_=ps[:].rearrange("p (i u r) -> p i r u", i=2, u=2))
            nc.vector.quantize_mx(out=xc[:, g, :].bitcast(FP8X4), scales=xs[:, g, :], in_=xg[:])
            if g == 0:
                weave(0, 0, von)
        quant(0, 0)
        um, um_finish = coefficients(um_raw, (0, 1, 2, 3, 4), 32, "um")
        widen(0, 1, (2, 3))
        weave(0, 1, von)
        um_finish()
        bm = cons.tile([128, 2, 32], F32, name="bm")
        nc.gpsimd.tensor_copy(out=bm[:], in_=bm_raw[:])
        c_main = small(um, "um_c")
        t_main = small(um, "um_t")
        tt(nc.gpsimd, t_main, um["wd"][:, 0, :], bm[:, 0, :], ALU.mult)
        partner_mul(c_main, um["wo"][:, 0, :], bm[:, 0, :], 0)
        tt(nc.gpsimd, c_main, c_main, t_main, ALU.add)
        upb = bm[:, 1, :]
        quant(0, 1)

        zt = [cons.tile([128, 2048], F32, tag="zc%d" % (k // 2), name="zt%d" % k, bufs=2, align_bytes=64) for k in range(4)]

        def first_product(y, c, ts):
            pss = {}
            for t in ts:
                b = 4 * c + t
                pss[b] = bank()
                for g in range(2):
                    nc.tensor.matmul_mx(out=pss[b][:], lhsT=wc_t[c][:, g, 128 * t : 128 * t + 128].bitcast(FP8X4), lhsT_scale=ws_t[c][:, g, 128 * t : 128 * t + 128],
                                        rhs=xc[:, g, :].bitcast(FP8X4), rhs_scale=xs[:, g, :], start=g == 0, stop=g == 1)
            for b in pss:
                y[b] = ytile()
                scaled(y[b][:], pss[b][:], um["wd"][:, 0, b : b + 1], c_main[:, b : b + 1])
            return pss

        def first_sum(y, pss):
            for b in pss:
                stt(y[b][:], pss[b ^ 1][:], um["wo"][:, 0, b : b + 1], y[b][:])

        def turn_out(y, blocks, to, frm):
            for k in range(4):
                ps = bank()
                for e, b in enumerate(blocks):
                    nc.tensor.transpose(ps[:, 128 * e : 128 * e + 128], y[b][:, 128 * k : 128 * k + 128], ident[:])
                nc.scalar.copy(out=to(zt[k]), in_=frm(ps))

        def turn_back(place):
            ps = bank()
            for k in range(4):
                nc.tensor.transpose(ps[:, 128 * k : 128 * k + 128], zt[k][:, 128 * place : 128 * place + 128], ident[:])
            return ps

        y = {}

        def turn_first(c):
            turn_out(y, range(4 * c, 4 * c + 4),
                     lambda z: z[:].rearrange("p (v t c h) -> p c v t h", v=16, t=4, c=4)[:, c],
                     lambda ps: ps[:].rearrange("p (t h v) -> p v t h", t=4, h=8))

        pm_up = {}
        steps_up = []

        def matrix_steps(n):
            for k in range(min(n, len(steps_up))):
                steps_up.pop(0)()

        widen(1, 0)
        widen(1, 1)
        for c in range(4):
            load_wexp(c + 3)
            p0 = first_product(y, c, (0, 1))
            p1 = first_product(y, c, (2, 3))
            weave(c + 1, 0, von)
            if c >= 2:
                matrix_steps(3)
            first_sum(y, p0)
            quant(c + 1, 0)
            first_sum(y, p1)
            widen(c + 2, 0, A_WIDEN)
            weave(c + 1, 1, von)
            norm_group(y, [(4 * c, 4 * c + 2), (4 * c + 1, 4 * c + 3)], um["rr"][:, 1, :])
            if c >= 2:
                matrix_steps(3)
            quant(c + 1, 1)
            turn_first(c)
            widen(c + 2, 1, A_WIDEN)
            if c == 0:
                f_up = load_factors(up_w, 4, 4)
                for k in (2, 3):
                    steps, pm_up[k] = products(nc.vector, f_up, um["den"][:, 1, :], k, 4)
                    steps_up += steps
                r1, r1_finish = coefficients(r_raw[:, 0:4, :], (0, 1, 2, 3), 16, "r1", stage_one)
            if c == 1:
                r1_finish()
                r1_r, r1_al = chain(r1, (0, 1, 2), "r1", 4)
                r1_ss, r1_so = closing(r1, 3, r1_al, "r1")
                dm_raw = load_main(down_w, "dm_raw")
                r2, r2_finish = coefficients(r_raw[:, 4:7, :], (0, 1, 2), 16, "r2")
            if c == 2:
                r2_finish()
                r2_r, r2_al = chain(r2, (0, 1), "r2")
                r2_ss, r2_so = closing(r2, 2, r2_al, "r2")
                um_r, um_al = chain(um, (2, 3, 4), "um")
                dm, dm_finish = coefficients(dm_raw, (0, 1, 2, 3, 4), 32, "dm")
            if c == 3:
                dm_finish()
                d01_r, d01_al = chain(dm, (0, 1), "d0")
                d9_r, d9_al = chain(dm, (2, 3), "d9")
                d_ss, d_so = closing(dm, 4, d9_al, "d11")

        fill = []
        psu = {}
        held = {}

        def filler(n):
            for k in range(min(n, len(fill))):
                fill.pop(0)()

        def s_product(c, ts):
            held[c, ts] = first_product(y, c, ts)

        def s0(c):
            s_product(c, (0, 1))
            if c + 3 < 8:
                load_wexp(c + 3)
            if c + 2 < 8:
                widen(c + 2, 0)

        def s1(c):
            first_sum(y, held[c, (0, 1)])
            s_product(c, (2, 3))
            if c + 1 < 8:
                weave(c + 1, 0, von if c < V_WEAVE else sca)

        def s2(c):
            first_sum(y, held[c, (2, 3)])
            if c + 2 < 8:
                widen(c + 2, 1)
            if c + 1 < 8:
                quant(c + 1, 0)

        def s3(c):
            norm_group(y, [(4 * c, 4 * c + 2), (4 * c + 1, 4 * c + 3)], um["rr"][:, 1, :])
            if c + 1 < 8:
                weave(c + 1, 1, von if c < V_WEAVE - 1 else sca)
            if c == 4:
                matrix_steps(len(steps_up))

        def s4(c):
            for t in range(4):
                b = 4 * c + t
                psu[b] = bank()
                nc.tensor.matmul(psu[b][:], block_matrix(pm_up[c // 2], b), y[b][:], start=True, stop=True)
                if c % 2 == 0:
                    low_copy(y, b, psu[b])
            if c + 1 < 8:
                quant(c + 1, 1)

        def s5(c, t0):
            norm_psum(y, [(4 * c - 4 + t, 4 * c + t) for t in (t0, t0 + 1)], psu, um_r[0])

        for c in range(4, 8):
            fill += [lambda c=c: s0(c), lambda c=c: s1(c), lambda c=c: s2(c), lambda c=c: s3(c), lambda c=c: s4(c)]
            if c % 2 == 1:
                fill += [lambda c=c: s5(c, 0), lambda c=c: s5(c, 2)]
        fill += [lambda grp=grp: stage_group(y, grp, um_r[1], "u10f") for grp in groups([p for p in pairs(3) if p[0] >= 16])]

        def turned(z, coefs, place, bit, ss, so, to, frm, plan, beside):
            todo = groups(pairs(0, 16))
            his = {}

            def begin(grp):
                for lo, hi in grp:
                    low_copy(z, lo, turn_back(place(lo)))
                    his[hi] = turn_back(place(hi))

            begin(todo[0])
            filler(plan[0])
            for n, grp in enumerate(todo):
                norm_psum(z, grp, his, coefs[0], beside if n == 0 else None)
                if n + 1 < 4:
                    begin(todo[n + 1])
                filler(plan[1][n])
            for k in range(1, bit):
                for n, grp in enumerate(groups(pairs(k, 16))):
                    stage_group(z, grp, coefs[k], "t%d%d" % (bit, k))
                    filler(plan[2][n])
            todo = pairs(bit, 16)
            ts = {0: close_scaled(z, todo[0], ss), 1: close_scaled(z, todo[1], ss)}
            ready = []
            for n, b in enumerate(todo):
                if n + 2 < 8:
                    ts[n + 2] = close_scaled(z, todo[n + 2], ss)
                close_sum(z, b, ts[n], so)
                if n % 4 == 3:
                    for e in b:
                        g = e // 4
                        turn_out(z, range(4 * g, 4 * g + 4), lambda q: to(q, g), frm)
                    filler(plan[3])

        pm_dn = {}

        def down_matrices(t, ks):
            wait_for(t)
            for k in ks:
                steps, pm_dn[k] = products(nc.gpsimd, f_dn, d01_al, k, 0)
                for st in steps:
                    st()

        turned({}, r1_r, lambda v: v, 3, r1_ss, r1_so,
               lambda q, g: q[:].rearrange("p (w g v r) -> p g w v r", w=16, g=4, v=4)[:, g],
               lambda ps: ps[:].rearrange("p (v r w) -> p w v r", v=4, r=8), PLAN_1, None)
        f_dn = load_factors(down_w, 0, 8)
        turned({}, r2_r, lambda s: s, 2, r2_ss, r2_so,
               lambda q, g: q[:].rearrange("p (c x e h v) -> p c e x h v", c=2, x=8, e=2, h=4)[:, g // 2, g % 2],
               lambda ps: ps[:].rearrange("p (h v x) -> p x h v", h=4, v=16), PLAN_2, lambda t: down_matrices(t, (0, 1)))
        his = {}
        todo = groups([(4 * c + t, 4 * c + 4 + t) for c in (0, 2) for t in range(4)])

        def nine_begin(grp):
            for lo, hi in grp:
                low_copy(y, lo, turn_back(8 * (lo // 4 % 2) + 2 * (lo % 4) + lo // 8))
                his[hi] = turn_back(8 * (hi // 4 % 2) + 2 * (hi % 4) + hi // 8)

        nine_begin(todo[0])
        filler(PLAN_3[0])
        for n, grp in enumerate(todo):
            norm_psum(y, grp, his, um_r[0], (lambda t: down_matrices(t, (2, 3))) if n == 0 else None)
            if n + 1 < 4:
                nine_begin(todo[n + 1])
            filler(PLAN_3[1])
        for grp in groups([p for p in pairs(3) if p[0] < 16]):
            stage_group(y, grp, um_r[1], "u10")
        filler(len(fill))

        wcc = [cons.tile([128, 2, D], U32, tag="zc%d" % (k // 2), name="wcc%d" % k, bufs=2, align_bytes=64) for k in range(4)]
        wcs = cons.tile([128, 8, D], U8, name="wcs", align_bytes=64)
        csrc = w_con.rearrange("(c p j) d -> c p j d", p=128, j=4)
        wr_t, wq_t = {}, {}

        def con_load(n):
            c, dh = n // 2, n % 2
            wr_t[n] = work.tile([128, 4, 512], BF16, tag="wide", name="wr", bufs=4, align_bytes=64)
            nc.sync.dma_start(out=wr_t[n][:], in_=csrc[c][:, :, 512 * dh : 512 * dh + 512])

        def con_weave(n):
            wq_t[n] = work.tile([128, 2048], BF16, tag="inter", name="wq", bufs=3, align_bytes=64)
            nc.scalar.copy(out=wq_t[n][:].rearrange("p (d j) -> p d j", j=4), in_=wr_t[n][:].rearrange("p j d -> p d j"))

        def con_quant(n):
            c, dh = n // 2, n % 2
            nc.vector.quantize_mx(out=wcc[c // 2][:, c % 2, 512 * dh : 512 * dh + 512].bitcast(FP8X4), scales=wcs[:, c, 512 * dh : 512 * dh + 512], in_=wq_t[n][:])

        con = [0]

        def con_step():
            n = con[0]
            if n == 0:
                con_load(0)
                con_load(1)
            if n < 16:
                if n + 2 < 16:
                    con_load(n + 2)
                con_weave(n)
            if 1 <= n <= 16:
                con_quant(n - 1)
            con[0] = n + 1

        his = {}

        def last_stage(c):
            for grp in groups([(4 * c + t, 4 * c + 16 + t) for t in range(4)]):
                stage_group(y, grp, um_r[2], "u11")
                for p in grp:
                    for b in p:
                        nc.scalar.activation(out=y[b][:], in_=y[b][:], func=ACT.Gelu, scale=um_al[:, b : b + 1], bias=upb[:, b : b + 1])

        def two_pairs(c, bit):
            return [(4 * c + p[0], 4 * c + p[1]) for p in pairs(bit)[0:2]]

        def down_first(c, bit):
            for cc in (c, c + 4):
                stage_group(y, two_pairs(cc, bit), d01_r[bit], "d%d" % bit)

        def down_middle(c):
            for t in range(4):
                b = 4 * c + t
                ps = bank()
                nc.tensor.matmul(ps[:], block_matrix(pm_dn[c // 2], b), y[b][:], start=True, stop=True)
                if c % 2 == 0:
                    low_copy(y, b, ps)
                else:
                    his[b] = ps

        def down_nine(c, group=None, r=None):
            beside = None
            if group is not None:
                ts = pool_begin(y, group, r)
                beside = lambda t: pool_sum(y, ts, t)
            for t0 in (0, 2):
                norm_psum(y, [(4 * c + t, 4 * c + 4 + t) for t in (t0, t0 + 1)], his, d9_r[0], beside if t0 == 0 else None)

        def ten_pairs(c, t0):
            return [(4 * c + t, 4 * c + 8 + t) for t in (t0, t0 + 1)]

        def down_ten(c, t0s=(0, 2)):
            for t0 in t0s:
                stage_group(y, ten_pairs(c, t0), d9_r[1], "d10")

        last_stage(0)
        con_step()
        last_stage(1)
        down_first(0, 0)
        con_step()
        last_stage(2)
        down_first(0, 1)
        down_middle(0)
        con_step()
        down_first(1, 0)
        down_middle(4)
        con_step()
        last_stage(3)
        down_first(1, 1)
        down_middle(1)
        con_step()
        down_first(2, 0)
        down_nine(0, two_pairs(2, 1), d01_r[1])
        down_middle(5)
        con_step()
        stage_group(y, two_pairs(6, 1), d01_r[1], "d1")
        down_first(3, 0)
        down_nine(4, two_pairs(3, 1), d01_r[1])
        down_middle(2)
        con_step()
        down_middle(6)
        con_step()
        stage_group(y, two_pairs(7, 1), d01_r[1], "d1")
        down_middle(3)
        con_step()
        down_nine(2)
        con_step()
        down_middle(7)
        down_ten(0)
        con_step()
        down_nine(6, ten_pairs(1, 0), d9_r[1])
        con_step()
        down_ten(1, (2,))
        con_step()
        con_step()
        down_ten(4)
        con_step()
        con_step()
        down_ten(5)
        con_step()
        con_step()
        con_step()

        bb = work.tile([128, D], F32, tag="wb", name="bb", bufs=3, align_bytes=64)
        braw = []
        for v in (b_con, down_bias):
            br = work.tile([128, D], BF16, tag="wb", name="br", bufs=3, align_bytes=64)
            nc.sync.dma_start(out=br[:], in_=v.partition_broadcast(128))
            braw.append(br)
        tt(nc.vector, bb[:], braw[0][:], braw[1][:], ALU.add)

        ht = cons.tile([128, 8, 4, TOK], BF16, tag="fh", name="ht")
        acc = [bank() for n in range(8)]
        hq_t, hs_t, hi_t = {}, {}, {}

        def h_weave(c, cp):
            hi_t[c] = work.tile([128, 2048], BF16, tag="inter", name="hi", bufs=3, align_bytes=64)
            cp(out=hi_t[c][:].rearrange("p (r t) -> p r t", t=4), in_=ht[:, c].rearrange("p t r -> p r t"))

        def h_quant(c):
            hq_t[c] = work.tile([128, 512], U32, tag="wc", name="hq", bufs=2, align_bytes=64)
            hs_t[c] = work.tile([128, 512], U8, tag="ws", name="hs", bufs=2, align_bytes=64)
            nc.vector.quantize_mx(out=hq_t[c][:].bitcast(FP8X4), scales=hs_t[c][:], in_=hi_t[c][:])

        def second_product(c, first, last):
            for k in range(8):
                i, dh = k // 2, k % 2
                nc.tensor.matmul_mx(out=acc[k][:], lhsT=hq_t[c][:, 128 * i : 128 * i + 128].bitcast(FP8X4), lhsT_scale=hs_t[c][:, 128 * i : 128 * i + 128],
                                    rhs=wcc[c // 2][:, c % 2, 512 * dh : 512 * dh + 512].bitcast(FP8X4), rhs_scale=wcs[:, c, 512 * dh : 512 * dh + 512],
                                    start=first, stop=last)

        todo = [(4 * c + t, 4 * c + 16 + t) for c in range(4) for t in range(4)]
        ts = {0: close_scaled(y, todo[0], d_ss), 1: close_scaled(y, todo[1], d_ss)}
        for k, b in enumerate(todo):
            c, t = k // 4, k % 4
            if k + 2 < 16:
                ts[k + 2] = close_scaled(y, todo[k + 2], d_ss)
            close_sum(y, b, ts[k], d_so, {b[0]: ht[:, c, t, :], b[1]: ht[:, c + 4, t, :]})
            if c > 0 and t == 0:
                h_weave(c - 1, sca)
                h_weave(c + 3, von if c + 3 in H_ON_V else sca)
                h_quant(c + 3)
                second_product(c + 3, c == 1, False)
            if c > 0 and t == 2:
                h_quant(c - 1)
                second_product(c - 1, False, False)
        h_weave(3, sca)
        h_weave(7, von if 7 in H_ON_V else sca)
        h_quant(7)
        second_product(7, False, False)
        h_quant(3)
        second_product(3, False, True)
        orows = out.rearrange("b s d -> (b s) d")
        for k in range(8):
            i, dh = k // 2, k % 2
            ot = work.tile([128, 512], F32, tag="wide" if k % 2 else "inter", name="ot", bufs=4 if k % 2 else 3, align_bytes=64)
            tt(nc.vector, ot[:], acc[k][:], bb[:, 512 * dh : 512 * dh + 512], ALU.add)
            nc.sync.dma_start(out=orows[128 * i : 128 * i + 128, 512 * dh : 512 * dh + 512], in_=ot[:])
